import numpy as np
import ml_dtypes


def mxq(x, axis, fmt="e4m3"):
    dtype, down = {"e4m3": (ml_dtypes.float8_e4m3fn, 7), "e5m2": (ml_dtypes.float8_e5m2, 14)}[fmt]
    v = np.moveaxis(np.asarray(x, np.float32).astype(ml_dtypes.bfloat16).astype(np.float64), axis, -1)
    blocks = v.reshape(v.shape[:-1] + (-1, 32))
    amax = np.abs(blocks).max(-1, keepdims=True)
    byte = np.maximum(np.where(amax > 0, np.frexp(amax)[1] - 1 + 127, 0) - down, 1)
    scale = np.exp2(byte - 127.0)
    codes = (blocks / scale).astype(np.float32).astype(dtype).astype(np.float64)
    return np.moveaxis((codes * scale).reshape(v.shape), -1, axis)


WIDE = False


def mx_kscale(k):
    if not WIDE:
        return np.ones(k)
    levels = np.array([10, -10, 5, -5, 0])
    if k % 512:
        return np.exp2(np.random.permutation(np.resize(levels, k // 32))).repeat(32)
    a = np.empty((k // 512, 16))
    for p in range(k // 512):
        a[p, :8] = np.random.permutation(np.resize(levels, 8))
        for g in range(8):
            far = levels[np.abs(levels - a[p, g]) >= 10]
            a[p, g + 8] = far[np.random.randint(len(far))]
    return np.exp2(a.ravel()).repeat(32)


BF16 = ml_dtypes.bfloat16


def bf(x):
    return np.asarray(x, np.float32).astype(BF16)


def f64(x):
    return np.asarray(x).astype(np.float64)


E2M1 = np.array([0.0, 0.5, 1.0, 1.5, 2.0, 3.0, 4.0, 6.0, -0.0, -0.5, -1.0, -1.5, -2.0, -3.0, -4.0, -6.0])


def pack_weight(w, fmt):
    k, n = w.shape
    w = f64(bf(w)).reshape(k // 32, 32, n)
    amax = np.abs(w).max(1)
    if fmt == "e4m3":
        byte = np.frexp(amax)[1] - 1 + 127 - 7
    else:
        mant, ex = np.frexp(amax / 6.0)
        byte = np.where(mant > 0.5, ex, ex - 1) + 127
    byte = np.clip(np.where(amax > 0, byte, 1), 1, 254)
    scaled = (w * np.exp2(127.0 - byte)[:, None, :]).reshape(k, n).astype(np.float32)
    by_word = np.ascontiguousarray(scaled.reshape(k // 512, 128, 4, n).transpose(0, 1, 3, 2))
    if fmt == "e4m3":
        words = by_word.astype(ml_dtypes.float8_e4m3fn).view(np.uint8)
    else:
        c = by_word.astype(ml_dtypes.float4_e2m1fn).view(np.uint8) & 0xF
        words = c[..., 0::2] | (c[..., 1::2] << 4)
    return np.ascontiguousarray(words), np.ascontiguousarray(byte.astype(np.uint8).reshape(k // 512, 16, n))


def unpack_weight(words, scales, fmt):
    g, p, n, _ = words.shape
    if fmt == "e4m3":
        vals = np.ascontiguousarray(words).view(ml_dtypes.float8_e4m3fn).astype(np.float64)
    else:
        nib = np.empty((g, p, n, 4), np.uint8)
        nib[..., 0::2] = words & 0xF
        nib[..., 1::2] = words >> 4
        vals = E2M1[nib]
    vals = vals * np.repeat(np.exp2(scales.astype(np.float64) - 127.0), 8, axis=1)[..., None]
    return vals.transpose(0, 1, 3, 2).reshape(g * 512, n)
def pack4(w):
    words, scales = pack_weight(w, "e2m1")
    return words.reshape(words.shape[0], 128, -1), scales


def unpack4(words, scales):
    return unpack_weight(words.reshape(words.shape[0], 128, -1, 2), scales, "e2m1")


N, F, H = 1536, 512, 512
SIG = 1.5


def draw_adj():
    r = np.random.uniform(0.5, 1.5, (N, 1))
    return 2.0 * r * np.exp(SIG * np.random.standard_normal((N, N)) - 0.5 * SIG * SIG) / N


def draw0():
    s, t = mx_kscale(F), mx_kscale(N)
    x_init = bf(np.random.standard_normal((N, F)) * s / t[:, None])
    adj1 = bf(draw_adj() * t)
    words, scales = pack4(np.random.standard_normal((F, H)) * 4.0 / np.sqrt(F) / s[:, None])
    return {"x_init": x_init,
            "adj1": adj1,
            "W1_words": words,
            "W1_scales": scales,
            "b1": bf(np.random.standard_normal(H) * 0.3)}


def core(x_init, adj1, W1_words, W1_scales, b1):
    support = mxq(f64(x_init), 1, "e4m3") @ unpack4(W1_words, W1_scales)
    y = (mxq(f64(adj1), 1, "e4m3") @ mxq(support, 0, "e4m3")) + f64(b1)
    return np.maximum(y, 0.0)


def e4m3fn_bytes(y):
    return np.clip(np.asarray(y, np.float64), -448.0, 448.0).astype(np.float32).astype(ml_dtypes.float8_e4m3fn).view(np.uint8)


def e4m3fn_values(b):
    return np.asarray(b, np.uint8).view(ml_dtypes.float8_e4m3fn).astype(np.float64)


def setup_inputs():
    d = draw0()
    x0 = np.asarray(d['adj1']).astype(np.float64)
    s = (np.max(np.abs(x0), axis=(0,), keepdims=True) / 448.0).astype(np.float32)
    out = {}
    for k, v in d.items():
        if k == 'adj1':
            out['adj1_bytes'] = e4m3fn_bytes(x0 / s.astype(np.float64))
            out['adj1_scale'] = s
        else:
            out[k] = v
    return out


def reference(x_init, adj1_bytes, adj1_scale, W1_words, W1_scales, b1):
    return core(x_init, e4m3fn_values(adj1_bytes) * adj1_scale.astype(np.float64), W1_words, W1_scales, b1)

@@ -1,0 +1,343 @@
+from contextlib import ExitStack
+
+import concourse.mybir as mybir
+from concourse.masks import make_identity
+
+NODES, FEAT, HID = 1536, 512, 512
+
+F32 = mybir.dt.float32
+BF16 = mybir.dt.bfloat16
+I32 = mybir.dt.int32
+U32 = mybir.dt.uint32
+U8 = mybir.dt.uint8
+E4M3 = mybir.dt.float8_e4m3fn
+E4M3X4 = mybir.dt.float8_e4m3fn_x4
+E2M1X4 = mybir.dt.float4_e2m1fn_x4
+ALU = mybir.AluOpType
+ACT = mybir.ActivationFunctionType
+
+P = 128
+K_PASS = 4 * P
+PASSES = NODES // K_PASS
+PAIR_ROWS = 2 * P
+PAIRS = NODES // PAIR_ROWS
+
+FLOPS = 2 * NODES * FEAT * HID + 2 * NODES * NODES * HID
+
+
+def tile_gcn_pa_w4_kernel(tc, x_init, adj_bytes, adj_scale, w_words, w_scales, b1, out):
+    nc = tc.nc
+    with ExitStack() as ctx:
+        keep = ctx.enter_context(tc.tile_pool(name="keep", bufs=1))
+        a_in = ctx.enter_context(tc.tile_pool(name="a_in", bufs=PAIRS))
+        x_in = ctx.enter_context(tc.tile_pool(name="x_in", bufs=PASSES))
+        wide = ctx.enter_context(tc.tile_pool(name="wide", bufs=3))
+        narrow = ctx.enter_context(tc.tile_pool(name="narrow", bufs=3))
+        flipped = ctx.enter_context(tc.tile_pool(name="flipped", bufs=2))
+        results = ctx.enter_context(tc.tile_pool(name="results", bufs=PAIRS))
+        tp = ctx.enter_context(tc.psum_pool(name="tp", bufs=5))
+        sums = ctx.enter_context(tc.psum_pool(name="sums", bufs=3))
+
+        ident = keep.tile([P, P], F32, name="ident")
+        scale_cols = [keep.tile([P, 4], F32, name="scale_cols%d" % g) for g in range(PASSES)]
+        scale = keep.tile([P, NODES], F32, name="scale")
+        bias = keep.tile([P, HID], BF16, name="bias")
+        bias_rows = keep.tile([P, P], BF16, name="bias_rows")
+        bias_rows_f32 = keep.tile([P, P], F32, name="bias_rows_f32")
+        bias_col = keep.tile([P, 4], F32, name="bias_col")
+        w_codes = keep.tile([P, 2 * HID], U8, name="w_codes", align_bytes=64)
+        w_plane = keep.tile([P, HID], U8, name="w_plane", align_bytes=64)
+        x_codes = keep.tile([P, PASSES, K_PASS], U32, name="x_codes", align_bytes=64)
+        x_plane = keep.tile([P, PASSES, K_PASS], U8, name="x_plane", align_bytes=64)
+        s_codes = keep.tile([P, PASSES, HID], U32, name="s_codes", align_bytes=64)
+        s_plane = keep.tile([P, PASSES, HID], U8, name="s_plane", align_bytes=64)
+        a_codes = keep.tile([P, PAIRS, PASSES, PAIR_ROWS], U32, name="a_codes", align_bytes=64)
+        a_plane = keep.tile([P, PAIRS, PASSES, PAIR_ROWS], U8, name="a_plane", align_bytes=64)
+        a_vals = keep.tile([P, PAIRS, 2, NODES], BF16, name="a_vals")
+
+        a_raw, x_raw, x_grp, s_grp, a_grp = {}, {}, {}, {}, {}
+        acc, flip, result = {}, {}, {}
+
+        def load_scale(g):
+            by_partition = adj_scale[:, K_PASS * g : K_PASS * (g + 1)].rearrange("o (p t) -> p (o t)", t=4)
+            nc.sync.dma_start(out=scale_cols[g][:], in_=by_partition)
+
+        def load_adj(q, first=0, last=NODES):
+            if first == 0:
+                raw = a_in.tile([P, 2, NODES], U8, name="raw")
+                a_raw[q] = raw
+            cols = slice(first, last)
+            rows = adj_bytes[PAIR_ROWS * q : PAIR_ROWS * (q + 1), cols]
+            nc.sync.dma_start(out=a_raw[q][:, :, cols], in_=rows.rearrange("(m j) k -> m j k", j=2))
+
+        def load_x(g, c=0, pieces=1):
+            if c == 0:
+                x = x_in.tile([P, 4, FEAT], BF16, name="x")
+                x_raw[g] = x
+            ts = slice(4 // pieces * c, 4 // pieces * (c + 1))
+            rows = x_init[K_PASS * g : K_PASS * (g + 1), :].rearrange("(m t) f -> m t f", t=4)
+            nc.sync.dma_start(out=x_raw[g][:, ts, :], in_=rows[:, ts, :])
+
+        def load_w_codes():
+            nc.sync.dma_start(out=w_codes[:].bitcast(I32), in_=w_words[0].bitcast(I32))
+
+        def load_w_plane():
+            for quad in range(4):
+                nc.sync.dma_start(
+                    out=w_plane[32 * quad : 32 * quad + 4, :].bitcast(I32),
+                    in_=w_scales[0, 4 * quad : 4 * quad + 4, :].bitcast(I32),
+                )
+
+        def spread_scale(g):
+            bank = tp.tile([P, 4, P], F32, name="bank")
+            for t in range(4):
+                nc.tensor.transpose(bank[:, t, :], scale_cols[g][:, t : t + 1].to_broadcast([P, P]), ident[:])
+            out_ap = scale[:, K_PASS * g : K_PASS * (g + 1)].rearrange("p (n t) -> p n t", t=4)
+            in_ap = bank[:].rearrange("p t n -> p n t")
+            if g == 0:
+                nc.vector.tensor_copy(out=out_ap, in_=in_ap)
+            else:
+                nc.scalar.copy(out=out_ap, in_=in_ap)
+
+        def turn_bias():
+            nc.vector.tensor_copy(out=bias_rows_f32[:], in_=bias_rows[:])
+            bank = tp.tile([P, 4, P], F32, name="bank")
+            nc.tensor.transpose(bank[:, 0, :], bias_rows_f32[:], ident[:])
+            nc.scalar.copy(out=bias_col[:], in_=bank[:, 0, 0:4])
+
+        def adj_mult(i, c=0, pieces=1):
+            q, j = divmod(i, 2)
+            cols = slice(NODES // pieces * c, NODES // pieces * (c + 1))
+            nc.vector.tensor_tensor(
+                out=a_vals[:, q, j, cols],
+                in0=a_raw[q][:, j, cols].bitcast(E4M3),
+                in1=scale[:, cols],
+                op=ALU.mult,
+            )
+
+        def turn(runs, grouped):
+            bank = tp.tile([P, 4, P], F32, name="bank")
+            for a in range(2):
+                for u in range(2):
+                    nc.tensor.transpose(bank[:, 2 * a + u, :], runs[a][:, u : 2 * P : 2], ident[:])
+            nc.scalar.copy(
+                out=grouped.bitcast(F32).rearrange("p (a m u) -> p a m u", a=2, u=2),
+                in_=bank[:].rearrange("p (a u) m -> p a m u", a=2),
+            )
+
+        def x_turn(g, b):
+            if b == 0:
+                grouped = wide.tile([P, 4 * K_PASS], BF16, name="x_grouped", align_bytes=64)
+                x_grp[g] = grouped
+            runs = [x_raw[g][:, 2 * b + a, :].bitcast(F32) for a in range(2)]
+            turn(runs, x_grp[g][:, 8 * P * b : 8 * P * (b + 1)])
+
+        def x_quant(g):
+            nc.vector.quantize_mx(out=x_codes[:, g, :].bitcast(E4M3X4), scales=x_plane[:, g, :], in_=x_grp[g][:])
+
+        def stage1(g):
+            grouped = wide.tile([P, 4 * HID], BF16, name="s_grouped", align_bytes=64)
+            s_grp[g] = grouped
+            for c in range(HID // P):
+                bank = tp.tile([P, 4, P], F32, name="bank")
+                for t in range(4):
+                    cols = slice(P * t, P * (t + 1))
+                    nc.tensor.matmul_mx(
+                        out=bank[:, t, :],
+                        lhsT=x_codes[:, g, cols].bitcast(E4M3X4),
+                        lhsT_scale=x_plane[:, g, cols],
+                        rhs=w_codes[:, 2 * P * c : 2 * P * (c + 1)].bitcast(E2M1X4),
+                        rhs_scale=w_plane[:, P * c : P * (c + 1)],
+                        start=True,
+                        stop=True,
+                    )
+                nc.scalar.copy(
+                    out=grouped[:, 4 * P * c : 4 * P * (c + 1)].rearrange("p (n t) -> p n t", t=4),
+                    in_=bank[:].rearrange("p t n -> p n t"),
+                )
+
+        def s_quant(g):
+            nc.vector.quantize_mx(out=s_codes[:, g, :].bitcast(E4M3X4), scales=s_plane[:, g, :], in_=s_grp[g][:])
+
+        def adj_turn(q, g):
+            if g == 0:
+                grouped = narrow.tile([P, PASSES, 4 * PAIR_ROWS], BF16, name="a_grouped", align_bytes=64)
+                a_grp[q] = grouped
+            runs = [a_vals[:, q, j, K_PASS * g : K_PASS * (g + 1)].bitcast(F32) for j in range(2)]
+            turn(runs, a_grp[q][:, g, :])
+
+        def adj_quant(q):
+            for gs in (slice(0, 2), slice(2, 3)):
+                nc.vector.quantize_mx(
+                    out=a_codes[:, q, gs, :].rearrange("p g r -> p (g r)").bitcast(E4M3X4),
+                    scales=a_plane[:, q, gs, :].rearrange("p g r -> p (g r)"),
+                    in_=a_grp[q][:, gs, :].rearrange("p g r -> p (g r)"),
+                )
+
+        def out_rows(q):
+            return out[PAIR_ROWS * q : PAIR_ROWS * (q + 1), :].rearrange("(m j) h -> m j h", j=2)
+
+        def stage2(q, j):
+            total = sums.tile([P, HID], F32, name="total")
+            acc[q, j] = total
+            for g in range(PASSES):
+                cols = slice(P * j, P * (j + 1))
+                nc.tensor.matmul_mx(
+                    out=total[:],
+                    lhsT=a_codes[:, q, g, cols].bitcast(E4M3X4),
+                    lhsT_scale=a_plane[:, q, g, cols],
+                    rhs=s_codes[:, g, :].bitcast(E4M3X4),
+                    rhs_scale=s_plane[:, g, :],
+                    start=(g == 0),
+                    stop=(g == PASSES - 1),
+                )
+
+        def finish(q, j, pieces=1):
+            if j == 0:
+                res = results.tile([P, 2, HID], F32, name="res")
+                result[q] = res
+            for c in range(pieces):
+                cols = slice(HID // pieces * c, HID // pieces * (c + 1))
+                part = result[q][:, j, cols]
+                nc.vector.tensor_tensor(out=part, in0=acc[q, j][:, cols], in1=bias[:, cols], op=ALU.add)
+                nc.scalar.activation(out=part, in_=part, func=ACT.Relu)
+                nc.sync.dma_start(out=out_rows(q)[:, j, cols], in_=part)
+
+        def stage2_flipped(q, h):
+            if h == 0:
+                flat = flipped.tile([P, 4, PAIR_ROWS], F32, name="flat")
+                flip[q] = flat
+            total = sums.tile([P, HID], F32, name="total")
+            halves = [total[:, PAIR_ROWS * i : PAIR_ROWS * (i + 1)] for i in range(2)]
+            for i in range(2):
+                cols = slice(P * (2 * h + i), P * (2 * h + i + 1))
+                for g in range(PASSES):
+                    nc.tensor.matmul_mx(
+                        out=halves[i],
+                        lhsT=s_codes[:, g, cols].bitcast(E4M3X4),
+                        lhsT_scale=s_plane[:, g, cols],
+                        rhs=a_codes[:, q, g, :].bitcast(E4M3X4),
+                        rhs_scale=a_plane[:, q, g, :],
+                        start=(g == 0),
+                        stop=(g == PASSES - 1),
+                    )
+            for i in range(2):
+                c = 2 * h + i
+                nc.scalar.activation(
+                    out=flip[q][:, c, :], in_=halves[i], func=ACT.Relu, bias=bias_col[:, c : c + 1]
+                )
+
+        def flip_back(q, j):
+            if j == 0:
+                res = results.tile([P, 2, HID], F32, name="res")
+                result[q] = res
+            bank = tp.tile([P, 4, P], F32, name="bank")
+            for c in range(4):
+                nc.tensor.transpose(bank[:, c, :], flip[q][:, c, P * j : P * (j + 1)], ident[:])
+            nc.scalar.copy(out=result[q][:, j, :], in_=bank[:].rearrange("p c m -> p (c m)"))
+            nc.sync.dma_start(out=out_rows(q)[:, j, :], in_=result[q][:, j, :])
+
+        with tc.manual_schedule():
+            make_identity(nc, ident[:])
+            nc.gpsimd.memset(w_plane[:].bitcast(I32), 0)
+            nc.gpsimd.memset(bias_rows[:], 0.0)
+            load_scale(0)
+            load_adj(0, 0, K_PASS)
+            load_scale(1)
+            load_scale(2)
+            load_x(0, 0, 2)
+            load_adj(0, K_PASS, NODES)
+            load_x(0, 1, 2)
+            load_x(1)
+            load_adj(1)
+            load_x(2)
+            load_w_codes()
+            load_w_plane()
+            nc.sync.dma_start(out=bias_rows[0:4, :], in_=b1.rearrange("(c m) -> c m", m=P))
+            for q in range(2, PAIRS):
+                load_adj(q)
+            nc.sync.dma_start(out=bias[:], in_=b1.partition_broadcast(P))
+
+            spread_scale(0)
+            spread_scale(1)
+            spread_scale(2)
+            adj_mult(0, 0, 3)
+            adj_mult(1, 0, 3)
+            x_turn(0, 0)
+            x_turn(0, 1)
+            adj_mult(0, 1, 3)
+            adj_mult(1, 1, 3)
+            adj_turn(0, 0)
+            x_turn(1, 0)
+            x_turn(1, 1)
+            adj_mult(0, 2, 3)
+            adj_mult(1, 2, 3)
+            adj_turn(0, 1)
+            x_quant(0)
+            x_turn(2, 0)
+            x_turn(2, 1)
+            adj_mult(2)
+            x_quant(1)
+            adj_turn(0, 2)
+            x_quant(2)
+            stage1(0)
+            adj_mult(3)
+            stage1(1)
+            adj_mult(4)
+            stage1(2)
+            turn_bias()
+            adj_mult(5)
+            adj_quant(0)
+            adj_turn(1, 0)
+            adj_turn(1, 1)
+            adj_turn(1, 2)
+            adj_turn(2, 0)
+            adj_turn(2, 1)
+            adj_turn(2, 2)
+            s_quant(0)
+            s_quant(1)
+            s_quant(2)
+            adj_mult(6)
+            adj_quant(1)
+            adj_quant(2)
+            adj_mult(7)
+            stage2_flipped(0, 0)
+            stage2_flipped(0, 1)
+            stage2_flipped(1, 0)
+            stage2_flipped(1, 1)
+            stage2(2, 0)
+            flip_back(0, 0)
+            adj_turn(3, 0)
+            adj_turn(3, 1)
+            adj_turn(3, 2)
+            flip_back(1, 0)
+            adj_mult(8)
+            adj_mult(9)
+            adj_quant(3)
+            stage2(2, 1)
+            finish(2, 0)
+            adj_mult(10)
+            flip_back(0, 1)
+            adj_turn(4, 0)
+            adj_turn(4, 1)
+            adj_turn(4, 2)
+            stage2(3, 0)
+            stage2(3, 1)
+            adj_mult(11)
+            flip_back(1, 1)
+            adj_turn(5, 0)
+            adj_turn(5, 1)
+            adj_turn(5, 2)
+            finish(2, 1)
+            adj_quant(4)
+            finish(3, 0)
+            stage2(4, 0)
+            finish(3, 1)
+            adj_quant(5)
+            stage2(4, 1)
+            finish(4, 0)
+            finish(4, 1)
+            stage2(5, 0)
+            stage2(5, 1)
+            finish(5, 0)
+            finish(5, 1, 2)

@@ -29,22 +29,12 @@ def tile_gcn_pa_w4_kernel(tc, x_init, adj_bytes, adj_scale, w_words, w_scales, b
     nc = tc.nc
     with ExitStack() as ctx:
         keep = ctx.enter_context(tc.tile_pool(name="keep", bufs=1))
-        a_in = ctx.enter_context(tc.tile_pool(name="a_in", bufs=PAIRS))
-        x_in = ctx.enter_context(tc.tile_pool(name="x_in", bufs=PASSES))
-        wide = ctx.enter_context(tc.tile_pool(name="wide", bufs=3))
-        narrow = ctx.enter_context(tc.tile_pool(name="narrow", bufs=3))
-        flipped = ctx.enter_context(tc.tile_pool(name="flipped", bufs=2))
-        results = ctx.enter_context(tc.tile_pool(name="results", bufs=PAIRS))
-        tp = ctx.enter_context(tc.psum_pool(name="tp", bufs=5))
-        sums = ctx.enter_context(tc.psum_pool(name="sums", bufs=3))
+        tp = ctx.enter_context(tc.psum_pool(name="tp", bufs=4))
+        sums = ctx.enter_context(tc.psum_pool(name="sums", bufs=4))
 
         ident = keep.tile([P, P], F32, name="ident")
-        scale_cols = [keep.tile([P, 4], F32, name="scale_cols%d" % g) for g in range(PASSES)]
-        scale = keep.tile([P, NODES], F32, name="scale")
+        scale_cols = keep.tile([P, PASSES, 4], F32, name="scale_cols")
         bias = keep.tile([P, HID], BF16, name="bias")
-        bias_rows = keep.tile([P, P], BF16, name="bias_rows")
-        bias_rows_f32 = keep.tile([P, P], F32, name="bias_rows_f32")
-        bias_col = keep.tile([P, 4], F32, name="bias_col")
         w_codes = keep.tile([P, 2 * HID], U8, name="w_codes", align_bytes=64)
         w_plane = keep.tile([P, HID], U8, name="w_plane", align_bytes=64)
         x_codes = keep.tile([P, PASSES, K_PASS], U32, name="x_codes", align_bytes=64)
@@ -53,30 +43,34 @@ def tile_gcn_pa_w4_kernel(tc, x_init, adj_bytes, adj_scale, w_words, w_scales, b
         s_plane = keep.tile([P, PASSES, HID], U8, name="s_plane", align_bytes=64)
         a_codes = keep.tile([P, PAIRS, PASSES, PAIR_ROWS], U32, name="a_codes", align_bytes=64)
         a_plane = keep.tile([P, PAIRS, PASSES, PAIR_ROWS], U8, name="a_plane", align_bytes=64)
-        a_vals = keep.tile([P, PAIRS, 2, NODES], BF16, name="a_vals")
 
-        a_raw, x_raw, x_grp, s_grp, a_grp = {}, {}, {}, {}, {}
-        acc, flip, result = {}, {}, {}
+        a_raw, a_wide, a_bank, a_grp = {}, {}, {}, {}
+        x_raw, x_grp, s_grp = {}, {}, {}
+        acc, flip, result, banks = {}, {}, {}, {}
 
-        def load_scale(g):
-            by_partition = adj_scale[:, K_PASS * g : K_PASS * (g + 1)].rearrange("o (p t) -> p (o t)", t=4)
-            nc.sync.dma_start(out=scale_cols[g][:], in_=by_partition)
+        def load_scale():
+            nc.sync.dma_start(out=scale_cols[:], in_=adj_scale.rearrange("o (g p t) -> p (o g) t", p=P, t=4))
 
-        def load_adj(q, first=0, last=NODES):
-            if first == 0:
-                raw = a_in.tile([P, 2, NODES], U8, name="raw")
-                a_raw[q] = raw
-            cols = slice(first, last)
-            rows = adj_bytes[PAIR_ROWS * q : PAIR_ROWS * (q + 1), cols]
-            nc.sync.dma_start(out=a_raw[q][:, :, cols], in_=rows.rearrange("(m j) k -> m j k", j=2))
+        def load_adj(q, first=0, last=PASSES, rows=(0, 1)):
+            width = K_PASS * (last - first)
+            raw = keep.tile([P, len(rows), width], U8, name="a_raw%d_%d_%d" % (q, first, rows[0]))
+            a_raw[q, first, rows[0]] = raw
+            block = adj_bytes[PAIR_ROWS * q : PAIR_ROWS * (q + 1), K_PASS * first : K_PASS * last]
+            by_row = block.rearrange("(m j) k -> m j k", j=2)
+            nc.sync.dma_start(out=raw[:], in_=by_row[:, rows[0] : rows[-1] + 1, :])
 
-        def load_x(g, c=0, pieces=1):
-            if c == 0:
-                x = x_in.tile([P, 4, FEAT], BF16, name="x")
-                x_raw[g] = x
-            ts = slice(4 // pieces * c, 4 // pieces * (c + 1))
+        def load_x(g, b):
+            x = keep.tile([P, 2, FEAT], BF16, name="x_raw%d_%d" % (g, b))
+            x_raw[g, b] = x
             rows = x_init[K_PASS * g : K_PASS * (g + 1), :].rearrange("(m t) f -> m t f", t=4)
-            nc.sync.dma_start(out=x_raw[g][:, ts, :], in_=rows[:, ts, :])
+            nc.sync.dma_start(out=x[:], in_=rows[:, 2 * b : 2 * b + 2, :])
+
+        def load_x_whole(g):
+            x = keep.tile([P, 4, FEAT], BF16, name="x_raw%d" % g)
+            x_raw[g, 0] = x[:, 0:2, :]
+            x_raw[g, 1] = x[:, 2:4, :]
+            rows = x_init[K_PASS * g : K_PASS * (g + 1), :].rearrange("(m t) f -> m t f", t=4)
+            nc.sync.dma_start(out=x[:], in_=rows)
 
         def load_w_codes():
             nc.sync.dma_start(out=w_codes[:].bitcast(I32), in_=w_words[0].bitcast(I32))
@@ -88,102 +82,117 @@ def tile_gcn_pa_w4_kernel(tc, x_init, adj_bytes, adj_scale, w_words, w_scales, b
                     in_=w_scales[0, 4 * quad : 4 * quad + 4, :].bitcast(I32),
                 )
 
-        def spread_scale(g):
-            bank = tp.tile([P, 4, P], F32, name="bank")
-            for t in range(4):
-                nc.tensor.transpose(bank[:, t, :], scale_cols[g][:, t : t + 1].to_broadcast([P, P]), ident[:])
-            out_ap = scale[:, K_PASS * g : K_PASS * (g + 1)].rearrange("p (n t) -> p n t", t=4)
-            in_ap = bank[:].rearrange("p t n -> p n t")
-            if g == 0:
-                nc.vector.tensor_copy(out=out_ap, in_=in_ap)
-            else:
-                nc.scalar.copy(out=out_ap, in_=in_ap)
+        def load_bias():
+            nc.sync.dma_start(out=bias[:], in_=b1.partition_broadcast(P))
 
-        def turn_bias():
-            nc.vector.tensor_copy(out=bias_rows_f32[:], in_=bias_rows[:])
-            bank = tp.tile([P, 4, P], F32, name="bank")
-            nc.tensor.transpose(bank[:, 0, :], bias_rows_f32[:], ident[:])
-            nc.scalar.copy(out=bias_col[:], in_=bank[:, 0, 0:4])
+        def widen(copy, q, first, last, lo, hi, row=0):
+            wide = keep.tile([P, K_PASS * (hi - lo)], BF16, name="a_wide%d_%d_%d_%d" % (q, first, lo, row))
+            flat = a_raw[q, first, row][:].rearrange("p j k -> p (j k)")
+            copy(out=wide[:], in_=flat[:, K_PASS * lo : K_PASS * hi].bitcast(E4M3))
+            for seg in range(lo, hi):
+                j, g = divmod(seg, last - first)
+                a_wide[q, row + j, first + g] = wide[:, K_PASS * (seg - lo) : K_PASS * (seg - lo + 1)]
 
-        def adj_mult(i, c=0, pieces=1):
-            q, j = divmod(i, 2)
-            cols = slice(NODES // pieces * c, NODES // pieces * (c + 1))
+        def widen_v(q, first, last, lo, hi, row=0):
+            widen(nc.vector.tensor_copy, q, first, last, lo, hi, row)
+
+        def widen_s(q, first, last, lo, hi, row=0):
+            widen(nc.scalar.copy, q, first, last, lo, hi, row)
+
+        def adj_turn(q, g, rows=(0, 1)):
+            bank = tp.tile([P, 2, P * len(rows)], F32, name="a_bank")
+            a_bank[q, g, rows[0]] = bank
+            for i, j in enumerate(rows):
+                words = a_wide[q, j, g].bitcast(F32)
+                for u in range(2):
+                    nc.tensor.transpose(bank[:, u, P * i : P * (i + 1)], words[:, u : 2 * P : 2], ident[:])
+
+        def adj_mult(q, g, rows=(0, 1)):
+            if g != 1 and rows[0] == 0:
+                grouped = keep.tile([P, (8 - 2 * g) * PAIR_ROWS], BF16, name="a_grp%d_%d" % (q, g), align_bytes=64)
+                a_grp[q, g] = grouped
+            first = 4 * (PAIR_ROWS * (g % 2) + P * rows[0])
+            part = a_grp[q, g - g % 2][:, first : first + 4 * P * len(rows)]
+            halves = a_bank[q, g, rows[0]][:].rearrange("p u r -> p (u r)").bitcast(BF16)
+            factor = scale_cols[:, g, :].rearrange("p (o u e) -> p o u e", o=1, u=2)
             nc.vector.tensor_tensor(
-                out=a_vals[:, q, j, cols],
-                in0=a_raw[q][:, j, cols].bitcast(E4M3),
-                in1=scale[:, cols],
+                out=part.rearrange("p (r u e) -> p r u e", u=2, e=2),
+                in0=halves.rearrange("p (u r e) -> p r u e", u=2, e=2),
+                in1=factor.to_broadcast([P, P * len(rows), 2, 2]),
                 op=ALU.mult,
             )
 
-        def turn(runs, grouped):
-            bank = tp.tile([P, 4, P], F32, name="bank")
-            for a in range(2):
-                for u in range(2):
-                    nc.tensor.transpose(bank[:, 2 * a + u, :], runs[a][:, u : 2 * P : 2], ident[:])
-            nc.scalar.copy(
-                out=grouped.bitcast(F32).rearrange("p (a m u) -> p a m u", a=2, u=2),
-                in_=bank[:].rearrange("p (a u) m -> p a m u", a=2),
+        def adj_quant(q, first, last):
+            lo = first - first % 2
+            part = a_grp[q, lo][:, 4 * PAIR_ROWS * (first - lo) : 4 * PAIR_ROWS * (last - lo)]
+            gs = slice(first, last)
+            nc.vector.quantize_mx(
+                out=a_codes[:, q, gs, :].rearrange("p g r -> p (g r)").bitcast(E4M3X4),
+                scales=a_plane[:, q, gs, :].rearrange("p g r -> p (g r)"),
+                in_=part,
             )
 
         def x_turn(g, b):
             if b == 0:
-                grouped = wide.tile([P, 4 * K_PASS], BF16, name="x_grouped", align_bytes=64)
+                grouped = keep.tile([P, 4 * K_PASS], BF16, name="x_grp%d" % g, align_bytes=64)
                 x_grp[g] = grouped
-            runs = [x_raw[g][:, 2 * b + a, :].bitcast(F32) for a in range(2)]
-            turn(runs, x_grp[g][:, 8 * P * b : 8 * P * (b + 1)])
+            bank = sums.tile([P, 4, P], F32, name="bank")
+            for a in range(2):
+                words = x_raw[g, b][:, a, :].bitcast(F32)
+                for u in range(2):
+                    nc.tensor.transpose(bank[:, 2 * a + u, :], words[:, u : 2 * P : 2], ident[:])
+            banks["x", g, b] = bank
+
+        def x_out(g, b):
+            bank = banks["x", g, b]
+            part = x_grp[g][:, 8 * P * b : 8 * P * (b + 1)]
+            nc.scalar.copy(
+                out=part.bitcast(F32).rearrange("p (a m u) -> p a m u", a=2, u=2),
+                in_=bank[:].rearrange("p (a u) m -> p a m u", a=2),
+            )
 
         def x_quant(g):
             nc.vector.quantize_mx(out=x_codes[:, g, :].bitcast(E4M3X4), scales=x_plane[:, g, :], in_=x_grp[g][:])
 
-        def stage1(g):
-            grouped = wide.tile([P, 4 * HID], BF16, name="s_grouped", align_bytes=64)
-            s_grp[g] = grouped
-            for c in range(HID // P):
-                bank = tp.tile([P, 4, P], F32, name="bank")
-                for t in range(4):
-                    cols = slice(P * t, P * (t + 1))
-                    nc.tensor.matmul_mx(
-                        out=bank[:, t, :],
-                        lhsT=x_codes[:, g, cols].bitcast(E4M3X4),
-                        lhsT_scale=x_plane[:, g, cols],
-                        rhs=w_codes[:, 2 * P * c : 2 * P * (c + 1)].bitcast(E2M1X4),
-                        rhs_scale=w_plane[:, P * c : P * (c + 1)],
-                        start=True,
-                        stop=True,
-                    )
-                nc.scalar.copy(
-                    out=grouped[:, 4 * P * c : 4 * P * (c + 1)].rearrange("p (n t) -> p n t", t=4),
-                    in_=bank[:].rearrange("p t n -> p n t"),
+        def stage1(g, c):
+            if c == 0:
+                grouped = keep.tile([P, 4 * HID], BF16, name="s_grp%d" % g, align_bytes=64)
+                s_grp[g] = grouped
+            bank = sums.tile([P, 4, P], F32, name="bank")
+            for t in range(4):
+                cols = slice(P * t, P * (t + 1))
+                nc.tensor.matmul_mx(
+                    out=bank[:, t, :],
+                    lhsT=x_codes[:, g, cols].bitcast(E4M3X4),
+                    lhsT_scale=x_plane[:, g, cols],
+                    rhs=w_codes[:, 2 * P * c : 2 * P * (c + 1)].bitcast(E2M1X4),
+                    rhs_scale=w_plane[:, P * c : P * (c + 1)],
+                    start=True,
+                    stop=True,
                 )
+            banks["s", g, c] = bank
+
+        def s_out(g, c):
+            bank = banks["s", g, c]
+            nc.scalar.copy(
+                out=s_grp[g][:, 4 * P * c : 4 * P * (c + 1)].rearrange("p (n t) -> p n t", t=4),
+                in_=bank[:].rearrange("p t n -> p n t"),
+            )
 
         def s_quant(g):
             nc.vector.quantize_mx(out=s_codes[:, g, :].bitcast(E4M3X4), scales=s_plane[:, g, :], in_=s_grp[g][:])
 
-        def adj_turn(q, g):
-            if g == 0:
-                grouped = narrow.tile([P, PASSES, 4 * PAIR_ROWS], BF16, name="a_grouped", align_bytes=64)
-                a_grp[q] = grouped
-            runs = [a_vals[:, q, j, K_PASS * g : K_PASS * (g + 1)].bitcast(F32) for j in range(2)]
-            turn(runs, a_grp[q][:, g, :])
-
-        def adj_quant(q):
-            for gs in (slice(0, 2), slice(2, 3)):
-                nc.vector.quantize_mx(
-                    out=a_codes[:, q, gs, :].rearrange("p g r -> p (g r)").bitcast(E4M3X4),
-                    scales=a_plane[:, q, gs, :].rearrange("p g r -> p (g r)"),
-                    in_=a_grp[q][:, gs, :].rearrange("p g r -> p (g r)"),
-                )
-
         def out_rows(q):
             return out[PAIR_ROWS * q : PAIR_ROWS * (q + 1), :].rearrange("(m j) h -> m j h", j=2)
 
-        def stage2(q, j):
-            total = sums.tile([P, HID], F32, name="total")
-            acc[q, j] = total
-            for g in range(PASSES):
+        def stage2(q, j, first=0, last=PASSES):
+            if first == 0:
+                total = sums.tile([P, HID], F32, name="bank")
+                acc[q, j] = total
+            for g in range(first, last):
                 cols = slice(P * j, P * (j + 1))
                 nc.tensor.matmul_mx(
-                    out=total[:],
+                    out=acc[q, j][:],
                     lhsT=a_codes[:, q, g, cols].bitcast(E4M3X4),
                     lhsT_scale=a_plane[:, q, g, cols],
                     rhs=s_codes[:, g, :].bitcast(E4M3X4),
@@ -192,152 +201,199 @@ def tile_gcn_pa_w4_kernel(tc, x_init, adj_bytes, adj_scale, w_words, w_scales, b
                     stop=(g == PASSES - 1),
                 )
 
-        def finish(q, j, pieces=1):
-            if j == 0:
-                res = results.tile([P, 2, HID], F32, name="res")
-                result[q] = res
-            for c in range(pieces):
-                cols = slice(HID // pieces * c, HID // pieces * (c + 1))
-                part = result[q][:, j, cols]
-                nc.vector.tensor_tensor(out=part, in0=acc[q, j][:, cols], in1=bias[:, cols], op=ALU.add)
-                nc.scalar.activation(out=part, in_=part, func=ACT.Relu)
-                nc.sync.dma_start(out=out_rows(q)[:, j, cols], in_=part)
+        def add_bias(q, j, c=0, pieces=1):
+            cols = slice(HID // pieces * c, HID // pieces * (c + 1))
+            part = keep.tile([P, HID // pieces], F32, name="res%d_%d_%d" % (q, j, c))
+            result[q, j, c] = part
+            nc.vector.tensor_tensor(out=part[:], in0=acc[q, j][:, cols], in1=bias[:, cols], op=ALU.add)
 
-        def stage2_flipped(q, h):
-            if h == 0:
-                flat = flipped.tile([P, 4, PAIR_ROWS], F32, name="flat")
-                flip[q] = flat
-            total = sums.tile([P, HID], F32, name="total")
-            halves = [total[:, PAIR_ROWS * i : PAIR_ROWS * (i + 1)] for i in range(2)]
-            for i in range(2):
-                cols = slice(P * (2 * h + i), P * (2 * h + i + 1))
-                for g in range(PASSES):
-                    nc.tensor.matmul_mx(
-                        out=halves[i],
-                        lhsT=s_codes[:, g, cols].bitcast(E4M3X4),
-                        lhsT_scale=s_plane[:, g, cols],
-                        rhs=a_codes[:, q, g, :].bitcast(E4M3X4),
-                        rhs_scale=a_plane[:, q, g, :],
-                        start=(g == 0),
-                        stop=(g == PASSES - 1),
-                    )
-            for i in range(2):
-                c = 2 * h + i
-                nc.scalar.activation(
-                    out=flip[q][:, c, :], in_=halves[i], func=ACT.Relu, bias=bias_col[:, c : c + 1]
-                )
+        def relu_store(q, j, c=0, pieces=1):
+            cols = slice(HID // pieces * c, HID // pieces * (c + 1))
+            part = result[q, j, c]
+            nc.scalar.activation(out=part[:], in_=part[:], func=ACT.Relu)
+            nc.sync.dma_start(out=out_rows(q)[:, j, cols], in_=part[:])
 
-        def flip_back(q, j):
+        def finish(q, j, c=0, pieces=1):
+            add_bias(q, j, c, pieces)
+            relu_store(q, j, c, pieces)
+
+        def turn(i):
+            adj_turn(*divmod(i, PASSES))
+
+        def mult(i):
+            adj_mult(*divmod(i, PASSES))
+
+        def pair_quant(q):
+            adj_quant(q, 2, 3)
+            adj_quant(q, 0, 2)
+
+        def widen_pair(q):
+            widen_s(q, 0, PASSES, 0, 2 * PASSES)
+
+        def park(q, j):
             if j == 0:
-                res = results.tile([P, 2, HID], F32, name="res")
-                result[q] = res
-            bank = tp.tile([P, 4, P], F32, name="bank")
-            for c in range(4):
-                nc.tensor.transpose(bank[:, c, :], flip[q][:, c, P * j : P * (j + 1)], ident[:])
-            nc.scalar.copy(out=result[q][:, j, :], in_=bank[:].rearrange("p c m -> p (c m)"))
-            nc.sync.dma_start(out=out_rows(q)[:, j, :], in_=result[q][:, j, :])
+                parked = keep.tile([P, 2, HID], F32, name="parked%d" % q)
+                flip[q] = parked
+            nc.scalar.copy(out=flip[q][:, j, :], in_=acc[q, j][:])
+
+        def pool_bias(q, host):
+            res = a_grp[host, 0][:].bitcast(F32).rearrange("p (j h) -> p j h", j=2)
+            result[q] = res
+            spread = bias[:].rearrange("p (o h) -> p o h", o=1).to_broadcast([P, 2, HID])
+            nc.gpsimd.tensor_tensor(out=res, in0=flip[q][:], in1=spread, op=ALU.add)
+
+        def pool_store(q, j):
+            part = result[q][:, j, :]
+            nc.scalar.activation(out=part, in_=part, func=ACT.Relu)
+            nc.sync.dma_start(out=out_rows(q)[:, j, :], in_=part)
 
         with tc.manual_schedule():
             make_identity(nc, ident[:])
             nc.gpsimd.memset(w_plane[:].bitcast(I32), 0)
-            nc.gpsimd.memset(bias_rows[:], 0.0)
-            load_scale(0)
-            load_adj(0, 0, K_PASS)
-            load_scale(1)
-            load_scale(2)
-            load_x(0, 0, 2)
-            load_adj(0, K_PASS, NODES)
-            load_x(0, 1, 2)
-            load_x(1)
+            load_scale()
+            load_adj(0, 0, 1)
+            load_x(0, 0)
+            load_adj(0, 1, 3)
+            load_x(0, 1)
             load_adj(1)
-            load_x(2)
+            load_x_whole(1)
             load_w_codes()
             load_w_plane()
-            nc.sync.dma_start(out=bias_rows[0:4, :], in_=b1.rearrange("(c m) -> c m", m=P))
-            for q in range(2, PAIRS):
+            load_adj(2)
+            load_x_whole(2)
+            for q in range(3, PAIRS):
                 load_adj(q)
-            nc.sync.dma_start(out=bias[:], in_=b1.partition_broadcast(P))
+            load_bias()
 
-            spread_scale(0)
-            spread_scale(1)
-            spread_scale(2)
-            adj_mult(0, 0, 3)
-            adj_mult(1, 0, 3)
+            widen_v(0, 0, 1, 0, 2)
+            widen_v(0, 1, 3, 0, 2)
+            widen_s(0, 1, 3, 2, 4)
+            turn(0)
             x_turn(0, 0)
+            turn(1)
             x_turn(0, 1)
-            adj_mult(0, 1, 3)
-            adj_mult(1, 1, 3)
-            adj_turn(0, 0)
+            turn(2)
+            x_out(0, 0)
+            widen_s(1, 0, 3, 0, 3)
+            x_out(0, 1)
+            widen_s(1, 0, 3, 3, 6)
+            mult(0)
+            mult(1)
             x_turn(1, 0)
             x_turn(1, 1)
-            adj_mult(0, 2, 3)
-            adj_mult(1, 2, 3)
-            adj_turn(0, 1)
+            turn(3)
+            turn(4)
+            x_out(1, 0)
+            x_out(1, 1)
+            widen_pair(2)
             x_quant(0)
+            mult(2)
+            adj_quant(0, 0, 2)
+            x_quant(1)
+            for c in range(4):
+                stage1(0, c)
+            turn(5)
+            for c in range(4):
+                s_out(0, c)
             x_turn(2, 0)
             x_turn(2, 1)
-            adj_mult(2)
-            x_quant(1)
-            adj_turn(0, 2)
-            x_quant(2)
-            stage1(0)
-            adj_mult(3)
-            stage1(1)
-            adj_mult(4)
-            stage1(2)
-            turn_bias()
-            adj_mult(5)
-            adj_quant(0)
-            adj_turn(1, 0)
-            adj_turn(1, 1)
-            adj_turn(1, 2)
-            adj_turn(2, 0)
-            adj_turn(2, 1)
-            adj_turn(2, 2)
+            turn(6)
+            stage1(1, 0)
+            stage1(1, 1)
+            x_out(2, 0)
+            x_out(2, 1)
+            mult(3)
+            adj_quant(0, 2, 3)
+            mult(4)
+            mult(5)
+            adj_quant(1, 0, 2)
             s_quant(0)
+            x_quant(2)
+            stage1(1, 2)
+            stage1(1, 3)
+            s_out(1, 0)
+            s_out(1, 1)
+            widen_pair(3)
+            s_out(1, 2)
+            s_out(1, 3)
+            turn(7)
+            turn(8)
+            for c in range(4):
+                stage1(2, c)
+            for c in range(4):
+                s_out(2, c)
+            mult(6)
+            adj_quant(1, 2, 3)
+            turn(9)
+            turn(10)
+            mult(7)
             s_quant(1)
+            stage2(0, 0, 0, 2)
+            stage2(0, 1, 0, 2)
+            turn(11)
+            stage2(1, 0, 0, 2)
+            stage2(1, 1, 0, 2)
+            widen_pair(4)
+            mult(8)
+            mult(9)
             s_quant(2)
-            adj_mult(6)
-            adj_quant(1)
-            adj_quant(2)
-            adj_mult(7)
-            stage2_flipped(0, 0)
-            stage2_flipped(0, 1)
-            stage2_flipped(1, 0)
-            stage2_flipped(1, 1)
+
+            stage2(0, 0, 2, 3)
+            stage2(0, 1, 2, 3)
+            turn(12)
+            stage2(1, 0, 2, 3)
+            stage2(1, 1, 2, 3)
+            turn(13)
+            park(0, 0)
+            park(0, 1)
+            mult(10)
+            pair_quant(2)
+            pool_bias(0, 2)
+            widen_pair(5)
+            park(1, 0)
+            park(1, 1)
             stage2(2, 0)
-            flip_back(0, 0)
-            adj_turn(3, 0)
-            adj_turn(3, 1)
-            adj_turn(3, 2)
-            flip_back(1, 0)
-            adj_mult(8)
-            adj_mult(9)
-            adj_quant(3)
+            turn(14)
+            mult(11)
+            turn(15)
             stage2(2, 1)
-            finish(2, 0)
-            adj_mult(10)
-            flip_back(0, 1)
-            adj_turn(4, 0)
-            adj_turn(4, 1)
-            adj_turn(4, 2)
+            park(2, 0)
+            pool_store(0, 0)
+            pool_store(0, 1)
+            park(2, 1)
+            mult(12)
+            mult(13)
+            pair_quant(3)
+            pool_bias(1, 3)
+            turn(16)
             stage2(3, 0)
+            turn(17)
             stage2(3, 1)
-            adj_mult(11)
-            flip_back(1, 1)
-            adj_turn(5, 0)
-            adj_turn(5, 1)
-            adj_turn(5, 2)
-            finish(2, 1)
-            adj_quant(4)
+            pool_store(1, 0)
+            pool_store(1, 1)
+            mult(14)
+            mult(15)
             finish(3, 0)
+            pair_quant(4)
+            adj_quant(5, 0, 1)
+            pool_bias(2, 4)
             stage2(4, 0)
-            finish(3, 1)
-            adj_quant(5)
             stage2(4, 1)
+            finish(3, 1)
+            stage2(5, 0, 0, 1)
+            stage2(5, 1, 0, 1)
+            mult(16)
+            mult(17)
+            pool_store(2, 0)
+            pool_store(2, 1)
+            adj_quant(5, 1, 2)
+            stage2(5, 0, 1, 2)
+            stage2(5, 1, 1, 2)
             finish(4, 0)
+            adj_quant(5, 2, 3)
+            stage2(5, 0, 2, 3)
+            stage2(5, 1, 2, 3)
             finish(4, 1)
-            stage2(5, 0)
-            stage2(5, 1)
             finish(5, 0)
-            finish(5, 1, 2)
+            finish(5, 1, 0, 2)
+            finish(5, 1, 1, 2)

@@ -85,10 +85,12 @@ def tile_gcn_pa_w4_kernel(tc, x_init, adj_bytes, adj_scale, w_words, w_scales, b
         def load_bias():
             nc.sync.dma_start(out=bias[:], in_=b1.partition_broadcast(P))
 
-        def widen(copy, q, first, last, lo, hi, row=0):
-            wide = keep.tile([P, K_PASS * (hi - lo)], BF16, name="a_wide%d_%d_%d_%d" % (q, first, lo, row))
+        def widen(copy, q, first, last, lo, hi, row=0, host=None):
+            if host is None:
+                host = keep.tile([P, K_PASS * (hi - lo)], BF16, name="a_wide%d_%d_%d_%d" % (q, first, lo, row))
+            wide = host[:, 0 : K_PASS * (hi - lo)]
             flat = a_raw[q, first, row][:].rearrange("p j k -> p (j k)")
-            copy(out=wide[:], in_=flat[:, K_PASS * lo : K_PASS * hi].bitcast(E4M3))
+            copy(out=wide, in_=flat[:, K_PASS * lo : K_PASS * hi].bitcast(E4M3))
             for seg in range(lo, hi):
                 j, g = divmod(seg, last - first)
                 a_wide[q, row + j, first + g] = wide[:, K_PASS * (seg - lo) : K_PASS * (seg - lo + 1)]
@@ -99,6 +101,9 @@ def tile_gcn_pa_w4_kernel(tc, x_init, adj_bytes, adj_scale, w_words, w_scales, b
         def widen_s(q, first, last, lo, hi, row=0):
             widen(nc.scalar.copy, q, first, last, lo, hi, row)
 
+        def widen_g(q, lo, hi, host):
+            widen(nc.gpsimd.tensor_copy, q, 0, PASSES, lo, hi, 0, host)
+
         def adj_turn(q, g, rows=(0, 1)):
             bank = tp.tile([P, 2, P * len(rows)], F32, name="a_bank")
             a_bank[q, g, rows[0]] = bank
@@ -108,11 +113,11 @@ def tile_gcn_pa_w4_kernel(tc, x_init, adj_bytes, adj_scale, w_words, w_scales, b
                     nc.tensor.transpose(bank[:, u, P * i : P * (i + 1)], words[:, u : 2 * P : 2], ident[:])
 
         def adj_mult(q, g, rows=(0, 1)):
-            if g != 1 and rows[0] == 0:
-                grouped = keep.tile([P, (8 - 2 * g) * PAIR_ROWS], BF16, name="a_grp%d_%d" % (q, g), align_bytes=64)
-                a_grp[q, g] = grouped
-            first = 4 * (PAIR_ROWS * (g % 2) + P * rows[0])
-            part = a_grp[q, g - g % 2][:, first : first + 4 * P * len(rows)]
+            if g == 0 and rows[0] == 0:
+                grouped = keep.tile([P, 4 * PASSES * PAIR_ROWS], BF16, name="a_grp%d" % q, align_bytes=64)
+                a_grp[q] = grouped
+            first = 4 * (PAIR_ROWS * g + P * rows[0])
+            part = a_grp[q][:, first : first + 4 * P * len(rows)]
             halves = a_bank[q, g, rows[0]][:].rearrange("p u r -> p (u r)").bitcast(BF16)
             factor = scale_cols[:, g, :].rearrange("p (o u e) -> p o u e", o=1, u=2)
             nc.vector.tensor_tensor(
@@ -123,8 +128,7 @@ def tile_gcn_pa_w4_kernel(tc, x_init, adj_bytes, adj_scale, w_words, w_scales, b
             )
 
         def adj_quant(q, first, last):
-            lo = first - first % 2
-            part = a_grp[q, lo][:, 4 * PAIR_ROWS * (first - lo) : 4 * PAIR_ROWS * (last - lo)]
+            part = a_grp[q][:, 4 * PAIR_ROWS * first : 4 * PAIR_ROWS * last]
             gs = slice(first, last)
             nc.vector.quantize_mx(
                 out=a_codes[:, q, gs, :].rearrange("p g r -> p (g r)").bitcast(E4M3X4),
@@ -237,7 +241,7 @@ def tile_gcn_pa_w4_kernel(tc, x_init, adj_bytes, adj_scale, w_words, w_scales, b
             nc.scalar.copy(out=flip[q][:, j, :], in_=acc[q, j][:])
 
         def pool_bias(q, host):
-            res = a_grp[host, 0][:].bitcast(F32).rearrange("p (j h) -> p j h", j=2)
+            res = a_grp[host][:, 0 : 4 * HID].bitcast(F32).rearrange("p (j h) -> p j h", j=2)
             result[q] = res
             spread = bias[:].rearrange("p (o h) -> p o h", o=1).to_broadcast([P, 2, HID])
             nc.gpsimd.tensor_tensor(out=res, in0=flip[q][:], in1=spread, op=ALU.add)
@@ -246,6 +250,10 @@ def tile_gcn_pa_w4_kernel(tc, x_init, adj_bytes, adj_scale, w_words, w_scales, b
             part = result[q][:, j, :]
             nc.scalar.activation(out=part, in_=part, func=ACT.Relu)
             nc.sync.dma_start(out=out_rows(q)[:, j, :], in_=part)
+
+        def widen_pass(q, g):
+            for j in range(2):
+                widen_s(q, 0, PASSES, PASSES * j + g, PASSES * j + g + 1)
 
         with tc.manual_schedule():
             make_identity(nc, ident[:])
@@ -277,8 +285,8 @@ def tile_gcn_pa_w4_kernel(tc, x_init, adj_bytes, adj_scale, w_words, w_scales, b
             widen_s(1, 0, 3, 0, 3)
             x_out(0, 1)
             widen_s(1, 0, 3, 3, 6)
-            mult(0)
-            mult(1)
+            for i in range(3):
+                mult(i)
             x_turn(1, 0)
             x_turn(1, 1)
             turn(3)
@@ -287,7 +295,6 @@ def tile_gcn_pa_w4_kernel(tc, x_init, adj_bytes, adj_scale, w_words, w_scales, b
             x_out(1, 1)
             widen_pair(2)
             x_quant(0)
-            mult(2)
             adj_quant(0, 0, 2)
             x_quant(1)
             for c in range(4):
@@ -307,78 +314,79 @@ def tile_gcn_pa_w4_kernel(tc, x_init, adj_bytes, adj_scale, w_words, w_scales, b
             mult(4)
             mult(5)
             adj_quant(1, 0, 2)
-            s_quant(0)
             x_quant(2)
+            s_quant(0)
             stage1(1, 2)
             stage1(1, 3)
-            s_out(1, 0)
-            s_out(1, 1)
-            widen_pair(3)
-            s_out(1, 2)
-            s_out(1, 3)
+            for c in range(4):
+                s_out(1, c)
             turn(7)
             turn(8)
             for c in range(4):
                 stage1(2, c)
+            widen_pass(3, 0)
             for c in range(4):
                 s_out(2, c)
             mult(6)
             adj_quant(1, 2, 3)
             turn(9)
-            turn(10)
             mult(7)
             s_quant(1)
             stage2(0, 0, 0, 2)
             stage2(0, 1, 0, 2)
-            turn(11)
-            stage2(1, 0, 0, 2)
-            stage2(1, 1, 0, 2)
-            widen_pair(4)
+            widen_pass(3, 1)
+            turn(10)
+            widen_pass(3, 2)
+            widen_pass(4, 0)
             mult(8)
-            mult(9)
+            adj_quant(2, 0, 2)
             s_quant(2)
 
             stage2(0, 0, 2, 3)
             stage2(0, 1, 2, 3)
+            turn(11)
+            mult(9)
+            adj_quant(2, 2, 3)
             turn(12)
-            stage2(1, 0, 2, 3)
-            stage2(1, 1, 2, 3)
-            turn(13)
             park(0, 0)
             park(0, 1)
-            mult(10)
-            pair_quant(2)
             pool_bias(0, 2)
-            widen_pair(5)
+            widen_pass(4, 1)
+            widen_pass(4, 2)
+            stage2(1, 0)
+            stage2(1, 1)
             park(1, 0)
             park(1, 1)
-            stage2(2, 0)
+            widen_pair(5)
+            mult(10)
+            turn(13)
             turn(14)
-            mult(11)
-            turn(15)
+            stage2(2, 0)
             stage2(2, 1)
-            park(2, 0)
             pool_store(0, 0)
             pool_store(0, 1)
+            park(2, 0)
             park(2, 1)
+            mult(11)
             mult(12)
-            mult(13)
             pair_quant(3)
             pool_bias(1, 3)
+            turn(15)
             turn(16)
             stage2(3, 0)
-            turn(17)
             stage2(3, 1)
             pool_store(1, 0)
             pool_store(1, 1)
+            mult(13)
+            turn(17)
             mult(14)
             mult(15)
-            finish(3, 0)
             pair_quant(4)
             adj_quant(5, 0, 1)
             pool_bias(2, 4)
             stage2(4, 0)
             stage2(4, 1)
+            finish(3, 0)
             finish(3, 1)
             stage2(5, 0, 0, 1)
             stage2(5, 1, 0, 1)
@@ -394,6 +402,7 @@ def tile_gcn_pa_w4_kernel(tc, x_init, adj_bytes, adj_scale, w_words, w_scales, b
             stage2(5, 0, 2, 3)
             stage2(5, 1, 2, 3)
             finish(4, 1)
-            finish(5, 0)
+            finish(5, 0, 0, 2)
+            finish(5, 0, 1, 2)
             finish(5, 1, 0, 2)
             finish(5, 1, 1, 2)

@@ -22,6 +22,8 @@ PASSES = NODES // K_PASS
 PAIR_ROWS = 2 * P
 PAIRS = NODES // PAIR_ROWS
 
+QUANT_STARTS = (0, 4, 6, 10, 14, 16, 17, 18)
+
 FLOPS = 2 * NODES * FEAT * HID + 2 * NODES * NODES * HID
 
 
@@ -35,6 +37,9 @@ def tile_gcn_pa_w4_kernel(tc, x_init, adj_bytes, adj_scale, w_words, w_scales, b
         ident = keep.tile([P, P], F32, name="ident")
         scale_cols = keep.tile([P, PASSES, 4], F32, name="scale_cols")
         bias = keep.tile([P, HID], BF16, name="bias")
+        bias_rows = keep.tile([P, P], BF16, name="bias_rows")
+        bias_rows_f32 = keep.tile([P, P], F32, name="bias_rows_f32")
+        bias_col = keep.tile([P, 4], F32, name="bias_col")
         w_codes = keep.tile([P, 2 * HID], U8, name="w_codes", align_bytes=64)
         w_plane = keep.tile([P, HID], U8, name="w_plane", align_bytes=64)
         x_codes = keep.tile([P, PASSES, K_PASS], U32, name="x_codes", align_bytes=64)
@@ -44,8 +49,11 @@ def tile_gcn_pa_w4_kernel(tc, x_init, adj_bytes, adj_scale, w_words, w_scales, b
         a_codes = keep.tile([P, PAIRS, PASSES, PAIR_ROWS], U32, name="a_codes", align_bytes=64)
         a_plane = keep.tile([P, PAIRS, PASSES, PAIR_ROWS], U8, name="a_plane", align_bytes=64)
 
+        s_early = keep.tile([P, 8 * HID], BF16, name="s_early", align_bytes=64)
+        s_late = keep.tile([P, 4 * HID], BF16, name="s_late", align_bytes=64)
         a_raw, a_wide, a_bank, a_grp = {}, {}, {}, {}
-        x_raw, x_grp, s_grp = {}, {}, {}
+        x_raw, x_grp = {}, {}
+        s_grp = [s_early[:, 0 : 4 * HID], s_early[:, 4 * HID : 8 * HID], s_late[:]]
         acc, flip, result, banks = {}, {}, {}, {}
 
         def load_scale():
@@ -82,8 +90,19 @@ def tile_gcn_pa_w4_kernel(tc, x_init, adj_bytes, adj_scale, w_words, w_scales, b
                     in_=w_scales[0, 4 * quad : 4 * quad + 4, :].bitcast(I32),
                 )
 
+        def load_bias_rows():
+            nc.sync.dma_start(out=bias_rows[0:4, :], in_=b1.rearrange("(c m) -> c m", m=P))
+
         def load_bias():
             nc.sync.dma_start(out=bias[:], in_=b1.partition_broadcast(P))
+
+        def cast_bias():
+            nc.scalar.copy(out=bias_rows_f32[:], in_=bias_rows[:])
+
+        def turn_bias():
+            bank = sums.tile([P, 4, P], F32, name="bank")
+            nc.tensor.transpose(bank[:, 0, :], bias_rows_f32[:], ident[:])
+            nc.scalar.copy(out=bias_col[:], in_=bank[:, 0, 0:4])
 
         def widen(copy, q, first, last, lo, hi, row=0, host=None):
             if host is None:
@@ -113,11 +132,14 @@ def tile_gcn_pa_w4_kernel(tc, x_init, adj_bytes, adj_scale, w_words, w_scales, b
                     nc.tensor.transpose(bank[:, u, P * i : P * (i + 1)], words[:, u : 2 * P : 2], ident[:])
 
         def adj_mult(q, g, rows=(0, 1)):
-            if g == 0 and rows[0] == 0:
-                grouped = keep.tile([P, 4 * PASSES * PAIR_ROWS], BF16, name="a_grp%d" % q, align_bytes=64)
-                a_grp[q] = grouped
-            first = 4 * (PAIR_ROWS * g + P * rows[0])
-            part = a_grp[q][:, first : first + 4 * P * len(rows)]
+            i = PASSES * q + g
+            lo = max(s for s in QUANT_STARTS if s <= i)
+            if i == lo and rows[0] == 0:
+                hi = min(s for s in QUANT_STARTS if s > i)
+                grouped = keep.tile([P, 4 * PAIR_ROWS * (hi - lo)], BF16, name="a_grp%d" % lo, align_bytes=64)
+                a_grp[lo] = grouped
+            first = 4 * (PAIR_ROWS * (i - lo) + P * rows[0])
+            part = a_grp[lo][:, first : first + 4 * P * len(rows)]
             halves = a_bank[q, g, rows[0]][:].rearrange("p u r -> p (u r)").bitcast(BF16)
             factor = scale_cols[:, g, :].rearrange("p (o u e) -> p o u e", o=1, u=2)
             nc.vector.tensor_tensor(
@@ -127,13 +149,13 @@ def tile_gcn_pa_w4_kernel(tc, x_init, adj_bytes, adj_scale, w_words, w_scales, b
                 op=ALU.mult,
             )
 
-        def adj_quant(q, first, last):
-            part = a_grp[q][:, 4 * PAIR_ROWS * first : 4 * PAIR_ROWS * last]
-            gs = slice(first, last)
+        def adj_quant(lo):
+            hi = min(s for s in QUANT_STARTS if s > lo)
+            cols = slice(PAIR_ROWS * lo, PAIR_ROWS * hi)
             nc.vector.quantize_mx(
-                out=a_codes[:, q, gs, :].rearrange("p g r -> p (g r)").bitcast(E4M3X4),
-                scales=a_plane[:, q, gs, :].rearrange("p g r -> p (g r)"),
-                in_=part,
+                out=a_codes[:].rearrange("p q g r -> p (q g r)")[:, cols].bitcast(E4M3X4),
+                scales=a_plane[:].rearrange("p q g r -> p (q g r)")[:, cols],
+                in_=a_grp[lo][:],
             )
 
         def x_turn(g, b):
@@ -159,9 +181,6 @@ def tile_gcn_pa_w4_kernel(tc, x_init, adj_bytes, adj_scale, w_words, w_scales, b
             nc.vector.quantize_mx(out=x_codes[:, g, :].bitcast(E4M3X4), scales=x_plane[:, g, :], in_=x_grp[g][:])
 
         def stage1(g, c):
-            if c == 0:
-                grouped = keep.tile([P, 4 * HID], BF16, name="s_grp%d" % g, align_bytes=64)
-                s_grp[g] = grouped
             bank = sums.tile([P, 4, P], F32, name="bank")
             for t in range(4):
                 cols = slice(P * t, P * (t + 1))
@@ -183,8 +202,12 @@ def tile_gcn_pa_w4_kernel(tc, x_init, adj_bytes, adj_scale, w_words, w_scales, b
                 in_=bank[:].rearrange("p t n -> p n t"),
             )
 
-        def s_quant(g):
-            nc.vector.quantize_mx(out=s_codes[:, g, :].bitcast(E4M3X4), scales=s_plane[:, g, :], in_=s_grp[g][:])
+        def s_quant(first, last, source):
+            nc.vector.quantize_mx(
+                out=s_codes[:, first:last, :].rearrange("p g h -> p (g h)").bitcast(E4M3X4),
+                scales=s_plane[:, first:last, :].rearrange("p g h -> p (g h)"),
+                in_=source[:],
+            )
 
         def out_rows(q):
             return out[PAIR_ROWS * q : PAIR_ROWS * (q + 1), :].rearrange("(m j) h -> m j h", j=2)
@@ -217,19 +240,63 @@ def tile_gcn_pa_w4_kernel(tc, x_init, adj_bytes, adj_scale, w_words, w_scales, b
             nc.scalar.activation(out=part[:], in_=part[:], func=ACT.Relu)
             nc.sync.dma_start(out=out_rows(q)[:, j, cols], in_=part[:])
 
+        def finish_shared(q, j):
+            add_bias(q, j)
+            res = result[q, j, 0]
+            left, right = slice(0, HID // 2), slice(HID // 2, HID)
+            nc.scalar.activation(out=res[:, left], in_=res[:, left], func=ACT.Relu)
+            nc.vector.tensor_scalar(out=res[:, right], in0=res[:, right], scalar1=0.0, scalar2=None, op0=ALU.max)
+            for cols in (right, left):
+                nc.sync.dma_start(out=out_rows(q)[:, j, cols], in_=res[:, cols])
+
         def finish(q, j, c=0, pieces=1):
             add_bias(q, j, c, pieces)
             relu_store(q, j, c, pieces)
+
+        def stage2_flipped(q, h):
+            if h == 0:
+                flat = keep.tile([P, 4, PAIR_ROWS], F32, name="flat%d" % q)
+                flip[q] = flat
+            total = sums.tile([P, HID], F32, name="bank")
+            halves = [total[:, PAIR_ROWS * i : PAIR_ROWS * (i + 1)] for i in range(2)]
+            for i in range(2):
+                cols = slice(P * (2 * h + i), P * (2 * h + i + 1))
+                for g in range(PASSES):
+                    nc.tensor.matmul_mx(
+                        out=halves[i],
+                        lhsT=s_codes[:, g, cols].bitcast(E4M3X4),
+                        lhsT_scale=s_plane[:, g, cols],
+                        rhs=a_codes[:, q, g, :].bitcast(E4M3X4),
+                        rhs_scale=a_plane[:, q, g, :],
+                        start=(g == 0),
+                        stop=(g == PASSES - 1),
+                    )
+            banks["f", q, h] = halves
+
+        def flip_relu(q, h):
+            for i in range(2):
+                c = 2 * h + i
+                nc.scalar.activation(
+                    out=flip[q][:, c, :], in_=banks["f", q, h][i], func=ACT.Relu, bias=bias_col[:, c : c + 1]
+                )
+
+        def flip_back(q, j, pool, tag):
+            bank = pool.tile([P, 4, P], F32, name=tag)
+            for c in range(4):
+                nc.tensor.transpose(bank[:, c, :], flip[q][:, c, P * j : P * (j + 1)], ident[:])
+            banks["b", q, j] = bank
+
+        def flip_out(q, j):
+            bank = banks["b", q, j]
+            res = keep.tile([P, HID], F32, name="res%d_%d" % (q, j))
+            nc.scalar.copy(out=res[:], in_=bank[:].rearrange("p c m -> p (c m)"))
+            nc.sync.dma_start(out=out_rows(q)[:, j, :], in_=res[:])
 
         def turn(i):
             adj_turn(*divmod(i, PASSES))
 
         def mult(i):
             adj_mult(*divmod(i, PASSES))
-
-        def pair_quant(q):
-            adj_quant(q, 2, 3)
-            adj_quant(q, 0, 2)
 
         def widen_pair(q):
             widen_s(q, 0, PASSES, 0, 2 * PASSES)
@@ -240,8 +307,8 @@ def tile_gcn_pa_w4_kernel(tc, x_init, adj_bytes, adj_scale, w_words, w_scales, b
                 flip[q] = parked
             nc.scalar.copy(out=flip[q][:, j, :], in_=acc[q, j][:])
 
-        def pool_bias(q, host):
-            res = a_grp[host][:, 0 : 4 * HID].bitcast(F32).rearrange("p (j h) -> p j h", j=2)
+        def pool_bias(q, host, half):
+            res = a_grp[host][:, 4 * HID * half : 4 * HID * (half + 1)].bitcast(F32).rearrange("p (j h) -> p j h", j=2)
             result[q] = res
             spread = bias[:].rearrange("p (o h) -> p o h", o=1).to_broadcast([P, 2, HID])
             nc.gpsimd.tensor_tensor(out=res, in0=flip[q][:], in1=spread, op=ALU.add)
@@ -258,12 +325,15 @@ def tile_gcn_pa_w4_kernel(tc, x_init, adj_bytes, adj_scale, w_words, w_scales, b
         with tc.manual_schedule():
             make_identity(nc, ident[:])
             nc.gpsimd.memset(w_plane[:].bitcast(I32), 0)
+            nc.gpsimd.memset(bias_rows[:], 0.0)
+            load_adj(0, 0, 1, (0,))
             load_scale()
-            load_adj(0, 0, 1)
-            load_x(0, 0)
+            load_adj(0, 0, 1, (1,))
             load_adj(0, 1, 3)
-            load_x(0, 1)
+            load_x(0, 0)
             load_adj(1)
+            load_x(0, 1)
+            load_bias_rows()
             load_x_whole(1)
             load_w_codes()
             load_w_plane()
@@ -273,136 +343,139 @@ def tile_gcn_pa_w4_kernel(tc, x_init, adj_bytes, adj_scale, w_words, w_scales, b
                 load_adj(q)
             load_bias()
 
-            widen_v(0, 0, 1, 0, 2)
-            widen_v(0, 1, 3, 0, 2)
-            widen_s(0, 1, 3, 2, 4)
-            turn(0)
-            x_turn(0, 0)
+            widen_v(0, 0, 1, 0, 1, 0)
+            widen_v(0, 0, 1, 0, 1, 1)
+            for seg in (0, 2, 1, 3):
+                widen_s(0, 1, 3, seg, seg + 1)
+            adj_turn(0, 0, (0,))
+            adj_turn(0, 0, (1,))
+            adj_mult(0, 0, (0,))
+            adj_mult(0, 0, (1,))
             turn(1)
-            x_turn(0, 1)
             turn(2)
+            x_turn(0, 0)
+            widen_s(1, 0, 3, 0, 4)
+            widen_g(1, 4, 6, None)
+            x_turn(0, 1)
+            turn(3)
             x_out(0, 0)
-            widen_s(1, 0, 3, 0, 3)
             x_out(0, 1)
-            widen_s(1, 0, 3, 3, 6)
-            for i in range(3):
+            cast_bias()
+            for i in range(1, 4):
                 mult(i)
             x_turn(1, 0)
             x_turn(1, 1)
-            turn(3)
             turn(4)
+            turn(5)
             x_out(1, 0)
             x_out(1, 1)
             widen_pair(2)
             x_quant(0)
-            adj_quant(0, 0, 2)
             x_quant(1)
+            adj_quant(0)
+            widen_g(3, 3, 6, a_grp[0])
+            mult(4)
             for c in range(4):
                 stage1(0, c)
-            turn(5)
             for c in range(4):
                 s_out(0, c)
+            turn(6)
             x_turn(2, 0)
             x_turn(2, 1)
-            turn(6)
+            turn(7)
             stage1(1, 0)
             stage1(1, 1)
             x_out(2, 0)
             x_out(2, 1)
-            mult(3)
-            adj_quant(0, 2, 3)
-            mult(4)
             mult(5)
-            adj_quant(1, 0, 2)
+            mult(6)
             x_quant(2)
-            s_quant(0)
+            adj_quant(4)
             stage1(1, 2)
             stage1(1, 3)
             for c in range(4):
                 s_out(1, c)
-            turn(7)
             turn(8)
             for c in range(4):
                 stage1(2, c)
-            widen_pass(3, 0)
+            widen_s(3, 0, 3, 0, 1)
             for c in range(4):
                 s_out(2, c)
-            mult(6)
-            adj_quant(1, 2, 3)
             turn(9)
+            turn_bias()
             mult(7)
-            s_quant(1)
+            s_quant(0, 2, s_early)
             stage2(0, 0, 0, 2)
             stage2(0, 1, 0, 2)
-            widen_pass(3, 1)
+            widen_s(3, 0, 3, 1, 3)
             turn(10)
-            widen_pass(3, 2)
-            widen_pass(4, 0)
+            widen_pair(4)
             mult(8)
-            adj_quant(2, 0, 2)
-            s_quant(2)
+            s_quant(2, 3, s_late)
 
             stage2(0, 0, 2, 3)
             stage2(0, 1, 2, 3)
             turn(11)
             mult(9)
-            adj_quant(2, 2, 3)
+            adj_quant(6)
             turn(12)
             park(0, 0)
             park(0, 1)
-            pool_bias(0, 2)
-            widen_pass(4, 1)
-            widen_pass(4, 2)
+            pool_bias(0, 6, 0)
             stage2(1, 0)
             stage2(1, 1)
             park(1, 0)
             park(1, 1)
+            pool_bias(1, 6, 1)
             widen_pair(5)
             mult(10)
             turn(13)
             turn(14)
-            stage2(2, 0)
-            stage2(2, 1)
+            stage2_flipped(2, 0)
+            stage2_flipped(2, 1)
+            flip_relu(2, 0)
+            flip_relu(2, 1)
             pool_store(0, 0)
             pool_store(0, 1)
-            park(2, 0)
-            park(2, 1)
             mult(11)
             mult(12)
-            pair_quant(3)
-            pool_bias(1, 3)
             turn(15)
             turn(16)
-            stage2(3, 0)
-            stage2(3, 1)
+            flip_back(2, 0, sums, "bank")
+            flip_back(2, 1, sums, "bank")
+            flip_out(2, 0)
+            flip_out(2, 1)
             pool_store(1, 0)
             pool_store(1, 1)
             mult(13)
             turn(17)
             mult(14)
+            adj_quant(10)
+            stage2_flipped(3, 0)
+            stage2_flipped(3, 1)
+            stage2(4, 0, 0, 2)
+            stage2(4, 1, 0, 2)
+            flip_relu(3, 0)
+            flip_relu(3, 1)
             mult(15)
-            pair_quant(4)
-            adj_quant(5, 0, 1)
-            pool_bias(2, 4)
-            stage2(4, 0)
-            stage2(4, 1)
-            finish(3, 0)
-            finish(3, 1)
+            flip_back(3, 0, tp, "a_bank")
+            flip_back(3, 1, tp, "a_bank")
+            flip_out(3, 0)
+            flip_out(3, 1)
+            mult(16)
+            adj_quant(14)
+            stage2(4, 0, 2, 3)
+            stage2(4, 1, 2, 3)
             stage2(5, 0, 0, 1)
             stage2(5, 1, 0, 1)
-            mult(16)
             mult(17)
-            pool_store(2, 0)
-            pool_store(2, 1)
-            adj_quant(5, 1, 2)
+            adj_quant(16)
             stage2(5, 0, 1, 2)
             stage2(5, 1, 1, 2)
             finish(4, 0)
-            adj_quant(5, 2, 3)
+            adj_quant(17)
             stage2(5, 0, 2, 3)
             stage2(5, 1, 2, 3)
             finish(4, 1)
-            finish(5, 0, 0, 2)
-            finish(5, 0, 1, 2)
-            finish(5, 1, 0, 2)
-            finish(5, 1, 1, 2)
+            finish(5, 0)
+            finish_shared(5, 1)

@@ -21,8 +21,13 @@ K_PASS = 4 * P
 PASSES = NODES // K_PASS
 PAIR_ROWS = 2 * P
 PAIRS = NODES // PAIR_ROWS
+SEGMENTS = 2 * PASSES
+CHUNKS = HID // P
 
-QUANT_STARTS = (0, 4, 6, 10, 14, 16, 17, 18)
+QUANT_STARTS = (0, 4, 6, 10, 12, 16, 17, 18)
+
+SLAB_BANKS = 4
+OTHER_BANKS = 4
 
 FLOPS = 2 * NODES * FEAT * HID + 2 * NODES * NODES * HID
 
@@ -31,15 +36,15 @@ def tile_gcn_pa_w4_kernel(tc, x_init, adj_bytes, adj_scale, w_words, w_scales, b
     nc = tc.nc
     with ExitStack() as ctx:
         keep = ctx.enter_context(tc.tile_pool(name="keep", bufs=1))
-        tp = ctx.enter_context(tc.psum_pool(name="tp", bufs=4))
-        sums = ctx.enter_context(tc.psum_pool(name="sums", bufs=4))
+        slab_psum = ctx.enter_context(tc.psum_pool(name="slab_psum", bufs=SLAB_BANKS))
+        other_psum = ctx.enter_context(tc.psum_pool(name="other_psum", bufs=OTHER_BANKS))
 
         ident = keep.tile([P, P], F32, name="ident")
         scale_cols = keep.tile([P, PASSES, 4], F32, name="scale_cols")
         bias = keep.tile([P, HID], BF16, name="bias")
         bias_rows = keep.tile([P, P], BF16, name="bias_rows")
         bias_rows_f32 = keep.tile([P, P], F32, name="bias_rows_f32")
-        bias_col = keep.tile([P, 4], F32, name="bias_col")
+        bias_col = keep.tile([P, CHUNKS], F32, name="bias_col")
         w_codes = keep.tile([P, 2 * HID], U8, name="w_codes", align_bytes=64)
         w_plane = keep.tile([P, HID], U8, name="w_plane", align_bytes=64)
         x_codes = keep.tile([P, PASSES, K_PASS], U32, name="x_codes", align_bytes=64)
@@ -48,104 +53,78 @@ def tile_gcn_pa_w4_kernel(tc, x_init, adj_bytes, adj_scale, w_words, w_scales, b
         s_plane = keep.tile([P, PASSES, HID], U8, name="s_plane", align_bytes=64)
         a_codes = keep.tile([P, PAIRS, PASSES, PAIR_ROWS], U32, name="a_codes", align_bytes=64)
         a_plane = keep.tile([P, PAIRS, PASSES, PAIR_ROWS], U8, name="a_plane", align_bytes=64)
+        s_grouped = [keep.tile([P, 4 * HID], BF16, name="s_grouped%d" % g, align_bytes=64) for g in range(PASSES)]
 
-        s_early = keep.tile([P, 8 * HID], BF16, name="s_early", align_bytes=64)
-        s_late = keep.tile([P, 4 * HID], BF16, name="s_late", align_bytes=64)
-        a_raw, a_wide, a_bank, a_grp = {}, {}, {}, {}
-        x_raw, x_grp = {}, {}
-        s_grp = [s_early[:, 0 : 4 * HID], s_early[:, 4 * HID : 8 * HID], s_late[:]]
-        acc, flip, result, banks = {}, {}, {}, {}
+        a_raw, a_wide, a_bank, a_grouped = {}, {}, {}, {}
+        x_raw, x_bank, x_grouped, s_bank = {}, {}, {}, {}
+        total, parked, pool_sum = {}, {}, {}
+        flip_total, flip_flat, back_bank, bias_bank = {}, {}, {}, {}
+
+        def slab_bank(shape):
+            return slab_psum.tile(shape, F32, name="slab_bank")
+
+        def other_bank(shape):
+            return other_psum.tile(shape, F32, name="other_bank")
+
 
         def load_scale():
             nc.sync.dma_start(out=scale_cols[:], in_=adj_scale.rearrange("o (g p t) -> p (o g) t", p=P, t=4))
 
-        def load_adj(q, first=0, last=PASSES, rows=(0, 1)):
-            width = K_PASS * (last - first)
-            raw = keep.tile([P, len(rows), width], U8, name="a_raw%d_%d_%d" % (q, first, rows[0]))
-            a_raw[q, first, rows[0]] = raw
+        def load_adj(q, first=0, last=PASSES, tiles=(0, 1)):
+            raw = keep.tile([P, len(tiles), K_PASS * (last - first)], U8, name="a_raw%d_%d_%d" % (q, first, tiles[0]))
+            a_raw[q, first, tiles[0]] = raw
             block = adj_bytes[PAIR_ROWS * q : PAIR_ROWS * (q + 1), K_PASS * first : K_PASS * last]
-            by_row = block.rearrange("(m j) k -> m j k", j=2)
-            nc.sync.dma_start(out=raw[:], in_=by_row[:, rows[0] : rows[-1] + 1, :])
+            by_tile = block.rearrange("(m j) k -> m j k", j=2)
+            nc.sync.dma_start(out=raw[:], in_=by_tile[:, tiles[0] : tiles[-1] + 1, :])
 
-        def load_x(g, b):
-            x = keep.tile([P, 2, FEAT], BF16, name="x_raw%d_%d" % (g, b))
-            x_raw[g, b] = x
-            rows = x_init[K_PASS * g : K_PASS * (g + 1), :].rearrange("(m t) f -> m t f", t=4)
-            nc.sync.dma_start(out=x[:], in_=rows[:, 2 * b : 2 * b + 2, :])
+        def load_x(g, halves):
+            raw = keep.tile([P, 2 * len(halves), FEAT], BF16, name="x_raw%d_%d" % (g, halves[0]))
+            for i, b in enumerate(halves):
+                x_raw[g, b] = raw[:, 2 * i : 2 * i + 2, :]
+            by_t = x_init[K_PASS * g : K_PASS * (g + 1), :].rearrange("(m t) f -> m t f", t=4)
+            nc.sync.dma_start(out=raw[:], in_=by_t[:, 2 * halves[0] : 2 * halves[-1] + 2, :])
 
-        def load_x_whole(g):
-            x = keep.tile([P, 4, FEAT], BF16, name="x_raw%d" % g)
-            x_raw[g, 0] = x[:, 0:2, :]
-            x_raw[g, 1] = x[:, 2:4, :]
-            rows = x_init[K_PASS * g : K_PASS * (g + 1), :].rearrange("(m t) f -> m t f", t=4)
-            nc.sync.dma_start(out=x[:], in_=rows)
-
-        def load_w_codes():
+        def load_w():
             nc.sync.dma_start(out=w_codes[:].bitcast(I32), in_=w_words[0].bitcast(I32))
-
-        def load_w_plane():
             for quad in range(4):
                 nc.sync.dma_start(
                     out=w_plane[32 * quad : 32 * quad + 4, :].bitcast(I32),
                     in_=w_scales[0, 4 * quad : 4 * quad + 4, :].bitcast(I32),
                 )
 
-        def load_bias_rows():
-            nc.sync.dma_start(out=bias_rows[0:4, :], in_=b1.rearrange("(c m) -> c m", m=P))
 
-        def load_bias():
-            nc.sync.dma_start(out=bias[:], in_=b1.partition_broadcast(P))
-
-        def cast_bias():
-            nc.scalar.copy(out=bias_rows_f32[:], in_=bias_rows[:])
-
-        def turn_bias():
-            bank = sums.tile([P, 4, P], F32, name="bank")
-            nc.tensor.transpose(bank[:, 0, :], bias_rows_f32[:], ident[:])
-            nc.scalar.copy(out=bias_col[:], in_=bank[:, 0, 0:4])
-
-        def widen(copy, q, first, last, lo, hi, row=0, host=None):
+        def widen(copy, q, lo, hi, first=0, last=PASSES, tile0=0, host=None):
             if host is None:
-                host = keep.tile([P, K_PASS * (hi - lo)], BF16, name="a_wide%d_%d_%d_%d" % (q, first, lo, row))
+                host = keep.tile([P, K_PASS * (hi - lo)], BF16, name="a_wide%d_%d_%d_%d" % (q, first, lo, tile0))
             wide = host[:, 0 : K_PASS * (hi - lo)]
-            flat = a_raw[q, first, row][:].rearrange("p j k -> p (j k)")
+            flat = a_raw[q, first, tile0][:].rearrange("p j k -> p (j k)")
             copy(out=wide, in_=flat[:, K_PASS * lo : K_PASS * hi].bitcast(E4M3))
             for seg in range(lo, hi):
                 j, g = divmod(seg, last - first)
-                a_wide[q, row + j, first + g] = wide[:, K_PASS * (seg - lo) : K_PASS * (seg - lo + 1)]
+                a_wide[q, tile0 + j, first + g] = wide[:, K_PASS * (seg - lo) : K_PASS * (seg - lo + 1)]
 
-        def widen_v(q, first, last, lo, hi, row=0):
-            widen(nc.vector.tensor_copy, q, first, last, lo, hi, row)
-
-        def widen_s(q, first, last, lo, hi, row=0):
-            widen(nc.scalar.copy, q, first, last, lo, hi, row)
-
-        def widen_g(q, lo, hi, host):
-            widen(nc.gpsimd.tensor_copy, q, 0, PASSES, lo, hi, 0, host)
-
-        def adj_turn(q, g, rows=(0, 1)):
-            bank = tp.tile([P, 2, P * len(rows)], F32, name="a_bank")
-            a_bank[q, g, rows[0]] = bank
-            for i, j in enumerate(rows):
+        def adj_turn(slab, tiles=(0, 1)):
+            q, g = divmod(slab, PASSES)
+            bank = slab_bank([P, 2, P * len(tiles)])
+            a_bank[slab, tiles[0]] = bank
+            for i, j in enumerate(tiles):
                 words = a_wide[q, j, g].bitcast(F32)
                 for u in range(2):
                     nc.tensor.transpose(bank[:, u, P * i : P * (i + 1)], words[:, u : 2 * P : 2], ident[:])
 
-        def adj_mult(q, g, rows=(0, 1)):
-            i = PASSES * q + g
-            lo = max(s for s in QUANT_STARTS if s <= i)
-            if i == lo and rows[0] == 0:
-                hi = min(s for s in QUANT_STARTS if s > i)
-                grouped = keep.tile([P, 4 * PAIR_ROWS * (hi - lo)], BF16, name="a_grp%d" % lo, align_bytes=64)
-                a_grp[lo] = grouped
-            first = 4 * (PAIR_ROWS * (i - lo) + P * rows[0])
-            part = a_grp[lo][:, first : first + 4 * P * len(rows)]
-            halves = a_bank[q, g, rows[0]][:].rearrange("p u r -> p (u r)").bitcast(BF16)
-            factor = scale_cols[:, g, :].rearrange("p (o u e) -> p o u e", o=1, u=2)
+        def adj_mult(slab, tiles=(0, 1)):
+            lo = max(s for s in QUANT_STARTS if s <= slab)
+            if lo not in a_grouped:
+                hi = min(s for s in QUANT_STARTS if s > slab)
+                a_grouped[lo] = keep.tile([P, 4 * PAIR_ROWS * (hi - lo)], BF16, name="a_grouped%d" % lo, align_bytes=64)
+            start = 4 * (PAIR_ROWS * (slab - lo) + P * tiles[0])
+            part = a_grouped[lo][:, start : start + 4 * P * len(tiles)]
+            values = a_bank[slab, tiles[0]][:].rearrange("p u r -> p (u r)").bitcast(BF16)
+            factor = scale_cols[:, slab % PASSES, :].rearrange("p (o u e) -> p o u e", o=1, u=2)
             nc.vector.tensor_tensor(
                 out=part.rearrange("p (r u e) -> p r u e", u=2, e=2),
-                in0=halves.rearrange("p (u r e) -> p r u e", u=2, e=2),
-                in1=factor.to_broadcast([P, P * len(rows), 2, 2]),
+                in0=values.rearrange("p (u r e) -> p r u e", u=2, e=2),
+                in1=factor.to_broadcast([P, P * len(tiles), 2, 2]),
                 op=ALU.mult,
             )
 
@@ -155,33 +134,33 @@ def tile_gcn_pa_w4_kernel(tc, x_init, adj_bytes, adj_scale, w_words, w_scales, b
             nc.vector.quantize_mx(
                 out=a_codes[:].rearrange("p q g r -> p (q g r)")[:, cols].bitcast(E4M3X4),
                 scales=a_plane[:].rearrange("p q g r -> p (q g r)")[:, cols],
-                in_=a_grp[lo][:],
+                in_=a_grouped[lo][:],
             )
+
 
         def x_turn(g, b):
             if b == 0:
-                grouped = keep.tile([P, 4 * K_PASS], BF16, name="x_grp%d" % g, align_bytes=64)
-                x_grp[g] = grouped
-            bank = sums.tile([P, 4, P], F32, name="bank")
+                x_grouped[g] = keep.tile([P, 4 * K_PASS], BF16, name="x_grouped%d" % g, align_bytes=64)
+            bank = other_bank([P, 4, P])
+            x_bank[g, b] = bank
             for a in range(2):
                 words = x_raw[g, b][:, a, :].bitcast(F32)
                 for u in range(2):
                     nc.tensor.transpose(bank[:, 2 * a + u, :], words[:, u : 2 * P : 2], ident[:])
-            banks["x", g, b] = bank
 
         def x_out(g, b):
-            bank = banks["x", g, b]
-            part = x_grp[g][:, 8 * P * b : 8 * P * (b + 1)]
+            part = x_grouped[g][:, 8 * P * b : 8 * P * (b + 1)]
             nc.scalar.copy(
                 out=part.bitcast(F32).rearrange("p (a m u) -> p a m u", a=2, u=2),
-                in_=bank[:].rearrange("p (a u) m -> p a m u", a=2),
+                in_=x_bank[g, b][:].rearrange("p (a u) m -> p a m u", a=2),
             )
 
         def x_quant(g):
-            nc.vector.quantize_mx(out=x_codes[:, g, :].bitcast(E4M3X4), scales=x_plane[:, g, :], in_=x_grp[g][:])
+            nc.vector.quantize_mx(out=x_codes[:, g, :].bitcast(E4M3X4), scales=x_plane[:, g, :], in_=x_grouped[g][:])
 
-        def stage1(g, c):
-            bank = sums.tile([P, 4, P], F32, name="bank")
+        def support_mm(g, c):
+            bank = other_bank([P, 4, P])
+            s_bank[g, c] = bank
             for t in range(4):
                 cols = slice(P * t, P * (t + 1))
                 nc.tensor.matmul_mx(
@@ -193,33 +172,28 @@ def tile_gcn_pa_w4_kernel(tc, x_init, adj_bytes, adj_scale, w_words, w_scales, b
                     start=True,
                     stop=True,
                 )
-            banks["s", g, c] = bank
 
-        def s_out(g, c):
-            bank = banks["s", g, c]
+        def support_out(g, c):
             nc.scalar.copy(
-                out=s_grp[g][:, 4 * P * c : 4 * P * (c + 1)].rearrange("p (n t) -> p n t", t=4),
-                in_=bank[:].rearrange("p t n -> p n t"),
+                out=s_grouped[g][:, 4 * P * c : 4 * P * (c + 1)].rearrange("p (n t) -> p n t", t=4),
+                in_=s_bank[g, c][:].rearrange("p t n -> p n t"),
             )
 
-        def s_quant(first, last, source):
-            nc.vector.quantize_mx(
-                out=s_codes[:, first:last, :].rearrange("p g h -> p (g h)").bitcast(E4M3X4),
-                scales=s_plane[:, first:last, :].rearrange("p g h -> p (g h)"),
-                in_=source[:],
-            )
+        def support_quant(g):
+            nc.vector.quantize_mx(out=s_codes[:, g, :].bitcast(E4M3X4), scales=s_plane[:, g, :], in_=s_grouped[g][:])
 
-        def out_rows(q):
-            return out[PAIR_ROWS * q : PAIR_ROWS * (q + 1), :].rearrange("(m j) h -> m j h", j=2)
 
-        def stage2(q, j, first=0, last=PASSES):
+        def store(q, j, res, cols=slice(0, HID)):
+            rows = out[PAIR_ROWS * q : PAIR_ROWS * (q + 1), :].rearrange("(m j) h -> m j h", j=2)
+            nc.sync.dma_start(out=rows[:, j, cols], in_=res)
+
+        def out_mm(q, j, first=0, last=PASSES):
             if first == 0:
-                total = sums.tile([P, HID], F32, name="bank")
-                acc[q, j] = total
+                total[q, j] = other_bank([P, HID])
+            cols = slice(P * j, P * (j + 1))
             for g in range(first, last):
-                cols = slice(P * j, P * (j + 1))
                 nc.tensor.matmul_mx(
-                    out=acc[q, j][:],
+                    out=total[q, j][:],
                     lhsT=a_codes[:, q, g, cols].bitcast(E4M3X4),
                     lhsT_scale=a_plane[:, q, g, cols],
                     rhs=s_codes[:, g, :].bitcast(E4M3X4),
@@ -228,42 +202,51 @@ def tile_gcn_pa_w4_kernel(tc, x_init, adj_bytes, adj_scale, w_words, w_scales, b
                     stop=(g == PASSES - 1),
                 )
 
-        def add_bias(q, j, c=0, pieces=1):
-            cols = slice(HID // pieces * c, HID // pieces * (c + 1))
-            part = keep.tile([P, HID // pieces], F32, name="res%d_%d_%d" % (q, j, c))
-            result[q, j, c] = part
-            nc.vector.tensor_tensor(out=part[:], in0=acc[q, j][:, cols], in1=bias[:, cols], op=ALU.add)
+        def vector_bias(q, j):
+            res = keep.tile([P, HID], F32, name="res%d_%d" % (q, j))
+            nc.vector.tensor_tensor(out=res[:], in0=total[q, j][:], in1=bias[:], op=ALU.add)
+            return res
 
-        def relu_store(q, j, c=0, pieces=1):
-            cols = slice(HID // pieces * c, HID // pieces * (c + 1))
-            part = result[q, j, c]
-            nc.scalar.activation(out=part[:], in_=part[:], func=ACT.Relu)
-            nc.sync.dma_start(out=out_rows(q)[:, j, cols], in_=part[:])
+        def relu_store(q, j, res):
+            nc.scalar.activation(out=res, in_=res, func=ACT.Relu)
+            store(q, j, res)
 
-        def finish_shared(q, j):
-            add_bias(q, j)
-            res = result[q, j, 0]
+        def vector_finish(q, j):
+            relu_store(q, j, vector_bias(q, j)[:])
+
+        def last_finish(q, j):
+            res = vector_bias(q, j)
             left, right = slice(0, HID // 2), slice(HID // 2, HID)
             nc.scalar.activation(out=res[:, left], in_=res[:, left], func=ACT.Relu)
             nc.vector.tensor_scalar(out=res[:, right], in0=res[:, right], scalar1=0.0, scalar2=None, op0=ALU.max)
             for cols in (right, left):
-                nc.sync.dma_start(out=out_rows(q)[:, j, cols], in_=res[:, cols])
+                store(q, j, res[:, cols], cols)
 
-        def finish(q, j, c=0, pieces=1):
-            add_bias(q, j, c, pieces)
-            relu_store(q, j, c, pieces)
+        def park(q):
+            parked[q] = keep.tile([P, 2, HID], F32, name="parked%d" % q)
+            for j in range(2):
+                nc.scalar.copy(out=parked[q][:, j, :], in_=total[q, j][:])
 
-        def stage2_flipped(q, h):
+        def pool_bias(q, host):
+            pool_sum[q] = host[:, 0 : 4 * HID].bitcast(F32).rearrange("p (j h) -> p j h", j=2)
+            spread = bias[:].rearrange("p (o h) -> p o h", o=1).to_broadcast([P, 2, HID])
+            nc.gpsimd.tensor_tensor(out=pool_sum[q], in0=parked[q][:], in1=spread, op=ALU.add)
+
+        def pool_finish(q):
+            for j in range(2):
+                relu_store(q, j, pool_sum[q][:, j, :])
+
+
+        def flip_mm(q, h):
             if h == 0:
-                flat = keep.tile([P, 4, PAIR_ROWS], F32, name="flat%d" % q)
-                flip[q] = flat
-            total = sums.tile([P, HID], F32, name="bank")
-            halves = [total[:, PAIR_ROWS * i : PAIR_ROWS * (i + 1)] for i in range(2)]
+                flip_flat[q] = keep.tile([P, CHUNKS, PAIR_ROWS], F32, name="flip_flat%d" % q)
+            bank = other_bank([P, 2, PAIR_ROWS])
+            flip_total[q, h] = bank
             for i in range(2):
                 cols = slice(P * (2 * h + i), P * (2 * h + i + 1))
                 for g in range(PASSES):
                     nc.tensor.matmul_mx(
-                        out=halves[i],
+                        out=bank[:, i, :],
                         lhsT=s_codes[:, g, cols].bitcast(E4M3X4),
                         lhsT_scale=s_plane[:, g, cols],
                         rhs=a_codes[:, q, g, :].bitcast(E4M3X4),
@@ -271,211 +254,180 @@ def tile_gcn_pa_w4_kernel(tc, x_init, adj_bytes, adj_scale, w_words, w_scales, b
                         start=(g == 0),
                         stop=(g == PASSES - 1),
                     )
-            banks["f", q, h] = halves
 
         def flip_relu(q, h):
             for i in range(2):
                 c = 2 * h + i
                 nc.scalar.activation(
-                    out=flip[q][:, c, :], in_=banks["f", q, h][i], func=ACT.Relu, bias=bias_col[:, c : c + 1]
+                    out=flip_flat[q][:, c, :], in_=flip_total[q, h][:, i, :], func=ACT.Relu, bias=bias_col[:, c : c + 1]
                 )
 
-        def flip_back(q, j, pool, tag):
-            bank = pool.tile([P, 4, P], F32, name=tag)
-            for c in range(4):
-                nc.tensor.transpose(bank[:, c, :], flip[q][:, c, P * j : P * (j + 1)], ident[:])
-            banks["b", q, j] = bank
-
-        def flip_out(q, j):
-            bank = banks["b", q, j]
-            res = keep.tile([P, HID], F32, name="res%d_%d" % (q, j))
-            nc.scalar.copy(out=res[:], in_=bank[:].rearrange("p c m -> p (c m)"))
-            nc.sync.dma_start(out=out_rows(q)[:, j, :], in_=res[:])
-
-        def turn(i):
-            adj_turn(*divmod(i, PASSES))
-
-        def mult(i):
-            adj_mult(*divmod(i, PASSES))
-
-        def widen_pair(q):
-            widen_s(q, 0, PASSES, 0, 2 * PASSES)
-
-        def park(q, j):
-            if j == 0:
-                parked = keep.tile([P, 2, HID], F32, name="parked%d" % q)
-                flip[q] = parked
-            nc.scalar.copy(out=flip[q][:, j, :], in_=acc[q, j][:])
-
-        def pool_bias(q, host, half):
-            res = a_grp[host][:, 4 * HID * half : 4 * HID * (half + 1)].bitcast(F32).rearrange("p (j h) -> p j h", j=2)
-            result[q] = res
-            spread = bias[:].rearrange("p (o h) -> p o h", o=1).to_broadcast([P, 2, HID])
-            nc.gpsimd.tensor_tensor(out=res, in0=flip[q][:], in1=spread, op=ALU.add)
-
-        def pool_store(q, j):
-            part = result[q][:, j, :]
-            nc.scalar.activation(out=part, in_=part, func=ACT.Relu)
-            nc.sync.dma_start(out=out_rows(q)[:, j, :], in_=part)
-
-        def widen_pass(q, g):
+        def flip_back(q, new_bank):
             for j in range(2):
-                widen_s(q, 0, PASSES, PASSES * j + g, PASSES * j + g + 1)
+                bank = new_bank([P, CHUNKS, P])
+                back_bank[q, j] = bank
+                for c in range(CHUNKS):
+                    nc.tensor.transpose(bank[:, c, :], flip_flat[q][:, c, P * j : P * (j + 1)], ident[:])
+
+        def flip_finish(q):
+            for j in range(2):
+                res = keep.tile([P, HID], F32, name="res%d_%d" % (q, j))
+                nc.scalar.copy(out=res[:], in_=back_bank[q, j][:].rearrange("p c m -> p (c m)"))
+                store(q, j, res[:])
+
+        def turn_bias():
+            bias_bank[0] = other_bank([P, 4, P])
+            nc.tensor.transpose(bias_bank[0][:, 0, :], bias_rows_f32[:], ident[:])
+
+        on_vector, on_scalar, on_pool = nc.vector.tensor_copy, nc.scalar.copy, nc.gpsimd.tensor_copy
 
         with tc.manual_schedule():
             make_identity(nc, ident[:])
             nc.gpsimd.memset(w_plane[:].bitcast(I32), 0)
             nc.gpsimd.memset(bias_rows[:], 0.0)
+
             load_adj(0, 0, 1, (0,))
             load_scale()
             load_adj(0, 0, 1, (1,))
-            load_adj(0, 1, 3)
-            load_x(0, 0)
+            load_adj(0, 1, PASSES)
+            load_x(0, (0,))
             load_adj(1)
-            load_x(0, 1)
-            load_bias_rows()
-            load_x_whole(1)
-            load_w_codes()
-            load_w_plane()
+            load_x(0, (1,))
+            nc.sync.dma_start(out=bias_rows[0:CHUNKS, :], in_=b1.rearrange("(c m) -> c m", m=P))
+            load_x(1, (0, 1))
+            load_w()
             load_adj(2)
-            load_x_whole(2)
+            load_x(2, (0, 1))
             for q in range(3, PAIRS):
                 load_adj(q)
-            load_bias()
+            nc.sync.dma_start(out=bias[:], in_=b1.partition_broadcast(P))
 
-            widen_v(0, 0, 1, 0, 1, 0)
-            widen_v(0, 0, 1, 0, 1, 1)
-            for seg in (0, 2, 1, 3):
-                widen_s(0, 1, 3, seg, seg + 1)
-            adj_turn(0, 0, (0,))
-            adj_turn(0, 0, (1,))
-            adj_mult(0, 0, (0,))
-            adj_mult(0, 0, (1,))
-            turn(1)
-            turn(2)
+            for j in range(2):
+                widen(on_vector, 0, 0, 1, 0, 1, j)
+            for g in range(2):
+                for j in range(2):
+                    widen(on_scalar, 0, 2 * j + g, 2 * j + g + 1, 1, PASSES)
+            for j in range(2):
+                adj_turn(0, (j,))
+            for j in range(2):
+                adj_mult(0, (j,))
+            adj_turn(1)
+            adj_turn(2)
             x_turn(0, 0)
-            widen_s(1, 0, 3, 0, 4)
-            widen_g(1, 4, 6, None)
+            widen(on_scalar, 1, 0, 4)
+            widen(on_pool, 1, 4, SEGMENTS)
             x_turn(0, 1)
-            turn(3)
-            x_out(0, 0)
-            x_out(0, 1)
-            cast_bias()
-            for i in range(1, 4):
-                mult(i)
-            x_turn(1, 0)
-            x_turn(1, 1)
-            turn(4)
-            turn(5)
-            x_out(1, 0)
-            x_out(1, 1)
-            widen_pair(2)
+            adj_turn(3)
+            for b in range(2):
+                x_out(0, b)
+            nc.scalar.copy(out=bias_rows_f32[:], in_=bias_rows[:])
+            for slab in range(1, 4):
+                adj_mult(slab)
+            for b in range(2):
+                x_turn(1, b)
+            adj_turn(4)
+            adj_turn(5)
+            for b in range(2):
+                x_out(1, b)
+            turn_bias()
+            widen(on_scalar, 2, 0, SEGMENTS)
+            nc.scalar.copy(out=bias_col[:], in_=bias_bank[0][:, 0, 0:CHUNKS])
             x_quant(0)
             x_quant(1)
             adj_quant(0)
-            widen_g(3, 3, 6, a_grp[0])
-            mult(4)
-            for c in range(4):
-                stage1(0, c)
-            for c in range(4):
-                s_out(0, c)
-            turn(6)
-            x_turn(2, 0)
-            x_turn(2, 1)
-            turn(7)
-            stage1(1, 0)
-            stage1(1, 1)
-            x_out(2, 0)
-            x_out(2, 1)
-            mult(5)
-            mult(6)
-            x_quant(2)
-            adj_quant(4)
-            stage1(1, 2)
-            stage1(1, 3)
-            for c in range(4):
-                s_out(1, c)
-            turn(8)
-            for c in range(4):
-                stage1(2, c)
-            widen_s(3, 0, 3, 0, 1)
-            for c in range(4):
-                s_out(2, c)
-            turn(9)
-            turn_bias()
-            mult(7)
-            s_quant(0, 2, s_early)
-            stage2(0, 0, 0, 2)
-            stage2(0, 1, 0, 2)
-            widen_s(3, 0, 3, 1, 3)
-            turn(10)
-            widen_pair(4)
-            mult(8)
-            s_quant(2, 3, s_late)
+            widen(on_pool, 3, PASSES, SEGMENTS, host=a_grouped[0])
+            adj_mult(4)
 
-            stage2(0, 0, 2, 3)
-            stage2(0, 1, 2, 3)
-            turn(11)
-            mult(9)
+            for c in range(CHUNKS):
+                support_mm(0, c)
+            for c in range(CHUNKS):
+                support_out(0, c)
+            adj_turn(6)
+            x_turn(2, 0)
+            support_mm(1, 0)
+            support_mm(1, 1)
+            x_turn(2, 1)
+            adj_turn(7)
+            x_out(2, 0)
+            support_out(1, 0)
+            x_out(2, 1)
+            support_mm(1, 2)
+            support_mm(1, 3)
+            support_out(1, 1)
+            widen(on_scalar, 3, 0, 1)
+            support_out(1, 2)
+            support_out(1, 3)
+            widen(on_scalar, 3, 1, PASSES)
+            adj_mult(5)
+            adj_mult(6)
+            adj_quant(4)
+            support_quant(0)
+            x_quant(2)
+            adj_turn(8)
+            adj_turn(9)
+            adj_mult(7)
+            for c in range(CHUNKS):
+                support_mm(2, c)
+            for c in range(CHUNKS):
+                support_out(2, c)
+            adj_turn(10)
+            adj_turn(11)
+            adj_mult(8)
+            support_quant(1)
+            for j in range(2):
+                out_mm(0, j, 0, 2)
+            widen(on_scalar, 4, 0, SEGMENTS)
+            adj_mult(9)
+            support_quant(2)
             adj_quant(6)
-            turn(12)
-            park(0, 0)
-            park(0, 1)
-            pool_bias(0, 6, 0)
-            stage2(1, 0)
-            stage2(1, 1)
-            park(1, 0)
-            park(1, 1)
-            pool_bias(1, 6, 1)
-            widen_pair(5)
-            mult(10)
-            turn(13)
-            turn(14)
-            stage2_flipped(2, 0)
-            stage2_flipped(2, 1)
-            flip_relu(2, 0)
-            flip_relu(2, 1)
-            pool_store(0, 0)
-            pool_store(0, 1)
-            mult(11)
-            mult(12)
-            turn(15)
-            turn(16)
-            flip_back(2, 0, sums, "bank")
-            flip_back(2, 1, sums, "bank")
-            flip_out(2, 0)
-            flip_out(2, 1)
-            pool_store(1, 0)
-            pool_store(1, 1)
-            mult(13)
-            turn(17)
-            mult(14)
+
+            for j in range(2):
+                out_mm(0, j, 2, PASSES)
+            for j in range(2):
+                out_mm(1, j)
+            adj_turn(12)
+            adj_turn(13)
+            park(0)
+            pool_bias(0, a_grouped[6])
+            park(1)
+            widen(on_scalar, 5, 0, SEGMENTS)
+            for h in range(2):
+                flip_mm(2, h)
+            for slab in range(10, 13):
+                adj_mult(slab)
             adj_quant(10)
-            stage2_flipped(3, 0)
-            stage2_flipped(3, 1)
-            stage2(4, 0, 0, 2)
-            stage2(4, 1, 0, 2)
+            pool_bias(1, a_grouped[10])
+
+            adj_turn(14)
+            adj_turn(15)
+            for h in range(2):
+                flip_relu(2, h)
+            flip_mm(3, 0)
+            pool_finish(0)
+            adj_mult(13)
+            adj_turn(16)
+            flip_back(2, other_bank)
+            flip_mm(3, 1)
             flip_relu(3, 0)
+            flip_finish(2)
             flip_relu(3, 1)
-            mult(15)
-            flip_back(3, 0, tp, "a_bank")
-            flip_back(3, 1, tp, "a_bank")
-            flip_out(3, 0)
-            flip_out(3, 1)
-            mult(16)
-            adj_quant(14)
-            stage2(4, 0, 2, 3)
-            stage2(4, 1, 2, 3)
-            stage2(5, 0, 0, 1)
-            stage2(5, 1, 0, 1)
-            mult(17)
+            adj_mult(14)
+            adj_turn(17)
+            adj_mult(15)
+            flip_back(3, slab_bank)
+            pool_finish(1)
+            flip_finish(3)
+
+            adj_mult(16)
+            adj_quant(12)
+            for j in range(2):
+                out_mm(4, j)
+            adj_mult(17)
             adj_quant(16)
-            stage2(5, 0, 1, 2)
-            stage2(5, 1, 1, 2)
-            finish(4, 0)
+            vector_finish(4, 0)
             adj_quant(17)
-            stage2(5, 0, 2, 3)
-            stage2(5, 1, 2, 3)
-            finish(4, 1)
-            finish(5, 0)
-            finish_shared(5, 1)
+            for j in range(2):
+                out_mm(5, j)
+            vector_finish(4, 1)
+            vector_finish(5, 0)
+            last_finish(5, 1)

@@ -333,9 +333,9 @@ def tile_gcn_pa_w4_kernel(tc, x_init, adj_bytes, adj_scale, w_words, w_scales, b
             widen(on_scalar, 2, 0, SEGMENTS)
             nc.scalar.copy(out=bias_col[:], in_=bias_bank[0][:, 0, 0:CHUNKS])
             x_quant(0)
-            x_quant(1)
             adj_quant(0)
-            widen(on_pool, 3, PASSES, SEGMENTS, host=a_grouped[0])
+            x_quant(1)
+            widen(on_pool, 3, PASSES, SEGMENTS, host=x_grouped[1])
             adj_mult(4)
 
             for c in range(CHUNKS):
@@ -353,32 +353,33 @@ def tile_gcn_pa_w4_kernel(tc, x_init, adj_bytes, adj_scale, w_words, w_scales, b
             x_out(2, 1)
             support_mm(1, 2)
             support_mm(1, 3)
-            support_out(1, 1)
-            widen(on_scalar, 3, 0, 1)
-            support_out(1, 2)
-            support_out(1, 3)
-            widen(on_scalar, 3, 1, PASSES)
+            for c in range(1, CHUNKS):
+                support_out(1, c)
+            widen(on_scalar, 3, 0, 2)
             adj_mult(5)
             adj_mult(6)
             adj_quant(4)
             support_quant(0)
             x_quant(2)
+            widen(on_pool, 4, 4, SEGMENTS, host=x_grouped[2])
             adj_turn(8)
-            adj_turn(9)
             adj_mult(7)
             for c in range(CHUNKS):
                 support_mm(2, c)
             for c in range(CHUNKS):
                 support_out(2, c)
+            widen(on_scalar, 3, 2, PASSES)
+            adj_turn(9)
             adj_turn(10)
-            adj_turn(11)
             adj_mult(8)
             support_quant(1)
             for j in range(2):
                 out_mm(0, j, 0, 2)
-            widen(on_scalar, 4, 0, SEGMENTS)
+            adj_turn(11)
+            widen(on_scalar, 4, 0, 4)
             adj_mult(9)
             support_quant(2)
+            adj_mult(10)
             adj_quant(6)
 
             for j in range(2):
@@ -393,7 +394,7 @@ def tile_gcn_pa_w4_kernel(tc, x_init, adj_bytes, adj_scale, w_words, w_scales, b
             widen(on_scalar, 5, 0, SEGMENTS)
             for h in range(2):
                 flip_mm(2, h)
-            for slab in range(10, 13):
+            for slab in range(11, 14):
                 adj_mult(slab)
             adj_quant(10)
             pool_bias(1, a_grouped[10])
@@ -404,7 +405,6 @@ def tile_gcn_pa_w4_kernel(tc, x_init, adj_bytes, adj_scale, w_words, w_scales, b
                 flip_relu(2, h)
             flip_mm(3, 0)
             pool_finish(0)
-            adj_mult(13)
             adj_turn(16)
             flip_back(2, other_bank)
             flip_mm(3, 1)

@@ -23,11 +23,12 @@ PAIR_ROWS = 2 * P
 PAIRS = NODES // PAIR_ROWS
 SEGMENTS = 2 * PASSES
 CHUNKS = HID // P
-
-QUANT_STARTS = (0, 4, 6, 10, 12, 16, 17, 18)
-
+HALF = HID // 2
 SLAB_BANKS = 4
-OTHER_BANKS = 4
+OTHER_BANKS = 8 - SLAB_BANKS
+QUANT_CALLS = ((0, 1, 2, 3), (4, 5, 6, 7), (9, 8, 10, 11), (12, 13), (14,), (15, 16), (17,))
+POOL_ADDS = (((0, 0), (1, 0)),)
+STRIP_STARTS = {4: 0, 9: 3072, 12: 0, 15: 1024}
 
 FLOPS = 2 * NODES * FEAT * HID + 2 * NODES * NODES * HID
 
@@ -36,43 +37,48 @@ def tile_gcn_pa_w4_kernel(tc, x_init, adj_bytes, adj_scale, w_words, w_scales, b
     nc = tc.nc
     with ExitStack() as ctx:
         keep = ctx.enter_context(tc.tile_pool(name="keep", bufs=1))
-        slab_psum = ctx.enter_context(tc.psum_pool(name="slab_psum", bufs=SLAB_BANKS))
-        other_psum = ctx.enter_context(tc.psum_pool(name="other_psum", bufs=OTHER_BANKS))
+        psum = ctx.enter_context(tc.psum_pool(name="psum", bufs=1))
 
         ident = keep.tile([P, P], F32, name="ident")
         scale_cols = keep.tile([P, PASSES, 4], F32, name="scale_cols")
         bias = keep.tile([P, HID], BF16, name="bias")
+        w_codes = keep.tile([P, 2 * HID], U8, name="w_codes", align_bytes=64)
+        w_plane = keep.tile([P, HID], U8, name="w_plane", align_bytes=64)
+        x_codes = keep.tile([P, PASSES * K_PASS], U32, name="x_codes", align_bytes=64)
+        x_plane = keep.tile([P, PASSES * K_PASS], U8, name="x_plane", align_bytes=64)
+        s_codes = keep.tile([P, PASSES * HID], U32, name="s_codes", align_bytes=64)
+        s_plane = keep.tile([P, PASSES * HID], U8, name="s_plane", align_bytes=64)
+        a_codes = keep.tile([P, PAIRS * PASSES * PAIR_ROWS], U32, name="a_codes", align_bytes=64)
+        a_plane = keep.tile([P, PAIRS * PASSES * PAIR_ROWS], U8, name="a_plane", align_bytes=64)
+        x_grouped = keep.tile([P, 6144], BF16, name="x_grouped", align_bytes=64)
+        s_grouped = keep.tile([P, PASSES * 4 * HID], BF16, name="s_grouped", align_bytes=64)
+        strip = keep.tile([P, 8192], BF16, name="strip", align_bytes=64)
         bias_rows = keep.tile([P, P], BF16, name="bias_rows")
         bias_rows_f32 = keep.tile([P, P], F32, name="bias_rows_f32")
         bias_col = keep.tile([P, CHUNKS], F32, name="bias_col")
-        w_codes = keep.tile([P, 2 * HID], U8, name="w_codes", align_bytes=64)
-        w_plane = keep.tile([P, HID], U8, name="w_plane", align_bytes=64)
-        x_codes = keep.tile([P, PASSES, K_PASS], U32, name="x_codes", align_bytes=64)
-        x_plane = keep.tile([P, PASSES, K_PASS], U8, name="x_plane", align_bytes=64)
-        s_codes = keep.tile([P, PASSES, HID], U32, name="s_codes", align_bytes=64)
-        s_plane = keep.tile([P, PASSES, HID], U8, name="s_plane", align_bytes=64)
-        a_codes = keep.tile([P, PAIRS, PASSES, PAIR_ROWS], U32, name="a_codes", align_bytes=64)
-        a_plane = keep.tile([P, PAIRS, PASSES, PAIR_ROWS], U8, name="a_plane", align_bytes=64)
-        s_grouped = [keep.tile([P, 4 * HID], BF16, name="s_grouped%d" % g, align_bytes=64) for g in range(PASSES)]
-
-        a_raw, a_wide, a_bank, a_grouped = {}, {}, {}, {}
-        x_raw, x_bank, x_grouped, s_bank = {}, {}, {}, {}
-        total, parked, pool_sum = {}, {}, {}
+        a_raw, a_wide, a_bank, a_grouped, a_staged = {}, {}, {}, {}, {}
+        x_raw, x_bank, s_bank = {}, {}, {}
+        total, parked, res, pool_sum = {}, {}, {}, {}
         flip_total, flip_flat, back_bank, bias_bank = {}, {}, {}, {}
+        slab_uses, other_uses = [], []
 
         def slab_bank(shape):
-            return slab_psum.tile(shape, F32, name="slab_bank")
+            slab_uses.append(shape)
+            return psum.tile(shape, F32, name="slab_bank%d" % ((len(slab_uses) - 1) % SLAB_BANKS))
 
         def other_bank(shape):
-            return other_psum.tile(shape, F32, name="other_bank")
-
+            other_uses.append(shape)
+            return psum.tile(shape, F32, name="other_bank%d" % ((len(other_uses) - 1) % OTHER_BANKS))
 
         def load_scale():
             nc.sync.dma_start(out=scale_cols[:], in_=adj_scale.rearrange("o (g p t) -> p (o g) t", p=P, t=4))
 
         def load_adj(q, first=0, last=PASSES, tiles=(0, 1)):
             raw = keep.tile([P, len(tiles), K_PASS * (last - first)], U8, name="a_raw%d_%d_%d" % (q, first, tiles[0]))
-            a_raw[q, first, tiles[0]] = raw
+            flat = raw[:].rearrange("p j k -> p (j k)")
+            for i, j in enumerate(tiles):
+                for g in range(first, last):
+                    a_raw[q, j, g] = (flat, (last - first) * i + g - first)
             block = adj_bytes[PAIR_ROWS * q : PAIR_ROWS * (q + 1), K_PASS * first : K_PASS * last]
             by_tile = block.rearrange("(m j) k -> m j k", j=2)
             nc.sync.dma_start(out=raw[:], in_=by_tile[:, tiles[0] : tiles[-1] + 1, :])
@@ -84,24 +90,34 @@ def tile_gcn_pa_w4_kernel(tc, x_init, adj_bytes, adj_scale, w_words, w_scales, b
             by_t = x_init[K_PASS * g : K_PASS * (g + 1), :].rearrange("(m t) f -> m t f", t=4)
             nc.sync.dma_start(out=raw[:], in_=by_t[:, 2 * halves[0] : 2 * halves[-1] + 2, :])
 
-        def load_w():
+        def load_w_codes():
             nc.sync.dma_start(out=w_codes[:].bitcast(I32), in_=w_words[0].bitcast(I32))
+
+        def load_w_scales():
             for quad in range(4):
                 nc.sync.dma_start(
                     out=w_plane[32 * quad : 32 * quad + 4, :].bitcast(I32),
                     in_=w_scales[0, 4 * quad : 4 * quad + 4, :].bitcast(I32),
                 )
 
+        def load_bias():
+            nc.sync.dma_start(out=bias[:], in_=b1.partition_broadcast(P))
 
-        def widen(copy, q, lo, hi, first=0, last=PASSES, tile0=0, host=None):
+        def x_part(g):
+            return x_grouped[:, 4 * K_PASS * g : 4 * K_PASS * (g + 1)]
+
+        def s_part(first, last):
+            return s_grouped[:, 4 * HALF * first : 4 * HALF * last]
+
+        def widen(copy, segs, host=None):
+            flat, lo = a_raw[segs[0]]
+            n = len(segs)
             if host is None:
-                host = keep.tile([P, K_PASS * (hi - lo)], BF16, name="a_wide%d_%d_%d_%d" % (q, first, lo, tile0))
-            wide = host[:, 0 : K_PASS * (hi - lo)]
-            flat = a_raw[q, first, tile0][:].rearrange("p j k -> p (j k)")
-            copy(out=wide, in_=flat[:, K_PASS * lo : K_PASS * hi].bitcast(E4M3))
-            for seg in range(lo, hi):
-                j, g = divmod(seg, last - first)
-                a_wide[q, tile0 + j, first + g] = wide[:, K_PASS * (seg - lo) : K_PASS * (seg - lo + 1)]
+                host = keep.tile([P, K_PASS * n], BF16, name="a_wide%d_%d_%d" % segs[0])
+            wide = host[:, 0 : K_PASS * n]
+            copy(out=wide, in_=flat[:, K_PASS * lo : K_PASS * (lo + n)].bitcast(E4M3))
+            for i, seg in enumerate(segs):
+                a_wide[seg] = wide[:, K_PASS * i : K_PASS * (i + 1)]
 
         def adj_turn(slab, tiles=(0, 1)):
             q, g = divmod(slab, PASSES)
@@ -112,13 +128,22 @@ def tile_gcn_pa_w4_kernel(tc, x_init, adj_bytes, adj_scale, w_words, w_scales, b
                 for u in range(2):
                     nc.tensor.transpose(bank[:, u, P * i : P * (i + 1)], words[:, u : 2 * P : 2], ident[:])
 
-        def adj_mult(slab, tiles=(0, 1)):
-            lo = max(s for s in QUANT_STARTS if s <= slab)
-            if lo not in a_grouped:
-                hi = min(s for s in QUANT_STARTS if s > slab)
-                a_grouped[lo] = keep.tile([P, 4 * PAIR_ROWS * (hi - lo)], BF16, name="a_grouped%d" % lo, align_bytes=64)
-            start = 4 * (PAIR_ROWS * (slab - lo) + P * tiles[0])
-            part = a_grouped[lo][:, start : start + 4 * P * len(tiles)]
+        def grouped_part(slab, tiles, host=None):
+            call = [c for c in QUANT_CALLS if slab in c][0]
+            if call[0] not in a_grouped:
+                if call[0] in STRIP_STARTS:
+                    host = strip[:, STRIP_STARTS[call[0]] :]
+                if host is None:
+                    host = keep.tile([P, 4 * PAIR_ROWS * len(call)], BF16, name="a_grouped%d" % call[0], align_bytes=64)
+                a_grouped[call[0]] = host[:, 0 : 4 * PAIR_ROWS * len(call)]
+            start = 4 * (PAIR_ROWS * call.index(slab) + P * tiles[0])
+            return a_grouped[call[0]][:, start : start + 4 * P * len(tiles)]
+
+        def code_start(slab):
+            return PAIR_ROWS * [s for c in QUANT_CALLS for s in c].index(slab)
+
+        def adj_mult(slab, tiles=(0, 1), host=None):
+            part = grouped_part(slab, tiles, host)
             values = a_bank[slab, tiles[0]][:].rearrange("p u r -> p (u r)").bitcast(BF16)
             factor = scale_cols[:, slab % PASSES, :].rearrange("p (o u e) -> p o u e", o=1, u=2)
             nc.vector.tensor_tensor(
@@ -128,19 +153,30 @@ def tile_gcn_pa_w4_kernel(tc, x_init, adj_bytes, adj_scale, w_words, w_scales, b
                 op=ALU.mult,
             )
 
-        def adj_quant(lo):
-            hi = min(s for s in QUANT_STARTS if s > lo)
-            cols = slice(PAIR_ROWS * lo, PAIR_ROWS * hi)
-            nc.vector.quantize_mx(
-                out=a_codes[:].rearrange("p q g r -> p (q g r)")[:, cols].bitcast(E4M3X4),
-                scales=a_plane[:].rearrange("p q g r -> p (q g r)")[:, cols],
-                in_=a_grouped[lo][:],
+        def adj_out(slab):
+            staged = keep.tile([P, 4 * PAIR_ROWS], BF16, name="a_staged%d" % slab)
+            a_staged[slab] = staged
+            nc.scalar.copy(
+                out=staged[:].bitcast(F32).rearrange("p (r u) -> p r u", u=2),
+                in_=a_bank[slab, 0][:].rearrange("p u r -> p r u"),
             )
 
+        def pool_mult(slab, host):
+            part = grouped_part(slab, (0, 1), host)
+            factor = scale_cols[:, slab % PASSES, :].rearrange("p (o t) -> p o t", o=1)
+            nc.gpsimd.tensor_tensor(
+                out=part.rearrange("p (r t) -> p r t", t=4),
+                in0=a_staged[slab][:].rearrange("p (r t) -> p r t", t=4),
+                in1=factor.to_broadcast([P, PAIR_ROWS, 4]),
+                op=ALU.mult,
+            )
+
+        def adj_quant(lo):
+            call = [c for c in QUANT_CALLS if c[0] == lo][0]
+            cols = slice(code_start(lo), code_start(lo) + PAIR_ROWS * len(call))
+            nc.vector.quantize_mx(out=a_codes[:, cols].bitcast(E4M3X4), scales=a_plane[:, cols], in_=a_grouped[lo])
 
         def x_turn(g, b):
-            if b == 0:
-                x_grouped[g] = keep.tile([P, 4 * K_PASS], BF16, name="x_grouped%d" % g, align_bytes=64)
             bank = other_bank([P, 4, P])
             x_bank[g, b] = bank
             for a in range(2):
@@ -148,109 +184,148 @@ def tile_gcn_pa_w4_kernel(tc, x_init, adj_bytes, adj_scale, w_words, w_scales, b
                 for u in range(2):
                     nc.tensor.transpose(bank[:, 2 * a + u, :], words[:, u : 2 * P : 2], ident[:])
 
-        def x_out(g, b):
-            part = x_grouped[g][:, 8 * P * b : 8 * P * (b + 1)]
-            nc.scalar.copy(
+        def x_out(g, b, copy=nc.scalar.copy):
+            part = x_part(g)[:, 8 * P * b : 8 * P * (b + 1)]
+            copy(
                 out=part.bitcast(F32).rearrange("p (a m u) -> p a m u", a=2, u=2),
                 in_=x_bank[g, b][:].rearrange("p (a u) m -> p a m u", a=2),
             )
 
-        def x_quant(g):
-            nc.vector.quantize_mx(out=x_codes[:, g, :].bitcast(E4M3X4), scales=x_plane[:, g, :], in_=x_grouped[g][:])
+        def x_quant(first, last):
+            cols = slice(K_PASS * first, K_PASS * last)
+            nc.vector.quantize_mx(
+                out=x_codes[:, cols].bitcast(E4M3X4),
+                scales=x_plane[:, cols],
+                in_=x_grouped[:, 4 * K_PASS * first : 4 * K_PASS * last],
+            )
 
         def support_mm(g, c):
             bank = other_bank([P, 4, P])
             s_bank[g, c] = bank
             for t in range(4):
-                cols = slice(P * t, P * (t + 1))
+                cols = slice(K_PASS * g + P * t, K_PASS * g + P * (t + 1))
                 nc.tensor.matmul_mx(
                     out=bank[:, t, :],
-                    lhsT=x_codes[:, g, cols].bitcast(E4M3X4),
-                    lhsT_scale=x_plane[:, g, cols],
+                    lhsT=x_codes[:, cols].bitcast(E4M3X4),
+                    lhsT_scale=x_plane[:, cols],
                     rhs=w_codes[:, 2 * P * c : 2 * P * (c + 1)].bitcast(E2M1X4),
                     rhs_scale=w_plane[:, P * c : P * (c + 1)],
                     start=True,
                     stop=True,
                 )
 
-        def support_out(g, c):
-            nc.scalar.copy(
-                out=s_grouped[g][:, 4 * P * c : 4 * P * (c + 1)].rearrange("p (n t) -> p n t", t=4),
+        def support_out(g, c, copy=nc.scalar.copy):
+            h, i = divmod(c, 2)
+            part = s_part(PASSES * h + g, PASSES * h + g + 1)
+            copy(
+                out=part[:, 4 * P * i : 4 * P * (i + 1)].rearrange("p (n t) -> p n t", t=4),
                 in_=s_bank[g, c][:].rearrange("p t n -> p n t"),
             )
 
-        def support_quant(g):
-            nc.vector.quantize_mx(out=s_codes[:, g, :].bitcast(E4M3X4), scales=s_plane[:, g, :], in_=s_grouped[g][:])
+        def support_quant(first, last):
+            cols = slice(HALF * first, HALF * last)
+            nc.vector.quantize_mx(out=s_codes[:, cols].bitcast(E4M3X4), scales=s_plane[:, cols], in_=s_part(first, last))
 
+        def pieces(u):
+            return [(0, u), (1, u)] if u < 2 else [(u - 2, 0), (u - 2, 1)]
 
-        def store(q, j, res, cols=slice(0, HID)):
+        def unit_view(whole, u):
+            by_piece = whole.rearrange("p j (h c) -> p j h c", c=HALF)
+            return by_piece[:, :, u, :] if u < 2 else by_piece[:, u - 2, :, :]
+
+        def unit_bias(u):
+            by_half = bias[:].rearrange("p (h c) -> p h c", c=HALF)
+            return by_half[:, u : u + 1, :].to_broadcast([P, 2, HALF]) if u < 2 else by_half
+
+        def result(q):
+            if q not in res:
+                res[q] = keep.tile([P, 2, HID], F32, name="res%d" % q)[:]
+            return res[q]
+
+        def store(q, u=None, lo=0, hi=2):
             rows = out[PAIR_ROWS * q : PAIR_ROWS * (q + 1), :].rearrange("(m j) h -> m j h", j=2)
-            nc.sync.dma_start(out=rows[:, j, cols], in_=res)
+            if u is None:
+                nc.sync.dma_start(out=rows, in_=res[q])
+            else:
+                nc.sync.dma_start(out=unit_view(rows, u)[:, lo:hi, :], in_=unit_view(res[q], u)[:, lo:hi, :])
 
-        def out_mm(q, j, first=0, last=PASSES):
+        def out_mm(q, u, first=0, last=PASSES):
             if first == 0:
-                total[q, j] = other_bank([P, HID])
-            cols = slice(P * j, P * (j + 1))
+                total[q, u] = other_bank([P, 2, HALF])
             for g in range(first, last):
-                nc.tensor.matmul_mx(
-                    out=total[q, j][:],
-                    lhsT=a_codes[:, q, g, cols].bitcast(E4M3X4),
-                    lhsT_scale=a_plane[:, q, g, cols],
-                    rhs=s_codes[:, g, :].bitcast(E4M3X4),
-                    rhs_scale=s_plane[:, g, :],
-                    start=(g == 0),
-                    stop=(g == PASSES - 1),
-                )
+                for i, (j, h) in enumerate(pieces(u)):
+                    cols = slice(HALF * (PASSES * h + g), HALF * (PASSES * h + g + 1))
+                    start = code_start(PASSES * q + g) + P * j
+                    rows = slice(start, start + P)
+                    nc.tensor.matmul_mx(
+                        out=total[q, u][:, i, :],
+                        lhsT=a_codes[:, rows].bitcast(E4M3X4),
+                        lhsT_scale=a_plane[:, rows],
+                        rhs=s_codes[:, cols].bitcast(E4M3X4),
+                        rhs_scale=s_plane[:, cols],
+                        start=(g == 0 and i == 0),
+                        stop=(g == PASSES - 1 and i == 1),
+                    )
 
-        def vector_bias(q, j):
-            res = keep.tile([P, HID], F32, name="res%d_%d" % (q, j))
-            nc.vector.tensor_tensor(out=res[:], in0=total[q, j][:], in1=bias[:], op=ALU.add)
-            return res
+        def vector_bias(q, u):
+            nc.vector.tensor_tensor(out=unit_view(result(q), u), in0=total[q, u][:], in1=unit_bias(u), op=ALU.add)
 
-        def relu_store(q, j, res):
-            nc.scalar.activation(out=res, in_=res, func=ACT.Relu)
-            store(q, j, res)
+        def relu_operands(q, u, lo, hi):
+            if u is None:
+                dst = result(q).rearrange("p j h -> p (j h)")
+                return dst, pool_sum.get((q, u), dst)
+            dst = unit_view(result(q), u)
+            return dst[:, lo:hi, :], pool_sum.get((q, u), dst)[:, lo:hi, :]
 
-        def vector_finish(q, j):
-            relu_store(q, j, vector_bias(q, j)[:])
+        def scalar_relu(q, u=None, lo=0, hi=2):
+            dst, src = relu_operands(q, u, lo, hi)
+            nc.scalar.activation(out=dst, in_=src, func=ACT.Relu)
 
-        def last_finish(q, j):
-            res = vector_bias(q, j)
-            left, right = slice(0, HID // 2), slice(HID // 2, HID)
-            nc.scalar.activation(out=res[:, left], in_=res[:, left], func=ACT.Relu)
-            nc.vector.tensor_scalar(out=res[:, right], in0=res[:, right], scalar1=0.0, scalar2=None, op0=ALU.max)
-            for cols in (right, left):
-                store(q, j, res[:, cols], cols)
+        def vector_relu(q, u=None, lo=0, hi=2):
+            dst, src = relu_operands(q, u, lo, hi)
+            nc.vector.tensor_scalar(out=dst, in0=src, scalar1=0.0, scalar2=None, op0=ALU.max)
 
-        def park(q):
-            parked[q] = keep.tile([P, 2, HID], F32, name="parked%d" % q)
-            for j in range(2):
-                nc.scalar.copy(out=parked[q][:, j, :], in_=total[q, j][:])
+        def pool_relu(q, u=None, lo=0, hi=2):
+            dst, src = relu_operands(q, u, lo, hi)
+            nc.gpsimd.tensor_scalar(out=dst, in0=src, scalar1=0.0, scalar2=0.0, op0=ALU.max, op1=ALU.add)
 
-        def pool_bias(q, host):
-            pool_sum[q] = host[:, 0 : 4 * HID].bitcast(F32).rearrange("p (j h) -> p j h", j=2)
-            spread = bias[:].rearrange("p (o h) -> p o h", o=1).to_broadcast([P, 2, HID])
-            nc.gpsimd.tensor_tensor(out=pool_sum[q], in0=parked[q][:], in1=spread, op=ALU.add)
+        def park(q, u):
+            job = [b for b in POOL_ADDS if (q, u) in b][0]
+            if job not in parked:
+                parked[job] = keep.tile([P, len(job), 2, HALF], F32, name="parked%d_%d" % job[0])
+            nc.scalar.copy(out=parked[job][:, job.index((q, u)), :, :], in_=total[q, u][:])
 
-        def pool_finish(q):
-            for j in range(2):
-                relu_store(q, j, pool_sum[q][:, j, :])
-
+        def pool_bias(q, u, host):
+            job = [b for b in POOL_ADDS if (q, u) in b][0]
+            n = len(job)
+            flat = host[:, 0 : 4 * HALF * n].bitcast(F32)
+            width = HALF if u < 2 else HID
+            for i, unit in enumerate(job):
+                pool_sum[unit] = flat[:, HID * i : HID * (i + 1)].rearrange("p (i c) -> p i c", c=HALF)
+            pool_sum[q, None] = flat
+            cols = slice(HALF * u, HALF * (u + 1)) if u < 2 else slice(0, HID)
+            spread = bias[:, cols].rearrange("p (o c) -> p o c", o=1).to_broadcast([P, HID * n // width, width])
+            nc.gpsimd.tensor_tensor(
+                out=flat.rearrange("p (i c) -> p i c", c=width),
+                in0=parked[job][:].rearrange("p n i c -> p (n i c)").rearrange("p (i c) -> p i c", c=width),
+                in1=spread,
+                op=ALU.add,
+            )
 
         def flip_mm(q, h):
-            if h == 0:
-                flip_flat[q] = keep.tile([P, CHUNKS, PAIR_ROWS], F32, name="flip_flat%d" % q)
+            flip_flat[q, h] = keep.tile([P, 2, PAIR_ROWS], F32, name="flip_flat%d_%d" % (q, h))
             bank = other_bank([P, 2, PAIR_ROWS])
             flip_total[q, h] = bank
             for i in range(2):
-                cols = slice(P * (2 * h + i), P * (2 * h + i + 1))
                 for g in range(PASSES):
+                    cols = slice(HALF * (PASSES * h + g) + P * i, HALF * (PASSES * h + g) + P * (i + 1))
+                    rows = slice(code_start(PASSES * q + g), code_start(PASSES * q + g) + PAIR_ROWS)
                     nc.tensor.matmul_mx(
                         out=bank[:, i, :],
-                        lhsT=s_codes[:, g, cols].bitcast(E4M3X4),
-                        lhsT_scale=s_plane[:, g, cols],
-                        rhs=a_codes[:, q, g, :].bitcast(E4M3X4),
-                        rhs_scale=a_plane[:, q, g, :],
+                        lhsT=s_codes[:, cols].bitcast(E4M3X4),
+                        lhsT_scale=s_plane[:, cols],
+                        rhs=a_codes[:, rows].bitcast(E4M3X4),
+                        rhs_scale=a_plane[:, rows],
                         start=(g == 0),
                         stop=(g == PASSES - 1),
                     )
@@ -259,25 +334,31 @@ def tile_gcn_pa_w4_kernel(tc, x_init, adj_bytes, adj_scale, w_words, w_scales, b
             for i in range(2):
                 c = 2 * h + i
                 nc.scalar.activation(
-                    out=flip_flat[q][:, c, :], in_=flip_total[q, h][:, i, :], func=ACT.Relu, bias=bias_col[:, c : c + 1]
+                    out=flip_flat[q, h][:, i, :], in_=flip_total[q, h][:, i, :], func=ACT.Relu, bias=bias_col[:, c : c + 1]
                 )
 
-        def flip_back(q, new_bank):
-            for j in range(2):
-                bank = new_bank([P, CHUNKS, P])
-                back_bank[q, j] = bank
-                for c in range(CHUNKS):
-                    nc.tensor.transpose(bank[:, c, :], flip_flat[q][:, c, P * j : P * (j + 1)], ident[:])
+        def flip_back(q, u, new_bank):
+            bank = new_bank([P, 2, HALF])
+            back_bank[q, u] = bank
+            for n, (j, h) in enumerate(pieces(u)):
+                for i in range(2):
+                    nc.tensor.transpose(bank[:, n, P * i : P * (i + 1)], flip_flat[q, h][:, i, P * j : P * (j + 1)], ident[:])
 
-        def flip_finish(q):
-            for j in range(2):
-                res = keep.tile([P, HID], F32, name="res%d_%d" % (q, j))
-                nc.scalar.copy(out=res[:], in_=back_bank[q, j][:].rearrange("p c m -> p (c m)"))
-                store(q, j, res[:])
+        def flip_out(q, u):
+            nc.scalar.copy(out=unit_view(result(q), u), in_=back_bank[q, u][:])
+
+        def load_bias_rows():
+            nc.sync.dma_start(out=bias_rows[0:CHUNKS, :], in_=b1.rearrange("(c m) -> c m", m=P))
+
+        def cast_bias():
+            nc.scalar.copy(out=bias_rows_f32[:], in_=bias_rows[:])
 
         def turn_bias():
             bias_bank[0] = other_bank([P, 4, P])
             nc.tensor.transpose(bias_bank[0][:, 0, :], bias_rows_f32[:], ident[:])
+
+        def bias_out():
+            nc.scalar.copy(out=bias_col[:], in_=bias_bank[0][:, 0, 0:CHUNKS])
 
         on_vector, on_scalar, on_pool = nc.vector.tensor_copy, nc.scalar.copy, nc.gpsimd.tensor_copy
 
@@ -285,7 +366,6 @@ def tile_gcn_pa_w4_kernel(tc, x_init, adj_bytes, adj_scale, w_words, w_scales, b
             make_identity(nc, ident[:])
             nc.gpsimd.memset(w_plane[:].bitcast(I32), 0)
             nc.gpsimd.memset(bias_rows[:], 0.0)
-
             load_adj(0, 0, 1, (0,))
             load_scale()
             load_adj(0, 0, 1, (1,))
@@ -293,141 +373,171 @@ def tile_gcn_pa_w4_kernel(tc, x_init, adj_bytes, adj_scale, w_words, w_scales, b
             load_x(0, (0,))
             load_adj(1)
             load_x(0, (1,))
-            nc.sync.dma_start(out=bias_rows[0:CHUNKS, :], in_=b1.rearrange("(c m) -> c m", m=P))
+            load_bias_rows()
             load_x(1, (0, 1))
-            load_w()
-            load_adj(2)
             load_x(2, (0, 1))
-            for q in range(3, PAIRS):
-                load_adj(q)
-            nc.sync.dma_start(out=bias[:], in_=b1.partition_broadcast(P))
-
-            for j in range(2):
-                widen(on_vector, 0, 0, 1, 0, 1, j)
-            for g in range(2):
-                for j in range(2):
-                    widen(on_scalar, 0, 2 * j + g, 2 * j + g + 1, 1, PASSES)
-            for j in range(2):
-                adj_turn(0, (j,))
-            for j in range(2):
-                adj_mult(0, (j,))
+            load_w_codes()
+            load_w_scales()
+            load_adj(2)
+            load_adj(3)
+            load_bias()
+            load_adj(4)
+            load_adj(5)
+            widen(on_scalar, [(0, 0, 1)])
+            widen(on_scalar, [(0, 1, 1)])
+            widen(on_scalar, [(0, 0, 2)])
+            widen(on_scalar, [(0, 1, 2)])
+            widen(on_scalar, [(1, 0, 0), (1, 0, 1), (1, 0, 2), (1, 1, 0)])
+            widen(on_vector, [(0, 0, 0)])
+            widen(on_vector, [(0, 1, 0)])
+            widen(on_pool, [(1, 1, 1), (1, 1, 2)])
+            adj_turn(0, (0,))
+            adj_turn(0, (1,))
             adj_turn(1)
             adj_turn(2)
             x_turn(0, 0)
-            widen(on_scalar, 1, 0, 4)
-            widen(on_pool, 1, 4, SEGMENTS)
             x_turn(0, 1)
+            x_out(0, 0)
+            x_out(0, 1)
+            cast_bias()
+            adj_mult(0, (0,))
+            adj_mult(0, (1,))
+            adj_mult(1)
+            adj_mult(2)
             adj_turn(3)
-            for b in range(2):
-                x_out(0, b)
-            nc.scalar.copy(out=bias_rows_f32[:], in_=bias_rows[:])
-            for slab in range(1, 4):
-                adj_mult(slab)
-            for b in range(2):
-                x_turn(1, b)
+            x_turn(1, 0)
+            x_turn(1, 1)
+            x_turn(2, 0)
+            x_turn(2, 1)
             adj_turn(4)
             adj_turn(5)
-            for b in range(2):
-                x_out(1, b)
-            turn_bias()
-            widen(on_scalar, 2, 0, SEGMENTS)
-            nc.scalar.copy(out=bias_col[:], in_=bias_bank[0][:, 0, 0:CHUNKS])
-            x_quant(0)
-            adj_quant(0)
-            x_quant(1)
-            widen(on_pool, 3, PASSES, SEGMENTS, host=x_grouped[1])
-            adj_mult(4)
-
-            for c in range(CHUNKS):
-                support_mm(0, c)
-            for c in range(CHUNKS):
-                support_out(0, c)
-            adj_turn(6)
-            x_turn(2, 0)
-            support_mm(1, 0)
-            support_mm(1, 1)
-            x_turn(2, 1)
-            adj_turn(7)
+            x_out(1, 0)
+            x_out(1, 1)
             x_out(2, 0)
-            support_out(1, 0)
             x_out(2, 1)
+            widen(on_scalar, [(2, 0, 0), (2, 0, 1), (2, 0, 2), (2, 1, 0)])
+            adj_mult(3)
+            x_quant(0, 1)
+            adj_quant(0)
+            x_quant(1, 3)
+            adj_mult(4)
+            adj_mult(5)
+            widen(on_pool, [(3, 0, 0), (3, 0, 1), (3, 0, 2), (3, 1, 0)], x_grouped[:, 4 * K_PASS :])
+            turn_bias()
+            support_mm(0, 0)
+            support_mm(0, 1)
+            adj_turn(6)
+            support_mm(1, 0)
+            bias_out()
+            support_out(0, 0)
+            support_out(0, 1)
+            widen(on_scalar, [(2, 1, 1), (2, 1, 2)])
+            support_out(1, 0)
+            adj_mult(6)
+            support_mm(1, 1)
+            support_mm(2, 0)
+            support_mm(2, 1)
+            adj_turn(7)
+            adj_turn(8)
+            support_mm(0, 2)
+            support_out(1, 1)
+            support_out(2, 0)
+            support_out(2, 1)
+            widen(on_scalar, [(3, 1, 1), (3, 1, 2)])
+            support_out(0, 2)
+            adj_mult(7)
+            support_quant(0, 2)
+            support_quant(2, 3)
+            adj_quant(4)
+            adj_mult(8)
+            support_mm(0, 3)
+            adj_turn(9)
             support_mm(1, 2)
             support_mm(1, 3)
-            for c in range(1, CHUNKS):
-                support_out(1, c)
-            widen(on_scalar, 3, 0, 2)
-            adj_mult(5)
-            adj_mult(6)
-            adj_quant(4)
-            support_quant(0)
-            x_quant(2)
-            widen(on_pool, 4, 4, SEGMENTS, host=x_grouped[2])
-            adj_turn(8)
-            adj_mult(7)
-            for c in range(CHUNKS):
-                support_mm(2, c)
-            for c in range(CHUNKS):
-                support_out(2, c)
-            widen(on_scalar, 3, 2, PASSES)
-            adj_turn(9)
             adj_turn(10)
-            adj_mult(8)
-            support_quant(1)
-            for j in range(2):
-                out_mm(0, j, 0, 2)
             adj_turn(11)
-            widen(on_scalar, 4, 0, 4)
-            adj_mult(9)
-            support_quant(2)
+            support_mm(2, 2)
+            support_out(0, 3)
+            adj_out(9)
+            support_out(1, 2)
+            support_out(1, 3)
+            widen(on_scalar, [(4, 0, 0), (4, 0, 1), (4, 0, 2), (4, 1, 0), (4, 1, 1), (4, 1, 2)])
+            support_out(2, 2)
             adj_mult(10)
-            adj_quant(6)
-
-            for j in range(2):
-                out_mm(0, j, 2, PASSES)
-            for j in range(2):
-                out_mm(1, j)
+            adj_mult(11)
+            support_quant(3, 5)
+            pool_mult(9, None)
+            support_mm(2, 3)
+            out_mm(0, 0, 0, 3)
+            out_mm(1, 0, 0, 3)
             adj_turn(12)
             adj_turn(13)
-            park(0)
-            pool_bias(0, a_grouped[6])
-            park(1)
-            widen(on_scalar, 5, 0, SEGMENTS)
-            for h in range(2):
-                flip_mm(2, h)
-            for slab in range(11, 14):
-                adj_mult(slab)
-            adj_quant(10)
-            pool_bias(1, a_grouped[10])
-
             adj_turn(14)
-            adj_turn(15)
-            for h in range(2):
-                flip_relu(2, h)
-            flip_mm(3, 0)
-            pool_finish(0)
-            adj_turn(16)
-            flip_back(2, other_bank)
-            flip_mm(3, 1)
-            flip_relu(3, 0)
-            flip_finish(2)
-            flip_relu(3, 1)
+            support_out(2, 3)
+            park(0, 0)
+            park(1, 0)
+            widen(on_scalar, [(5, 0, 0), (5, 0, 1), (5, 0, 2), (5, 1, 0), (5, 1, 1), (5, 1, 2)])
+            support_quant(5, 6)
+            adj_quant(9)
+            adj_mult(12)
             adj_mult(14)
-            adj_turn(17)
-            adj_mult(15)
-            flip_back(3, slab_bank)
-            pool_finish(1)
-            flip_finish(3)
-
-            adj_mult(16)
+            adj_mult(13)
+            adj_quant(14)
             adj_quant(12)
-            for j in range(2):
-                out_mm(4, j)
+            pool_bias(0, 0, a_grouped[9])
+            flip_mm(0, 1)
+            flip_mm(1, 1)
+            flip_mm(2, 0)
+            flip_mm(2, 1)
+            adj_turn(15)
+            adj_turn(16)
+            flip_relu(0, 1)
+            flip_relu(1, 1)
+            flip_relu(2, 0)
+            flip_relu(2, 1)
+            adj_out(15)
+            scalar_relu(0, 0)
+            adj_mult(16)
+            pool_mult(15, None)
+            flip_back(0, 1, other_bank)
+            flip_back(1, 1, other_bank)
+            adj_turn(17)
+            flip_back(2, 2, slab_bank)
+            flip_back(2, 3, slab_bank)
+            out_mm(3, 2, 0, 3)
+            out_mm(3, 3, 0, 3)
+            flip_out(0, 1)
+            flip_out(1, 1)
+            scalar_relu(1, 0)
+            flip_out(2, 2)
+            flip_out(2, 3)
             adj_mult(17)
-            adj_quant(16)
-            vector_finish(4, 0)
+            vector_bias(3, 2)
+            adj_quant(15)
             adj_quant(17)
-            for j in range(2):
-                out_mm(5, j)
-            vector_finish(4, 1)
-            vector_finish(5, 0)
-            last_finish(5, 1)
+            vector_bias(3, 3)
+            store(0)
+            store(1)
+            store(2)
+            out_mm(4, 2, 0, 3)
+            out_mm(4, 3, 0, 3)
+            out_mm(5, 2, 0, 3)
+            out_mm(5, 3, 0, 3)
+            scalar_relu(3, 2)
+            scalar_relu(3, 3)
+            vector_bias(4, 2)
+            vector_bias(4, 3)
+            vector_bias(5, 2)
+            vector_bias(5, 3)
+            vector_relu(5, 3, 1, 2)
+            store(3, 2)
+            store(3, 3)
+            scalar_relu(4, 2)
+            scalar_relu(4, 3)
+            scalar_relu(5, 2)
+            scalar_relu(5, 3, 0, 1)
+            store(4, 2)
+            store(4, 3)
+            store(5, 2)
+            store(5, 3, 1, 2)
+            store(5, 3, 0, 1)

@@ -27,8 +27,8 @@ HALF = HID // 2
 SLAB_BANKS = 4
 OTHER_BANKS = 8 - SLAB_BANKS
 QUANT_CALLS = ((0, 1, 2, 3), (4, 5, 6, 7), (9, 8, 10, 11), (12, 13), (14,), (15, 16), (17,))
-POOL_ADDS = (((0, 0), (1, 0)),)
-STRIP_STARTS = {4: 0, 9: 3072, 12: 0, 15: 1024}
+POOL_ADDS = ()
+STRIP_STARTS = {4: 0, 9: 3072, 12: 6144, 15: 7168}
 
 FLOPS = 2 * NODES * FEAT * HID + 2 * NODES * NODES * HID
 
@@ -41,6 +41,7 @@ def tile_gcn_pa_w4_kernel(tc, x_init, adj_bytes, adj_scale, w_words, w_scales, b
 
         ident = keep.tile([P, P], F32, name="ident")
         scale_cols = keep.tile([P, PASSES, 4], F32, name="scale_cols")
+        scale_tile = keep.tile([P, K_PASS], F32, name="scale_tile")
         bias = keep.tile([P, HID], BF16, name="bias")
         w_codes = keep.tile([P, 2 * HID], U8, name="w_codes", align_bytes=64)
         w_plane = keep.tile([P, HID], U8, name="w_plane", align_bytes=64)
@@ -52,7 +53,7 @@ def tile_gcn_pa_w4_kernel(tc, x_init, adj_bytes, adj_scale, w_words, w_scales, b
         a_plane = keep.tile([P, PAIRS * PASSES * PAIR_ROWS], U8, name="a_plane", align_bytes=64)
         x_grouped = keep.tile([P, 6144], BF16, name="x_grouped", align_bytes=64)
         s_grouped = keep.tile([P, PASSES * 4 * HID], BF16, name="s_grouped", align_bytes=64)
-        strip = keep.tile([P, 8192], BF16, name="strip", align_bytes=64)
+        strip = keep.tile([P, 9216], BF16, name="strip", align_bytes=64)
         bias_rows = keep.tile([P, P], BF16, name="bias_rows")
         bias_rows_f32 = keep.tile([P, P], F32, name="bias_rows_f32")
         bias_col = keep.tile([P, CHUNKS], F32, name="bias_col")
@@ -161,13 +162,17 @@ def tile_gcn_pa_w4_kernel(tc, x_init, adj_bytes, adj_scale, w_words, w_scales, b
                 in_=a_bank[slab, 0][:].rearrange("p u r -> p r u"),
             )
 
+        def repeat_scale():
+            factor = scale_cols[:, 0, :].rearrange("p (o t) -> p o t", o=1)
+            nc.scalar.copy(out=scale_tile[:].rearrange("p (r t) -> p r t", t=4), in_=factor.to_broadcast([P, P, 4]))
+
         def pool_mult(slab, host):
             part = grouped_part(slab, (0, 1), host)
-            factor = scale_cols[:, slab % PASSES, :].rearrange("p (o t) -> p o t", o=1)
+            factor = scale_tile[:].rearrange("p (o c) -> p o c", o=1)
             nc.gpsimd.tensor_tensor(
-                out=part.rearrange("p (r t) -> p r t", t=4),
-                in0=a_staged[slab][:].rearrange("p (r t) -> p r t", t=4),
-                in1=factor.to_broadcast([P, PAIR_ROWS, 4]),
+                out=part.rearrange("p (j c) -> p j c", j=2),
+                in0=a_staged[slab][:].rearrange("p (j c) -> p j c", j=2),
+                in1=factor.to_broadcast([P, 2, K_PASS]),
                 op=ALU.mult,
             )
 
@@ -383,6 +388,7 @@ def tile_gcn_pa_w4_kernel(tc, x_init, adj_bytes, adj_scale, w_words, w_scales, b
             load_bias()
             load_adj(4)
             load_adj(5)
+            repeat_scale()
             widen(on_scalar, [(0, 0, 1)])
             widen(on_scalar, [(0, 1, 1)])
             widen(on_scalar, [(0, 0, 2)])
@@ -461,7 +467,7 @@ def tile_gcn_pa_w4_kernel(tc, x_init, adj_bytes, adj_scale, w_words, w_scales, b
             adj_out(9)
             support_out(1, 2)
             support_out(1, 3)
-            widen(on_scalar, [(4, 0, 0), (4, 0, 1), (4, 0, 2), (4, 1, 0), (4, 1, 1), (4, 1, 2)])
+            widen(on_scalar, [(4, 0, 0), (4, 0, 1), (4, 0, 2), (4, 1, 0)])
             support_out(2, 2)
             adj_mult(10)
             adj_mult(11)
@@ -469,22 +475,19 @@ def tile_gcn_pa_w4_kernel(tc, x_init, adj_bytes, adj_scale, w_words, w_scales, b
             pool_mult(9, None)
             support_mm(2, 3)
             out_mm(0, 0, 0, 3)
-            out_mm(1, 0, 0, 3)
             adj_turn(12)
-            adj_turn(13)
-            adj_turn(14)
+            out_mm(1, 0, 0, 3)
             support_out(2, 3)
-            park(0, 0)
-            park(1, 0)
+            widen(on_scalar, [(4, 1, 1), (4, 1, 2)])
+            adj_out(12)
             widen(on_scalar, [(5, 0, 0), (5, 0, 1), (5, 0, 2), (5, 1, 0), (5, 1, 1), (5, 1, 2)])
             support_quant(5, 6)
             adj_quant(9)
-            adj_mult(12)
-            adj_mult(14)
-            adj_mult(13)
-            adj_quant(14)
-            adj_quant(12)
-            pool_bias(0, 0, a_grouped[9])
+            vector_bias(0, 0)
+            vector_bias(1, 0)
+            pool_mult(12, None)
+            adj_turn(13)
+            adj_turn(14)
             flip_mm(0, 1)
             flip_mm(1, 1)
             flip_mm(2, 0)
@@ -493,32 +496,39 @@ def tile_gcn_pa_w4_kernel(tc, x_init, adj_bytes, adj_scale, w_words, w_scales, b
             adj_turn(16)
             flip_relu(0, 1)
             flip_relu(1, 1)
+            scalar_relu(0, 0)
             flip_relu(2, 0)
             flip_relu(2, 1)
             adj_out(15)
-            scalar_relu(0, 0)
+            scalar_relu(1, 0)
+            adj_mult(14)
+            adj_mult(13)
+            adj_quant(14)
+            adj_quant(12)
             adj_mult(16)
             pool_mult(15, None)
+            store(0, 0)
+            store(1, 0)
             flip_back(0, 1, other_bank)
             flip_back(1, 1, other_bank)
+            out_mm(3, 2, 0, 3)
             adj_turn(17)
             flip_back(2, 2, slab_bank)
             flip_back(2, 3, slab_bank)
-            out_mm(3, 2, 0, 3)
             out_mm(3, 3, 0, 3)
             flip_out(0, 1)
             flip_out(1, 1)
-            scalar_relu(1, 0)
             flip_out(2, 2)
             flip_out(2, 3)
-            adj_mult(17)
             vector_bias(3, 2)
+            adj_mult(17)
+            vector_bias(3, 3)
             adj_quant(15)
             adj_quant(17)
-            vector_bias(3, 3)
-            store(0)
-            store(1)
-            store(2)
+            store(0, 1)
+            store(1, 1)
+            store(2, 2)
+            store(2, 3)
             out_mm(4, 2, 0, 3)
             out_mm(4, 3, 0, 3)
             out_mm(5, 2, 0, 3)

@@ -27,8 +27,8 @@ HALF = HID // 2
 SLAB_BANKS = 4
 OTHER_BANKS = 8 - SLAB_BANKS
 QUANT_CALLS = ((0, 1, 2, 3), (4, 5, 6, 7), (9, 8, 10, 11), (12, 13), (14,), (15, 16), (17,))
-POOL_ADDS = ()
-STRIP_STARTS = {4: 0, 9: 3072, 12: 6144, 15: 7168}
+POOL_ADDS = (((0, 0), (1, 0)),)
+STRIP_STARTS = {4: 0, 9: 3072, 12: 0, 15: 1024}
 
 FLOPS = 2 * NODES * FEAT * HID + 2 * NODES * NODES * HID
 
@@ -53,7 +53,7 @@ def tile_gcn_pa_w4_kernel(tc, x_init, adj_bytes, adj_scale, w_words, w_scales, b
         a_plane = keep.tile([P, PAIRS * PASSES * PAIR_ROWS], U8, name="a_plane", align_bytes=64)
         x_grouped = keep.tile([P, 6144], BF16, name="x_grouped", align_bytes=64)
         s_grouped = keep.tile([P, PASSES * 4 * HID], BF16, name="s_grouped", align_bytes=64)
-        strip = keep.tile([P, 9216], BF16, name="strip", align_bytes=64)
+        strip = keep.tile([P, 8192], BF16, name="strip", align_bytes=64)
         bias_rows = keep.tile([P, P], BF16, name="bias_rows")
         bias_rows_f32 = keep.tile([P, P], F32, name="bias_rows_f32")
         bias_col = keep.tile([P, CHUNKS], F32, name="bias_col")
@@ -254,9 +254,9 @@ def tile_gcn_pa_w4_kernel(tc, x_init, adj_bytes, adj_scale, w_words, w_scales, b
             else:
                 nc.sync.dma_start(out=unit_view(rows, u)[:, lo:hi, :], in_=unit_view(res[q], u)[:, lo:hi, :])
 
-        def out_mm(q, u, first=0, last=PASSES):
+        def out_mm(q, u, first=0, last=PASSES, new_bank=other_bank):
             if first == 0:
-                total[q, u] = other_bank([P, 2, HALF])
+                total[q, u] = new_bank([P, 2, HALF])
             for g in range(first, last):
                 for i, (j, h) in enumerate(pieces(u)):
                     cols = slice(HALF * (PASSES * h + g), HALF * (PASSES * h + g + 1))
@@ -479,13 +479,13 @@ def tile_gcn_pa_w4_kernel(tc, x_init, adj_bytes, adj_scale, w_words, w_scales, b
             out_mm(1, 0, 0, 3)
             support_out(2, 3)
             widen(on_scalar, [(4, 1, 1), (4, 1, 2)])
-            adj_out(12)
+            park(0, 0)
+            park(1, 0)
             widen(on_scalar, [(5, 0, 0), (5, 0, 1), (5, 0, 2), (5, 1, 0), (5, 1, 1), (5, 1, 2)])
             support_quant(5, 6)
             adj_quant(9)
-            vector_bias(0, 0)
-            vector_bias(1, 0)
-            pool_mult(12, None)
+            adj_mult(12)
+            pool_bias(0, 0, a_grouped[9])
             adj_turn(13)
             adj_turn(14)
             flip_mm(0, 1)
@@ -496,19 +496,16 @@ def tile_gcn_pa_w4_kernel(tc, x_init, adj_bytes, adj_scale, w_words, w_scales, b
             adj_turn(16)
             flip_relu(0, 1)
             flip_relu(1, 1)
-            scalar_relu(0, 0)
             flip_relu(2, 0)
             flip_relu(2, 1)
             adj_out(15)
-            scalar_relu(1, 0)
+            scalar_relu(0, 0)
             adj_mult(14)
             adj_mult(13)
             adj_quant(14)
             adj_quant(12)
             adj_mult(16)
             pool_mult(15, None)
-            store(0, 0)
-            store(1, 0)
             flip_back(0, 1, other_bank)
             flip_back(1, 1, other_bank)
             out_mm(3, 2, 0, 3)
@@ -517,6 +514,7 @@ def tile_gcn_pa_w4_kernel(tc, x_init, adj_bytes, adj_scale, w_words, w_scales, b
             flip_back(2, 3, slab_bank)
             out_mm(3, 3, 0, 3)
             flip_out(0, 1)
+            scalar_relu(1, 0)
             flip_out(1, 1)
             flip_out(2, 2)
             flip_out(2, 3)
@@ -525,8 +523,8 @@ def tile_gcn_pa_w4_kernel(tc, x_init, adj_bytes, adj_scale, w_words, w_scales, b
             vector_bias(3, 3)
             adj_quant(15)
             adj_quant(17)
-            store(0, 1)
-            store(1, 1)
+            store(0)
+            store(1)
             store(2, 2)
             store(2, 3)
             out_mm(4, 2, 0, 3)

@@ -272,8 +272,10 @@ def tile_gcn_pa_w4_kernel(tc, x_init, adj_bytes, adj_scale, w_words, w_scales, b
                         stop=(g == PASSES - 1 and i == 1),
                     )
 
-        def vector_bias(q, u):
-            nc.vector.tensor_tensor(out=unit_view(result(q), u), in0=total[q, u][:], in1=unit_bias(u), op=ALU.add)
+        def vector_bias(q, u, lo=0, hi=2):
+            nc.vector.tensor_tensor(
+                out=unit_view(result(q), u)[:, lo:hi, :], in0=total[q, u][:, lo:hi, :], in1=unit_bias(u)[:, lo:hi, :], op=ALU.add
+            )
 
         def relu_operands(q, u, lo, hi):
             if u is None:
@@ -317,13 +319,13 @@ def tile_gcn_pa_w4_kernel(tc, x_init, adj_bytes, adj_scale, w_words, w_scales, b
                 op=ALU.add,
             )
 
-        def flip_mm(q, h):
-            flip_flat[q, h] = keep.tile([P, 2, PAIR_ROWS], F32, name="flip_flat%d_%d" % (q, h))
+        def flip_mm(parts):
             bank = other_bank([P, 2, PAIR_ROWS])
-            flip_total[q, h] = bank
-            for i in range(2):
+            flip_total[parts] = bank
+            for i, (q, c) in enumerate(parts):
                 for g in range(PASSES):
-                    cols = slice(HALF * (PASSES * h + g) + P * i, HALF * (PASSES * h + g) + P * (i + 1))
+                    start = HALF * (PASSES * (c // 2) + g) + P * (c % 2)
+                    cols = slice(start, start + P)
                     rows = slice(code_start(PASSES * q + g), code_start(PASSES * q + g) + PAIR_ROWS)
                     nc.tensor.matmul_mx(
                         out=bank[:, i, :],
@@ -335,19 +337,23 @@ def tile_gcn_pa_w4_kernel(tc, x_init, adj_bytes, adj_scale, w_words, w_scales, b
                         stop=(g == PASSES - 1),
                     )
 
-        def flip_relu(q, h):
-            for i in range(2):
-                c = 2 * h + i
+        def flip_relu(parts):
+            flat = keep.tile([P, 2, PAIR_ROWS], F32, name="flip_flat%d_%d" % parts[0])
+            step = 2 if parts[0][1] == parts[1][1] else 1
+            for i in range(0, 2, step):
+                c = parts[i][1]
                 nc.scalar.activation(
-                    out=flip_flat[q, h][:, i, :], in_=flip_total[q, h][:, i, :], func=ACT.Relu, bias=bias_col[:, c : c + 1]
+                    out=flat[:, i : i + step, :], in_=flip_total[parts][:, i : i + step, :], func=ACT.Relu, bias=bias_col[:, c : c + 1]
                 )
+            for i, part in enumerate(parts):
+                flip_flat[part] = flat[:, i, :]
 
         def flip_back(q, u, new_bank):
             bank = new_bank([P, 2, HALF])
             back_bank[q, u] = bank
             for n, (j, h) in enumerate(pieces(u)):
                 for i in range(2):
-                    nc.tensor.transpose(bank[:, n, P * i : P * (i + 1)], flip_flat[q, h][:, i, P * j : P * (j + 1)], ident[:])
+                    nc.tensor.transpose(bank[:, n, P * i : P * (i + 1)], flip_flat[q, 2 * h + i][:, P * j : P * (j + 1)], ident[:])
 
         def flip_out(q, u):
             nc.scalar.copy(out=unit_view(result(q), u), in_=back_bank[q, u][:])
@@ -428,7 +434,7 @@ def tile_gcn_pa_w4_kernel(tc, x_init, adj_bytes, adj_scale, w_words, w_scales, b
             x_quant(1, 3)
             adj_mult(4)
             adj_mult(5)
-            widen(on_pool, [(3, 0, 0), (3, 0, 1), (3, 0, 2), (3, 1, 0)], x_grouped[:, 4 * K_PASS :])
+            widen(on_pool, [(3, 0, 0), (3, 0, 1), (3, 0, 2), (3, 1, 0), (3, 1, 1)], x_grouped[:, 4 * K_PASS :])
             turn_bias()
             support_mm(0, 0)
             support_mm(0, 1)
@@ -449,12 +455,12 @@ def tile_gcn_pa_w4_kernel(tc, x_init, adj_bytes, adj_scale, w_words, w_scales, b
             support_out(1, 1)
             support_out(2, 0)
             support_out(2, 1)
-            widen(on_scalar, [(3, 1, 1), (3, 1, 2)])
+            widen(on_scalar, [(3, 1, 2)])
             support_out(0, 2)
             adj_mult(7)
             support_quant(0, 2)
-            support_quant(2, 3)
             adj_quant(4)
+            support_quant(2, 3)
             adj_mult(8)
             support_mm(0, 3)
             adj_turn(9)
@@ -488,22 +494,22 @@ def tile_gcn_pa_w4_kernel(tc, x_init, adj_bytes, adj_scale, w_words, w_scales, b
             pool_bias(0, 0, a_grouped[9])
             adj_turn(13)
             adj_turn(14)
-            flip_mm(0, 1)
-            flip_mm(1, 1)
-            flip_mm(2, 0)
-            flip_mm(2, 1)
+            flip_mm(((0, 2), (1, 2)))
+            flip_mm(((0, 3), (1, 3)))
+            flip_mm(((2, 0), (2, 1)))
+            flip_mm(((2, 2), (2, 3)))
             adj_turn(15)
             adj_turn(16)
-            flip_relu(0, 1)
-            flip_relu(1, 1)
-            flip_relu(2, 0)
-            flip_relu(2, 1)
+            flip_relu(((0, 2), (1, 2)))
+            flip_relu(((0, 3), (1, 3)))
+            flip_relu(((2, 0), (2, 1)))
+            flip_relu(((2, 2), (2, 3)))
             adj_out(15)
             scalar_relu(0, 0)
-            adj_mult(14)
             adj_mult(13)
-            adj_quant(14)
+            adj_mult(14)
             adj_quant(12)
+            adj_quant(14)
             adj_mult(16)
             pool_mult(15, None)
             flip_back(0, 1, other_bank)

@@ -24,11 +24,9 @@ PAIRS = NODES // PAIR_ROWS
 SEGMENTS = 2 * PASSES
 CHUNKS = HID // P
 HALF = HID // 2
-SLAB_BANKS = 4
-OTHER_BANKS = 8 - SLAB_BANKS
-QUANT_CALLS = ((0, 1, 2, 3), (4, 5, 6, 7), (9, 8, 10, 11), (12, 13), (14,), (15, 16), (17,))
-POOL_ADDS = (((0, 0), (1, 0)),)
-STRIP_STARTS = {4: 0, 9: 3072, 12: 0, 15: 1024}
+QUANT_CALLS = ((0, 1, 2, 3), (18, 19), (4, 5, 6, 7), (20,), (21, 22), (23,), (9, 8, 10, 11), (12, 13), (14,), (15, 16), (17,))
+POOL_ADDS = ()
+STRIP_STARTS = {4: 0, 9: 3072, 23: 8192, 12: 8192, 15: 9216}
 
 FLOPS = 2 * NODES * FEAT * HID + 2 * NODES * NODES * HID
 
@@ -41,19 +39,16 @@ def tile_gcn_pa_w4_kernel(tc, x_init, adj_bytes, adj_scale, w_words, w_scales, b
 
         ident = keep.tile([P, P], F32, name="ident")
         scale_cols = keep.tile([P, PASSES, 4], F32, name="scale_cols")
-        scale_tile = keep.tile([P, K_PASS], F32, name="scale_tile")
+        scale_tile = {}
         bias = keep.tile([P, HID], BF16, name="bias")
         w_codes = keep.tile([P, 2 * HID], U8, name="w_codes", align_bytes=64)
         w_plane = keep.tile([P, HID], U8, name="w_plane", align_bytes=64)
         x_codes = keep.tile([P, PASSES * K_PASS], U32, name="x_codes", align_bytes=64)
         x_plane = keep.tile([P, PASSES * K_PASS], U8, name="x_plane", align_bytes=64)
-        s_codes = keep.tile([P, PASSES * HID], U32, name="s_codes", align_bytes=64)
-        s_plane = keep.tile([P, PASSES * HID], U8, name="s_plane", align_bytes=64)
-        a_codes = keep.tile([P, PAIRS * PASSES * PAIR_ROWS], U32, name="a_codes", align_bytes=64)
-        a_plane = keep.tile([P, PAIRS * PASSES * PAIR_ROWS], U8, name="a_plane", align_bytes=64)
+        a_codes = keep.tile([P, 24 * PAIR_ROWS], U32, name="a_codes", align_bytes=64)
+        a_plane = keep.tile([P, 24 * PAIR_ROWS], U8, name="a_plane", align_bytes=64)
         x_grouped = keep.tile([P, 6144], BF16, name="x_grouped", align_bytes=64)
-        s_grouped = keep.tile([P, PASSES * 4 * HID], BF16, name="s_grouped", align_bytes=64)
-        strip = keep.tile([P, 8192], BF16, name="strip", align_bytes=64)
+        strip = keep.tile([P, 11264], BF16, name="strip", align_bytes=64)
         bias_rows = keep.tile([P, P], BF16, name="bias_rows")
         bias_rows_f32 = keep.tile([P, P], F32, name="bias_rows_f32")
         bias_col = keep.tile([P, CHUNKS], F32, name="bias_col")
@@ -61,15 +56,9 @@ def tile_gcn_pa_w4_kernel(tc, x_init, adj_bytes, adj_scale, w_words, w_scales, b
         x_raw, x_bank, s_bank = {}, {}, {}
         total, parked, res, pool_sum = {}, {}, {}, {}
         flip_total, flip_flat, back_bank, bias_bank = {}, {}, {}, {}
-        slab_uses, other_uses = [], []
 
-        def slab_bank(shape):
-            slab_uses.append(shape)
-            return psum.tile(shape, F32, name="slab_bank%d" % ((len(slab_uses) - 1) % SLAB_BANKS))
-
-        def other_bank(shape):
-            other_uses.append(shape)
-            return psum.tile(shape, F32, name="other_bank%d" % ((len(other_uses) - 1) % OTHER_BANKS))
+        def take(bank, shape):
+            return psum.tile(shape, F32, name="bank%d" % bank)
 
         def load_scale():
             nc.sync.dma_start(out=scale_cols[:], in_=adj_scale.rearrange("o (g p t) -> p (o g) t", p=P, t=4))
@@ -107,9 +96,6 @@ def tile_gcn_pa_w4_kernel(tc, x_init, adj_bytes, adj_scale, w_words, w_scales, b
         def x_part(g):
             return x_grouped[:, 4 * K_PASS * g : 4 * K_PASS * (g + 1)]
 
-        def s_part(first, last):
-            return s_grouped[:, 4 * HALF * first : 4 * HALF * last]
-
         def widen(copy, segs, host=None):
             flat, lo = a_raw[segs[0]]
             n = len(segs)
@@ -120,9 +106,9 @@ def tile_gcn_pa_w4_kernel(tc, x_init, adj_bytes, adj_scale, w_words, w_scales, b
             for i, seg in enumerate(segs):
                 a_wide[seg] = wide[:, K_PASS * i : K_PASS * (i + 1)]
 
-        def adj_turn(slab, tiles=(0, 1)):
+        def adj_turn(bank_no, slab, tiles=(0, 1)):
             q, g = divmod(slab, PASSES)
-            bank = slab_bank([P, 2, P * len(tiles)])
+            bank = take(bank_no, [P, 2, P * len(tiles)])
             a_bank[slab, tiles[0]] = bank
             for i, j in enumerate(tiles):
                 words = a_wide[q, j, g].bitcast(F32)
@@ -162,13 +148,14 @@ def tile_gcn_pa_w4_kernel(tc, x_init, adj_bytes, adj_scale, w_words, w_scales, b
                 in_=a_bank[slab, 0][:].rearrange("p u r -> p r u"),
             )
 
-        def repeat_scale():
-            factor = scale_cols[:, 0, :].rearrange("p (o t) -> p o t", o=1)
-            nc.scalar.copy(out=scale_tile[:].rearrange("p (r t) -> p r t", t=4), in_=factor.to_broadcast([P, P, 4]))
+        def repeat_scale(g):
+            scale_tile[g] = keep.tile([P, K_PASS], F32, name="scale_tile%d" % g)
+            factor = scale_cols[:, g, :].rearrange("p (o t) -> p o t", o=1)
+            nc.scalar.copy(out=scale_tile[g][:].rearrange("p (r t) -> p r t", t=4), in_=factor.to_broadcast([P, P, 4]))
 
         def pool_mult(slab, host):
             part = grouped_part(slab, (0, 1), host)
-            factor = scale_tile[:].rearrange("p (o c) -> p o c", o=1)
+            factor = scale_tile[slab % PASSES][:].rearrange("p (o c) -> p o c", o=1)
             nc.gpsimd.tensor_tensor(
                 out=part.rearrange("p (j c) -> p j c", j=2),
                 in0=a_staged[slab][:].rearrange("p (j c) -> p j c", j=2),
@@ -181,8 +168,8 @@ def tile_gcn_pa_w4_kernel(tc, x_init, adj_bytes, adj_scale, w_words, w_scales, b
             cols = slice(code_start(lo), code_start(lo) + PAIR_ROWS * len(call))
             nc.vector.quantize_mx(out=a_codes[:, cols].bitcast(E4M3X4), scales=a_plane[:, cols], in_=a_grouped[lo])
 
-        def x_turn(g, b):
-            bank = other_bank([P, 4, P])
+        def x_turn(bank_no, g, b):
+            bank = take(bank_no, [P, 4, P])
             x_bank[g, b] = bank
             for a in range(2):
                 words = x_raw[g, b][:, a, :].bitcast(F32)
@@ -204,8 +191,8 @@ def tile_gcn_pa_w4_kernel(tc, x_init, adj_bytes, adj_scale, w_words, w_scales, b
                 in_=x_grouped[:, 4 * K_PASS * first : 4 * K_PASS * last],
             )
 
-        def support_mm(g, c):
-            bank = other_bank([P, 4, P])
+        def support_mm(bank_no, g, c):
+            bank = take(bank_no, [P, 4, P])
             s_bank[g, c] = bank
             for t in range(4):
                 cols = slice(K_PASS * g + P * t, K_PASS * g + P * (t + 1))
@@ -221,15 +208,11 @@ def tile_gcn_pa_w4_kernel(tc, x_init, adj_bytes, adj_scale, w_words, w_scales, b
 
         def support_out(g, c, copy=nc.scalar.copy):
             h, i = divmod(c, 2)
-            part = s_part(PASSES * h + g, PASSES * h + g + 1)
+            part = grouped_part(18 + PASSES * h + g, (0, 1))
             copy(
                 out=part[:, 4 * P * i : 4 * P * (i + 1)].rearrange("p (n t) -> p n t", t=4),
                 in_=s_bank[g, c][:].rearrange("p t n -> p n t"),
             )
-
-        def support_quant(first, last):
-            cols = slice(HALF * first, HALF * last)
-            nc.vector.quantize_mx(out=s_codes[:, cols].bitcast(E4M3X4), scales=s_plane[:, cols], in_=s_part(first, last))
 
         def pieces(u):
             return [(0, u), (1, u)] if u < 2 else [(u - 2, 0), (u - 2, 1)]
@@ -254,22 +237,22 @@ def tile_gcn_pa_w4_kernel(tc, x_init, adj_bytes, adj_scale, w_words, w_scales, b
             else:
                 nc.sync.dma_start(out=unit_view(rows, u)[:, lo:hi, :], in_=unit_view(res[q], u)[:, lo:hi, :])
 
-        def out_mm(q, u, first=0, last=PASSES, new_bank=other_bank):
-            if first == 0:
-                total[q, u] = new_bank([P, 2, HALF])
-            for g in range(first, last):
+        def out_mm(bank_no, q, u, passes=(0, 1, 2), opens=True, closes=True):
+            if opens:
+                total[q, u] = take(bank_no, [P, 2, HALF])
+            for g in passes:
                 for i, (j, h) in enumerate(pieces(u)):
-                    cols = slice(HALF * (PASSES * h + g), HALF * (PASSES * h + g + 1))
+                    cols = slice(code_start(18 + PASSES * h + g), code_start(18 + PASSES * h + g) + HALF)
                     start = code_start(PASSES * q + g) + P * j
                     rows = slice(start, start + P)
                     nc.tensor.matmul_mx(
                         out=total[q, u][:, i, :],
                         lhsT=a_codes[:, rows].bitcast(E4M3X4),
                         lhsT_scale=a_plane[:, rows],
-                        rhs=s_codes[:, cols].bitcast(E4M3X4),
-                        rhs_scale=s_plane[:, cols],
-                        start=(g == 0 and i == 0),
-                        stop=(g == PASSES - 1 and i == 1),
+                        rhs=a_codes[:, cols].bitcast(E4M3X4),
+                        rhs_scale=a_plane[:, cols],
+                        start=(opens and g == passes[0] and i == 0),
+                        stop=(closes and g == passes[-1] and i == 1),
                     )
 
         def vector_bias(q, u, lo=0, hi=2):
@@ -319,18 +302,18 @@ def tile_gcn_pa_w4_kernel(tc, x_init, adj_bytes, adj_scale, w_words, w_scales, b
                 op=ALU.add,
             )
 
-        def flip_mm(parts):
-            bank = other_bank([P, 2, PAIR_ROWS])
+        def flip_mm(bank_no, parts):
+            bank = take(bank_no, [P, 2, PAIR_ROWS])
             flip_total[parts] = bank
             for i, (q, c) in enumerate(parts):
                 for g in range(PASSES):
-                    start = HALF * (PASSES * (c // 2) + g) + P * (c % 2)
+                    start = code_start(18 + PASSES * (c // 2) + g) + P * (c % 2)
                     cols = slice(start, start + P)
                     rows = slice(code_start(PASSES * q + g), code_start(PASSES * q + g) + PAIR_ROWS)
                     nc.tensor.matmul_mx(
                         out=bank[:, i, :],
-                        lhsT=s_codes[:, cols].bitcast(E4M3X4),
-                        lhsT_scale=s_plane[:, cols],
+                        lhsT=a_codes[:, cols].bitcast(E4M3X4),
+                        lhsT_scale=a_plane[:, cols],
                         rhs=a_codes[:, rows].bitcast(E4M3X4),
                         rhs_scale=a_plane[:, rows],
                         start=(g == 0),
@@ -348,8 +331,8 @@ def tile_gcn_pa_w4_kernel(tc, x_init, adj_bytes, adj_scale, w_words, w_scales, b
             for i, part in enumerate(parts):
                 flip_flat[part] = flat[:, i, :]
 
-        def flip_back(q, u, new_bank):
-            bank = new_bank([P, 2, HALF])
+        def flip_back(bank_no, q, u):
+            bank = take(bank_no, [P, 2, HALF])
             back_bank[q, u] = bank
             for n, (j, h) in enumerate(pieces(u)):
                 for i in range(2):
@@ -364,8 +347,8 @@ def tile_gcn_pa_w4_kernel(tc, x_init, adj_bytes, adj_scale, w_words, w_scales, b
         def cast_bias():
             nc.scalar.copy(out=bias_rows_f32[:], in_=bias_rows[:])
 
-        def turn_bias():
-            bias_bank[0] = other_bank([P, 4, P])
+        def turn_bias(bank_no):
+            bias_bank[0] = take(bank_no, [P, 4, P])
             nc.tensor.transpose(bias_bank[0][:, 0, :], bias_rows_f32[:], ident[:])
 
         def bias_out():
@@ -394,7 +377,7 @@ def tile_gcn_pa_w4_kernel(tc, x_init, adj_bytes, adj_scale, w_words, w_scales, b
             load_bias()
             load_adj(4)
             load_adj(5)
-            repeat_scale()
+            repeat_scale(0)
             widen(on_scalar, [(0, 0, 1)])
             widen(on_scalar, [(0, 1, 1)])
             widen(on_scalar, [(0, 0, 2)])
@@ -403,12 +386,12 @@ def tile_gcn_pa_w4_kernel(tc, x_init, adj_bytes, adj_scale, w_words, w_scales, b
             widen(on_vector, [(0, 0, 0)])
             widen(on_vector, [(0, 1, 0)])
             widen(on_pool, [(1, 1, 1), (1, 1, 2)])
-            adj_turn(0, (0,))
-            adj_turn(0, (1,))
-            adj_turn(1)
-            adj_turn(2)
-            x_turn(0, 0)
-            x_turn(0, 1)
+            adj_turn(0, 0, (0,))
+            adj_turn(1, 0, (1,))
+            adj_turn(2, 1)
+            adj_turn(3, 2)
+            x_turn(4, 0, 0)
+            x_turn(5, 0, 1)
             x_out(0, 0)
             x_out(0, 1)
             cast_bias()
@@ -416,13 +399,13 @@ def tile_gcn_pa_w4_kernel(tc, x_init, adj_bytes, adj_scale, w_words, w_scales, b
             adj_mult(0, (1,))
             adj_mult(1)
             adj_mult(2)
-            adj_turn(3)
-            x_turn(1, 0)
-            x_turn(1, 1)
-            x_turn(2, 0)
-            x_turn(2, 1)
-            adj_turn(4)
-            adj_turn(5)
+            adj_turn(0, 3)
+            x_turn(6, 1, 0)
+            x_turn(7, 1, 1)
+            x_turn(4, 2, 0)
+            x_turn(5, 2, 1)
+            adj_turn(1, 4)
+            adj_turn(2, 5)
             x_out(1, 0)
             x_out(1, 1)
             x_out(2, 0)
@@ -435,40 +418,40 @@ def tile_gcn_pa_w4_kernel(tc, x_init, adj_bytes, adj_scale, w_words, w_scales, b
             adj_mult(4)
             adj_mult(5)
             widen(on_pool, [(3, 0, 0), (3, 0, 1), (3, 0, 2), (3, 1, 0), (3, 1, 1)], x_grouped[:, 4 * K_PASS :])
-            turn_bias()
-            support_mm(0, 0)
-            support_mm(0, 1)
-            adj_turn(6)
-            support_mm(1, 0)
+            turn_bias(6)
+            support_mm(7, 0, 0)
+            support_mm(4, 0, 1)
+            adj_turn(3, 6)
+            support_mm(5, 1, 0)
             bias_out()
             support_out(0, 0)
             support_out(0, 1)
             widen(on_scalar, [(2, 1, 1), (2, 1, 2)])
             support_out(1, 0)
             adj_mult(6)
-            support_mm(1, 1)
-            support_mm(2, 0)
-            support_mm(2, 1)
-            adj_turn(7)
-            adj_turn(8)
-            support_mm(0, 2)
+            support_mm(6, 1, 1)
+            support_mm(7, 2, 0)
+            support_mm(4, 2, 1)
+            adj_turn(0, 7)
+            adj_turn(1, 8)
+            support_mm(5, 0, 2)
             support_out(1, 1)
             support_out(2, 0)
             support_out(2, 1)
             widen(on_scalar, [(3, 1, 2)])
             support_out(0, 2)
             adj_mult(7)
-            support_quant(0, 2)
+            adj_quant(18)
             adj_quant(4)
-            support_quant(2, 3)
+            adj_quant(20)
             adj_mult(8)
-            support_mm(0, 3)
-            adj_turn(9)
-            support_mm(1, 2)
-            support_mm(1, 3)
-            adj_turn(10)
-            adj_turn(11)
-            support_mm(2, 2)
+            support_mm(6, 0, 3)
+            adj_turn(2, 9)
+            support_mm(7, 1, 2)
+            support_mm(4, 1, 3)
+            adj_turn(3, 10)
+            adj_turn(0, 11)
+            support_mm(5, 2, 2)
             support_out(0, 3)
             adj_out(9)
             support_out(1, 2)
@@ -477,50 +460,53 @@ def tile_gcn_pa_w4_kernel(tc, x_init, adj_bytes, adj_scale, w_words, w_scales, b
             support_out(2, 2)
             adj_mult(10)
             adj_mult(11)
-            support_quant(3, 5)
+            adj_quant(21)
             pool_mult(9, None)
-            support_mm(2, 3)
-            out_mm(0, 0, 0, 3)
-            adj_turn(12)
-            out_mm(1, 0, 0, 3)
+            support_mm(6, 2, 3)
+            out_mm(7, 0, 0)
+            adj_turn(1, 12)
+            out_mm(4, 1, 0)
             support_out(2, 3)
             widen(on_scalar, [(4, 1, 1), (4, 1, 2)])
-            park(0, 0)
-            park(1, 0)
+            adj_out(12)
             widen(on_scalar, [(5, 0, 0), (5, 0, 1), (5, 0, 2), (5, 1, 0), (5, 1, 1), (5, 1, 2)])
-            support_quant(5, 6)
+            adj_quant(23)
             adj_quant(9)
-            adj_mult(12)
-            pool_bias(0, 0, a_grouped[9])
-            adj_turn(13)
-            adj_turn(14)
-            flip_mm(((0, 2), (1, 2)))
-            flip_mm(((0, 3), (1, 3)))
-            flip_mm(((2, 0), (2, 1)))
-            flip_mm(((2, 2), (2, 3)))
-            adj_turn(15)
-            adj_turn(16)
+            vector_bias(0, 0)
+            vector_bias(1, 0)
+            pool_mult(12, None)
+            adj_turn(2, 13)
+            adj_turn(3, 14)
+            flip_mm(5, ((0, 2), (1, 2)))
+            flip_mm(6, ((0, 3), (1, 3)))
+            flip_mm(0, ((2, 0), (2, 1)))
+            flip_mm(1, ((2, 2), (2, 3)))
+            adj_turn(7, 15)
+            adj_turn(4, 16)
             flip_relu(((0, 2), (1, 2)))
             flip_relu(((0, 3), (1, 3)))
+            scalar_relu(0, 0)
             flip_relu(((2, 0), (2, 1)))
             flip_relu(((2, 2), (2, 3)))
             adj_out(15)
-            scalar_relu(0, 0)
+            scalar_relu(1, 0)
             adj_mult(13)
             adj_mult(14)
             adj_quant(12)
             adj_quant(14)
             adj_mult(16)
             pool_mult(15, None)
-            flip_back(0, 1, other_bank)
-            flip_back(1, 1, other_bank)
-            out_mm(3, 2, 0, 3)
-            adj_turn(17)
-            flip_back(2, 2, slab_bank)
-            flip_back(2, 3, slab_bank)
-            out_mm(3, 3, 0, 3)
+            store(0, 0)
+            store(1, 0)
+            flip_back(5, 0, 1)
+            flip_back(6, 1, 1)
+            out_mm(0, 3, 2)
+            adj_turn(2, 17)
+            flip_back(1, 2, 2)
+            flip_back(3, 2, 3)
+            out_mm(7, 3, 3)
+            out_mm(4, 4, 2)
             flip_out(0, 1)
-            scalar_relu(1, 0)
             flip_out(1, 1)
             flip_out(2, 2)
             flip_out(2, 3)
@@ -529,28 +515,26 @@ def tile_gcn_pa_w4_kernel(tc, x_init, adj_bytes, adj_scale, w_words, w_scales, b
             vector_bias(3, 3)
             adj_quant(15)
             adj_quant(17)
-            store(0)
-            store(1)
-            store(2, 2)
-            store(2, 3)
-            out_mm(4, 2, 0, 3)
-            out_mm(4, 3, 0, 3)
-            out_mm(5, 2, 0, 3)
-            out_mm(5, 3, 0, 3)
+            vector_bias(4, 2)
+            store(0, 1)
+            store(1, 1)
+            store(2)
+            out_mm(5, 4, 3)
+            out_mm(6, 5, 2)
+            out_mm(0, 5, 3)
             scalar_relu(3, 2)
             scalar_relu(3, 3)
-            vector_bias(4, 2)
+            scalar_relu(4, 2)
             vector_bias(4, 3)
             vector_bias(5, 2)
             vector_bias(5, 3)
             vector_relu(5, 3, 1, 2)
             store(3, 2)
             store(3, 3)
-            scalar_relu(4, 2)
+            store(4, 2)
             scalar_relu(4, 3)
             scalar_relu(5, 2)
             scalar_relu(5, 3, 0, 1)
-            store(4, 2)
             store(4, 3)
             store(5, 2)
             store(5, 3, 1, 2)

@@ -24,9 +24,11 @@ PAIRS = NODES // PAIR_ROWS
 SEGMENTS = 2 * PASSES
 CHUNKS = HID // P
 HALF = HID // 2
-QUANT_CALLS = ((0, 1, 2, 3), (18, 19), (4, 5, 6, 7), (20,), (21, 22), (23,), (9, 8, 10, 11), (12, 13), (14,), (15, 16), (17,))
-POOL_ADDS = ()
-STRIP_STARTS = {4: 0, 9: 3072, 23: 8192, 12: 8192, 15: 9216}
+QUANT_CALLS = ((0, 1, 2, 3), (18, 19), (4, 5, 6, 7), (20, 21), (22, 23), (9, 8, 10, 11), (12, 13, 14, 16), (15, 17))
+STRIP = 10240
+STRIP_STARTS = {22: 0, 9: 1024, 12: 5120, 15: 8192}
+
+F32_MAX = 3.4028234663852886e38
 
 FLOPS = 2 * NODES * FEAT * HID + 2 * NODES * NODES * HID
 
@@ -48,13 +50,14 @@ def tile_gcn_pa_w4_kernel(tc, x_init, adj_bytes, adj_scale, w_words, w_scales, b
         a_codes = keep.tile([P, 24 * PAIR_ROWS], U32, name="a_codes", align_bytes=64)
         a_plane = keep.tile([P, 24 * PAIR_ROWS], U8, name="a_plane", align_bytes=64)
         x_grouped = keep.tile([P, 6144], BF16, name="x_grouped", align_bytes=64)
-        strip = keep.tile([P, 11264], BF16, name="strip", align_bytes=64)
+        strip = keep.tile([P, STRIP], BF16, name="strip", align_bytes=64)
         bias_rows = keep.tile([P, P], BF16, name="bias_rows")
         bias_rows_f32 = keep.tile([P, P], F32, name="bias_rows_f32")
+        pool_in = keep.tile([P, 2, 2, HALF], F32, name="pool_in")
         bias_col = keep.tile([P, CHUNKS], F32, name="bias_col")
-        a_raw, a_wide, a_bank, a_grouped, a_staged = {}, {}, {}, {}, {}
+        a_raw, a_wide, a_bank, a_grouped, a_staged, a_planes = {}, {}, {}, {}, {}, {}
         x_raw, x_bank, s_bank = {}, {}, {}
-        total, parked, res, pool_sum = {}, {}, {}, {}
+        total, moved, res, pool_sum = {}, {}, {}, {}
         flip_total, flip_flat, back_bank, bias_bank = {}, {}, {}, {}
 
         def take(bank, shape):
@@ -83,9 +86,9 @@ def tile_gcn_pa_w4_kernel(tc, x_init, adj_bytes, adj_scale, w_words, w_scales, b
         def load_w_codes():
             nc.sync.dma_start(out=w_codes[:].bitcast(I32), in_=w_words[0].bitcast(I32))
 
-        def load_w_scales():
+        def load_w_scales(queue=nc.sync):
             for quad in range(4):
-                nc.sync.dma_start(
+                queue.dma_start(
                     out=w_plane[32 * quad : 32 * quad + 4, :].bitcast(I32),
                     in_=w_scales[0, 4 * quad : 4 * quad + 4, :].bitcast(I32),
                 )
@@ -105,6 +108,13 @@ def tile_gcn_pa_w4_kernel(tc, x_init, adj_bytes, adj_scale, w_words, w_scales, b
             copy(out=wide, in_=flat[:, K_PASS * lo : K_PASS * (lo + n)].bitcast(E4M3))
             for i, seg in enumerate(segs):
                 a_wide[seg] = wide[:, K_PASS * i : K_PASS * (i + 1)]
+
+        def widen_half(copy, seg, half):
+            flat, lo = a_raw[seg]
+            if seg not in a_wide:
+                a_wide[seg] = keep.tile([P, K_PASS], BF16, name="a_wide%d_%d_%d" % seg)[:]
+            cols = slice(HALF * half, HALF * (half + 1))
+            copy(out=a_wide[seg][:, cols], in_=flat[:, K_PASS * lo : K_PASS * (lo + 1)][:, cols].bitcast(E4M3))
 
         def adj_turn(bank_no, slab, tiles=(0, 1)):
             q, g = divmod(slab, PASSES)
@@ -163,6 +173,33 @@ def tile_gcn_pa_w4_kernel(tc, x_init, adj_bytes, adj_scale, w_words, w_scales, b
                 op=ALU.mult,
             )
 
+        def adj_planes(slab, into=None):
+            first = slab if into is None else into
+            if first not in a_planes:
+                a_planes[first] = keep.tile([P, 2, 4, PAIR_ROWS], BF16, name="a_planes%d" % first)
+            values = a_bank[slab, 0][:].rearrange("p u r -> p (u r)").bitcast(BF16).rearrange("p (u r e) -> p u e r", u=2, e=2)
+            for t in range(4):
+                nc.scalar.activation(
+                    out=a_planes[first][:, 0 if into is None else 1, t, :],
+                    in_=values[:, t // 2, t % 2, :],
+                    func=ACT.Copy,
+                    scale=scale_cols[:, slab % PASSES, t : t + 1],
+                )
+
+        def adj_weave(slabs):
+            parts = [grouped_part(s, (0, 1)) for s in slabs]
+            call = [c for c in QUANT_CALLS if slabs[0] in c][0]
+            start = 4 * PAIR_ROWS * call.index(slabs[0])
+            whole = a_grouped[call[0]][:, start : start + 4 * PAIR_ROWS * len(parts)]
+            nc.gpsimd.tensor_scalar(
+                out=whole.rearrange("p (n r t) -> p n r t", n=len(parts), t=4),
+                in0=a_planes[slabs[0]][:, 0 : len(parts), :, :].rearrange("p n t r -> p n r t"),
+                scalar1=1.0,
+                scalar2=0.0,
+                op0=ALU.mult,
+                op1=ALU.add,
+            )
+
         def adj_quant(lo):
             call = [c for c in QUANT_CALLS if c[0] == lo][0]
             cols = slice(code_start(lo), code_start(lo) + PAIR_ROWS * len(call))
@@ -215,14 +252,21 @@ def tile_gcn_pa_w4_kernel(tc, x_init, adj_bytes, adj_scale, w_words, w_scales, b
             )
 
         def pieces(u):
+            if u >= 4:
+                return [divmod(u - 4, 2)]
             return [(0, u), (1, u)] if u < 2 else [(u - 2, 0), (u - 2, 1)]
 
         def unit_view(whole, u):
             by_piece = whole.rearrange("p j (h c) -> p j h c", c=HALF)
+            if u >= 4:
+                j, h = divmod(u - 4, 2)
+                return by_piece[:, j, h : h + 1, :]
             return by_piece[:, :, u, :] if u < 2 else by_piece[:, u - 2, :, :]
 
         def unit_bias(u):
             by_half = bias[:].rearrange("p (h c) -> p h c", c=HALF)
+            if u >= 4:
+                return by_half[:, u % 2 : u % 2 + 1, :]
             return by_half[:, u : u + 1, :].to_broadcast([P, 2, HALF]) if u < 2 else by_half
 
         def result(q):
@@ -230,16 +274,16 @@ def tile_gcn_pa_w4_kernel(tc, x_init, adj_bytes, adj_scale, w_words, w_scales, b
                 res[q] = keep.tile([P, 2, HID], F32, name="res%d" % q)[:]
             return res[q]
 
-        def store(q, u=None, lo=0, hi=2):
+        def store(q, u=None, lo=0, hi=None):
             rows = out[PAIR_ROWS * q : PAIR_ROWS * (q + 1), :].rearrange("(m j) h -> m j h", j=2)
             if u is None:
                 nc.sync.dma_start(out=rows, in_=res[q])
             else:
-                nc.sync.dma_start(out=unit_view(rows, u)[:, lo:hi, :], in_=unit_view(res[q], u)[:, lo:hi, :])
+                nc.sync.dma_start(out=unit_view(rows, u)[:, lo:hi, :], in_=(moved[q, u] if (q, u) in moved else unit_view(res[q], u))[:, lo:hi, :])
 
         def out_mm(bank_no, q, u, passes=(0, 1, 2), opens=True, closes=True):
             if opens:
-                total[q, u] = take(bank_no, [P, 2, HALF])
+                total[q, u] = take(bank_no, [P, len(pieces(u)), HALF])
             for g in passes:
                 for i, (j, h) in enumerate(pieces(u)):
                     cols = slice(code_start(18 + PASSES * h + g), code_start(18 + PASSES * h + g) + HALF)
@@ -252,12 +296,13 @@ def tile_gcn_pa_w4_kernel(tc, x_init, adj_bytes, adj_scale, w_words, w_scales, b
                         rhs=a_codes[:, cols].bitcast(E4M3X4),
                         rhs_scale=a_plane[:, cols],
                         start=(opens and g == passes[0] and i == 0),
-                        stop=(closes and g == passes[-1] and i == 1),
+                        stop=(closes and g == passes[-1] and i == len(pieces(u)) - 1),
                     )
 
-        def vector_bias(q, u, lo=0, hi=2):
+        def vector_bias(q, u, lo=0, hi=None, slot=None):
+            dst = unit_view(result(q), u) if slot is None else pool_in[:, slot, :, :]
             nc.vector.tensor_tensor(
-                out=unit_view(result(q), u)[:, lo:hi, :], in0=total[q, u][:, lo:hi, :], in1=unit_bias(u)[:, lo:hi, :], op=ALU.add
+                out=dst[:, lo:hi, :], in0=total[q, u][:, lo:hi, :], in1=unit_bias(u)[:, lo:hi, :], op=ALU.add
             )
 
         def relu_operands(q, u, lo, hi):
@@ -267,40 +312,27 @@ def tile_gcn_pa_w4_kernel(tc, x_init, adj_bytes, adj_scale, w_words, w_scales, b
             dst = unit_view(result(q), u)
             return dst[:, lo:hi, :], pool_sum.get((q, u), dst)[:, lo:hi, :]
 
-        def scalar_relu(q, u=None, lo=0, hi=2):
+        def scalar_relu(q, u=None, lo=0, hi=None):
             dst, src = relu_operands(q, u, lo, hi)
             nc.scalar.activation(out=dst, in_=src, func=ACT.Relu)
 
-        def vector_relu(q, u=None, lo=0, hi=2):
+        def vector_relu(q, u=None, lo=0, hi=None):
             dst, src = relu_operands(q, u, lo, hi)
             nc.vector.tensor_scalar(out=dst, in0=src, scalar1=0.0, scalar2=None, op0=ALU.max)
 
-        def pool_relu(q, u=None, lo=0, hi=2):
+        def pool_relu(q, u=None, lo=0, hi=None, host=None):
             dst, src = relu_operands(q, u, lo, hi)
-            nc.gpsimd.tensor_scalar(out=dst, in0=src, scalar1=0.0, scalar2=0.0, op0=ALU.max, op1=ALU.add)
+            if host is not None:
+                dst = host[:, 0 : 2 * HID].bitcast(F32).rearrange("p (i c) -> p i c", c=HALF)
+                moved[q, u] = dst
+            nc.gpsimd.tensor_scalar(out=dst, in0=src, scalar1=F32_MAX, scalar2=0.0, op0=ALU.min, op1=ALU.max)
 
-        def park(q, u):
-            job = [b for b in POOL_ADDS if (q, u) in b][0]
-            if job not in parked:
-                parked[job] = keep.tile([P, len(job), 2, HALF], F32, name="parked%d_%d" % job[0])
-            nc.scalar.copy(out=parked[job][:, job.index((q, u)), :, :], in_=total[q, u][:])
-
-        def pool_bias(q, u, host):
-            job = [b for b in POOL_ADDS if (q, u) in b][0]
-            n = len(job)
-            flat = host[:, 0 : 4 * HALF * n].bitcast(F32)
-            width = HALF if u < 2 else HID
-            for i, unit in enumerate(job):
-                pool_sum[unit] = flat[:, HID * i : HID * (i + 1)].rearrange("p (i c) -> p i c", c=HALF)
-            pool_sum[q, None] = flat
-            cols = slice(HALF * u, HALF * (u + 1)) if u < 2 else slice(0, HID)
-            spread = bias[:, cols].rearrange("p (o c) -> p o c", o=1).to_broadcast([P, HID * n // width, width])
-            nc.gpsimd.tensor_tensor(
-                out=flat.rearrange("p (i c) -> p i c", c=width),
-                in0=parked[job][:].rearrange("p n i c -> p (n i c)").rearrange("p (i c) -> p i c", c=width),
-                in1=spread,
-                op=ALU.add,
-            )
+        def pool_relu_both(units, host):
+            dst = host[:, 0 : 4 * HID].bitcast(F32)
+            for i, unit in enumerate(units):
+                moved[unit] = dst[:, HID * i : HID * (i + 1)].rearrange("p (i c) -> p i c", c=HALF)
+            src = pool_in[:].rearrange("p n i c -> p (n i c)")
+            nc.gpsimd.tensor_scalar(out=dst, in0=src, scalar1=F32_MAX, scalar2=0.0, op0=ALU.min, op1=ALU.max)
 
         def flip_mm(bank_no, parts):
             bank = take(bank_no, [P, 2, PAIR_ROWS])
@@ -344,8 +376,8 @@ def tile_gcn_pa_w4_kernel(tc, x_init, adj_bytes, adj_scale, w_words, w_scales, b
         def load_bias_rows():
             nc.sync.dma_start(out=bias_rows[0:CHUNKS, :], in_=b1.rearrange("(c m) -> c m", m=P))
 
-        def cast_bias():
-            nc.scalar.copy(out=bias_rows_f32[:], in_=bias_rows[:])
+        def cast_bias(copy=nc.scalar.copy):
+            copy(out=bias_rows_f32[:], in_=bias_rows[:])
 
         def turn_bias(bank_no):
             bias_bank[0] = take(bank_no, [P, 4, P])
@@ -377,6 +409,8 @@ def tile_gcn_pa_w4_kernel(tc, x_init, adj_bytes, adj_scale, w_words, w_scales, b
             load_bias()
             load_adj(4)
             load_adj(5)
+            widen(on_pool, [(1, 1, 1), (1, 1, 2)])
+            cast_bias(on_pool)
             repeat_scale(0)
             widen(on_scalar, [(0, 0, 1)])
             widen(on_scalar, [(0, 1, 1)])
@@ -385,20 +419,18 @@ def tile_gcn_pa_w4_kernel(tc, x_init, adj_bytes, adj_scale, w_words, w_scales, b
             widen(on_scalar, [(1, 0, 0), (1, 0, 1), (1, 0, 2), (1, 1, 0)])
             widen(on_vector, [(0, 0, 0)])
             widen(on_vector, [(0, 1, 0)])
-            widen(on_pool, [(1, 1, 1), (1, 1, 2)])
             adj_turn(0, 0, (0,))
             adj_turn(1, 0, (1,))
             adj_turn(2, 1)
             adj_turn(3, 2)
             x_turn(4, 0, 0)
             x_turn(5, 0, 1)
-            x_out(0, 0)
-            x_out(0, 1)
-            cast_bias()
             adj_mult(0, (0,))
             adj_mult(0, (1,))
             adj_mult(1)
             adj_mult(2)
+            x_out(0, 0)
+            x_out(0, 1)
             adj_turn(0, 3)
             x_turn(6, 1, 0)
             x_turn(7, 1, 1)
@@ -406,136 +438,145 @@ def tile_gcn_pa_w4_kernel(tc, x_init, adj_bytes, adj_scale, w_words, w_scales, b
             x_turn(5, 2, 1)
             adj_turn(1, 4)
             adj_turn(2, 5)
+            adj_mult(3)
+            x_quant(0, 1)
+            adj_quant(0)
             x_out(1, 0)
             x_out(1, 1)
             x_out(2, 0)
             x_out(2, 1)
             widen(on_scalar, [(2, 0, 0), (2, 0, 1), (2, 0, 2), (2, 1, 0)])
-            adj_mult(3)
-            x_quant(0, 1)
-            adj_quant(0)
-            x_quant(1, 3)
-            adj_mult(4)
-            adj_mult(5)
-            widen(on_pool, [(3, 0, 0), (3, 0, 1), (3, 0, 2), (3, 1, 0), (3, 1, 1)], x_grouped[:, 4 * K_PASS :])
             turn_bias(6)
             support_mm(7, 0, 0)
             support_mm(4, 0, 1)
             adj_turn(3, 6)
-            support_mm(5, 1, 0)
+            x_quant(1, 3)
+            adj_mult(4)
+            adj_mult(5)
+            adj_mult(6)
+            widen(on_pool, [(3, 0, 0), (3, 0, 1), (3, 0, 2), (3, 1, 0), (3, 1, 1), (3, 1, 2)], x_grouped[:, 4 * K_PASS :])
             bias_out()
             support_out(0, 0)
             support_out(0, 1)
             widen(on_scalar, [(2, 1, 1), (2, 1, 2)])
-            support_out(1, 0)
-            adj_mult(6)
+            support_mm(5, 1, 0)
             support_mm(6, 1, 1)
             support_mm(7, 2, 0)
             support_mm(4, 2, 1)
             adj_turn(0, 7)
             adj_turn(1, 8)
-            support_mm(5, 0, 2)
+            adj_mult(7)
+            support_out(1, 0)
             support_out(1, 1)
             support_out(2, 0)
             support_out(2, 1)
-            widen(on_scalar, [(3, 1, 2)])
-            support_out(0, 2)
-            adj_mult(7)
-            adj_quant(18)
-            adj_quant(4)
-            adj_quant(20)
-            adj_mult(8)
+            support_mm(5, 0, 2)
             support_mm(6, 0, 3)
-            adj_turn(2, 9)
             support_mm(7, 1, 2)
             support_mm(4, 1, 3)
+            adj_turn(2, 9)
             adj_turn(3, 10)
-            adj_turn(0, 11)
-            support_mm(5, 2, 2)
+            adj_quant(18)
+            adj_quant(4)
+            support_out(0, 2)
             support_out(0, 3)
-            adj_out(9)
             support_out(1, 2)
             support_out(1, 3)
-            widen(on_scalar, [(4, 0, 0), (4, 0, 1), (4, 0, 2), (4, 1, 0)])
+            support_mm(5, 2, 2)
+            support_mm(6, 2, 3)
+            adj_turn(0, 11)
+            adj_quant(20)
+            adj_mult(8)
             support_out(2, 2)
+            support_out(2, 3)
+            adj_out(9)
+            widen(on_scalar, [(4, 0, 0), (4, 0, 1), (4, 0, 2), (4, 1, 0)])
+            widen(on_scalar, [(4, 1, 1), (4, 1, 2)])
+            widen(on_scalar, [(5, 0, 0), (5, 0, 1), (5, 0, 2), (5, 1, 0), (5, 1, 1), (5, 1, 2)])
+            out_mm(7, 0, 0)
+            out_mm(4, 1, 0)
+            adj_quant(22)
             adj_mult(10)
             adj_mult(11)
-            adj_quant(21)
+            vector_bias(0, 0, slot=0)
+            vector_bias(1, 0, slot=1)
             pool_mult(9, None)
-            support_mm(6, 2, 3)
-            out_mm(7, 0, 0)
-            adj_turn(1, 12)
-            out_mm(4, 1, 0)
-            support_out(2, 3)
-            widen(on_scalar, [(4, 1, 1), (4, 1, 2)])
-            adj_out(12)
-            widen(on_scalar, [(5, 0, 0), (5, 0, 1), (5, 0, 2), (5, 1, 0), (5, 1, 1), (5, 1, 2)])
-            adj_quant(23)
-            adj_quant(9)
-            vector_bias(0, 0)
-            vector_bias(1, 0)
-            pool_mult(12, None)
-            adj_turn(2, 13)
-            adj_turn(3, 14)
             flip_mm(5, ((0, 2), (1, 2)))
+            adj_turn(1, 12)
+            adj_turn(2, 13)
             flip_mm(6, ((0, 3), (1, 3)))
-            flip_mm(0, ((2, 0), (2, 1)))
-            flip_mm(1, ((2, 2), (2, 3)))
+            adj_turn(3, 14)
+            adj_turn(0, 16)
             adj_turn(7, 15)
-            adj_turn(4, 16)
-            flip_relu(((0, 2), (1, 2)))
-            flip_relu(((0, 3), (1, 3)))
-            scalar_relu(0, 0)
-            flip_relu(((2, 0), (2, 1)))
-            flip_relu(((2, 2), (2, 3)))
-            adj_out(15)
-            scalar_relu(1, 0)
+            adj_quant(9)
             adj_mult(13)
             adj_mult(14)
-            adj_quant(12)
-            adj_quant(14)
             adj_mult(16)
-            pool_mult(15, None)
-            store(0, 0)
-            store(1, 0)
-            flip_back(5, 0, 1)
-            flip_back(6, 1, 1)
-            out_mm(0, 3, 2)
-            adj_turn(2, 17)
-            flip_back(1, 2, 2)
-            flip_back(3, 2, 3)
-            out_mm(7, 3, 3)
-            out_mm(4, 4, 2)
+            pool_relu_both(((0, 0), (1, 0)), strip[:, 1024:])
+            flip_relu(((0, 2), (1, 2)))
+            flip_relu(((0, 3), (1, 3)))
+            adj_planes(12)
+            flip_back(4, 0, 1)
+            flip_back(5, 1, 1)
+            flip_mm(6, ((2, 2), (3, 2)))
+            flip_mm(1, ((2, 3), (3, 3)))
+            adj_weave((12,))
             flip_out(0, 1)
             flip_out(1, 1)
-            flip_out(2, 2)
-            flip_out(2, 3)
-            vector_bias(3, 2)
+            flip_relu(((2, 2), (3, 2)))
+            adj_planes(15)
+            flip_relu(((2, 3), (3, 3)))
+            out_mm(4, 3, 0)
+            flip_mm(2, ((2, 0), (2, 1)))
+            adj_turn(5, 17)
+            flip_back(3, 3, 1)
+            vector_bias(3, 0)
+            adj_quant(12)
             adj_mult(17)
-            vector_bias(3, 3)
-            adj_quant(15)
-            adj_quant(17)
-            vector_bias(4, 2)
             store(0, 1)
             store(1, 1)
-            store(2)
-            out_mm(5, 4, 3)
-            out_mm(6, 5, 2)
-            out_mm(0, 5, 3)
-            scalar_relu(3, 2)
-            scalar_relu(3, 3)
-            scalar_relu(4, 2)
+            store(0, 0)
+            store(1, 0)
+            adj_weave((15,))
+            flip_relu(((2, 0), (2, 1)))
+            scalar_relu(3, 0)
+            flip_out(3, 1)
+            flip_back(6, 2, 2)
+            flip_back(7, 2, 3)
+            out_mm(0, 4, 2)
+            out_mm(1, 4, 3)
+            out_mm(4, 5, 4, passes=(1,), closes=False)
+            out_mm(2, 5, 5, passes=(1,), closes=False)
+            out_mm(3, 5, 6, passes=(1,), closes=False)
+            out_mm(5, 5, 7, passes=(1,), closes=False)
+            vector_bias(4, 2)
+            adj_quant(15)
             vector_bias(4, 3)
-            vector_bias(5, 2)
-            vector_bias(5, 3)
-            vector_relu(5, 3, 1, 2)
-            store(3, 2)
-            store(3, 3)
+            store(3, 0)
+            store(3, 1)
+            flip_out(2, 2)
+            flip_out(2, 3)
+            scalar_relu(4, 2)
+            scalar_relu(4, 3, 0, 1)
+            scalar_relu(4, 3, 1, 2)
+            out_mm(4, 5, 4, passes=(0, 2), opens=False)
+            out_mm(2, 5, 5, passes=(0, 2), opens=False)
+            out_mm(3, 5, 6, passes=(0, 2), opens=False)
+            out_mm(5, 5, 7, passes=(0, 2), opens=False)
+            vector_bias(5, 4)
+            vector_bias(5, 5)
+            vector_bias(5, 6)
+            vector_bias(5, 7)
+            vector_relu(5, 7)
+            store(2, 2)
+            store(2, 3)
             store(4, 2)
-            scalar_relu(4, 3)
-            scalar_relu(5, 2)
-            scalar_relu(5, 3, 0, 1)
-            store(4, 3)
-            store(5, 2)
-            store(5, 3, 1, 2)
-            store(5, 3, 0, 1)
+            store(4, 3, 0, 1)
+            store(4, 3, 1, 2)
+            scalar_relu(5, 4)
+            scalar_relu(5, 5)
+            scalar_relu(5, 6)
+            store(5, 4)
+            store(5, 5)
+            store(5, 6)
+            store(5, 7)

@@ -24,9 +24,9 @@ PAIRS = NODES // PAIR_ROWS
 SEGMENTS = 2 * PASSES
 CHUNKS = HID // P
 HALF = HID // 2
-QUANT_CALLS = ((0, 1, 2, 3), (18, 19), (4, 5, 6, 7), (20, 21), (22, 23), (9, 8, 10, 11), (12, 13, 14, 16), (15, 17))
-STRIP = 10240
-STRIP_STARTS = {22: 0, 9: 1024, 12: 5120, 15: 8192}
+QUANT_CALLS = ((0, 1, 2, 3), (18, 19), (4, 5, 6, 7), (20, 21), (22, 23), (8,), (9, 10), (11,), (13, 14), (12, 16), (15, 17))
+STRIP = 8192
+STRIP_STARTS = {22: 0, 9: 1024, 13: 4096, 15: 5120}
 
 F32_MAX = 3.4028234663852886e38
 
@@ -301,6 +301,8 @@ def tile_gcn_pa_w4_kernel(tc, x_init, adj_bytes, adj_scale, w_words, w_scales, b
 
         def vector_bias(q, u, lo=0, hi=None, slot=None):
             dst = unit_view(result(q), u) if slot is None else pool_in[:, slot, :, :]
+            if slot is not None:
+                moved[q, u] = dst
             nc.vector.tensor_tensor(
                 out=dst[:, lo:hi, :], in0=total[q, u][:, lo:hi, :], in1=unit_bias(u)[:, lo:hi, :], op=ALU.add
             )
@@ -309,7 +311,7 @@ def tile_gcn_pa_w4_kernel(tc, x_init, adj_bytes, adj_scale, w_words, w_scales, b
             if u is None:
                 dst = result(q).rearrange("p j h -> p (j h)")
                 return dst, pool_sum.get((q, u), dst)
-            dst = unit_view(result(q), u)
+            dst = moved[q, u] if (q, u) in moved else unit_view(result(q), u)
             return dst[:, lo:hi, :], pool_sum.get((q, u), dst)[:, lo:hi, :]
 
         def scalar_relu(q, u=None, lo=0, hi=None):
@@ -451,125 +453,129 @@ def tile_gcn_pa_w4_kernel(tc, x_init, adj_bytes, adj_scale, w_words, w_scales, b
             support_mm(4, 0, 1)
             adj_turn(3, 6)
             x_quant(1, 3)
-            adj_mult(4)
             adj_mult(5)
+            adj_mult(4)
             adj_mult(6)
-            widen(on_pool, [(3, 0, 0), (3, 0, 1), (3, 0, 2), (3, 1, 0), (3, 1, 1), (3, 1, 2)], x_grouped[:, 4 * K_PASS :])
+            widen(on_pool, [(3, 0, 0), (3, 0, 1), (3, 0, 2), (3, 1, 0), (3, 1, 1)], x_grouped[:, 4 * K_PASS :])
             bias_out()
-            support_out(0, 0)
-            support_out(0, 1)
             widen(on_scalar, [(2, 1, 1), (2, 1, 2)])
+            support_out(0, 1)
+            support_out(0, 0)
             support_mm(5, 1, 0)
             support_mm(6, 1, 1)
-            support_mm(7, 2, 0)
-            support_mm(4, 2, 1)
-            adj_turn(0, 7)
-            adj_turn(1, 8)
+            support_mm(0, 2, 0)
+            support_mm(2, 2, 1)
+            adj_turn(4, 7)
+            adj_turn(7, 8)
+            support_mm(1, 0, 2)
             adj_mult(7)
-            support_out(1, 0)
             support_out(1, 1)
-            support_out(2, 0)
+            support_out(1, 0)
             support_out(2, 1)
-            support_mm(5, 0, 2)
+            support_out(2, 0)
+            widen(on_scalar, [(3, 1, 2)])
             support_mm(6, 0, 3)
-            support_mm(7, 1, 2)
-            support_mm(4, 1, 3)
+            support_mm(5, 1, 2)
+            support_mm(3, 1, 3)
             adj_turn(2, 9)
-            adj_turn(3, 10)
+            adj_turn(0, 10)
+            support_mm(4, 2, 2)
             adj_quant(18)
             adj_quant(4)
-            support_out(0, 2)
             support_out(0, 3)
-            support_out(1, 2)
+            support_out(0, 2)
             support_out(1, 3)
-            support_mm(5, 2, 2)
+            support_out(1, 2)
             support_mm(6, 2, 3)
-            adj_turn(0, 11)
+            adj_turn(1, 11)
             adj_quant(20)
             adj_mult(8)
-            support_out(2, 2)
             support_out(2, 3)
+            support_out(2, 2)
             adj_out(9)
             widen(on_scalar, [(4, 0, 0), (4, 0, 1), (4, 0, 2), (4, 1, 0)])
             widen(on_scalar, [(4, 1, 1), (4, 1, 2)])
             widen(on_scalar, [(5, 0, 0), (5, 0, 1), (5, 0, 2), (5, 1, 0), (5, 1, 1), (5, 1, 2)])
-            out_mm(7, 0, 0)
-            out_mm(4, 1, 0)
+            out_mm(3, 0, 0)
+            out_mm(5, 1, 0)
             adj_quant(22)
+            adj_quant(8)
+            vector_bias(0, 0, slot=0)
             adj_mult(10)
             adj_mult(11)
-            vector_bias(0, 0, slot=0)
             vector_bias(1, 0, slot=1)
             pool_mult(9, None)
-            flip_mm(5, ((0, 2), (1, 2)))
-            adj_turn(1, 12)
+            flip_mm(6, ((0, 2), (1, 2)))
+            flip_mm(4, ((0, 3), (1, 3)))
+            adj_turn(7, 12)
             adj_turn(2, 13)
-            flip_mm(6, ((0, 3), (1, 3)))
-            adj_turn(3, 14)
-            adj_turn(0, 16)
-            adj_turn(7, 15)
+            flip_mm(3, ((2, 0), (2, 1)))
+            adj_turn(0, 14)
+            adj_turn(1, 16)
             adj_quant(9)
+            adj_quant(11)
             adj_mult(13)
             adj_mult(14)
             adj_mult(16)
+            adj_quant(13)
             pool_relu_both(((0, 0), (1, 0)), strip[:, 1024:])
-            flip_relu(((0, 2), (1, 2)))
             flip_relu(((0, 3), (1, 3)))
+            flip_relu(((0, 2), (1, 2)))
+            flip_relu(((2, 0), (2, 1)))
             adj_planes(12)
-            flip_back(4, 0, 1)
-            flip_back(5, 1, 1)
-            flip_mm(6, ((2, 2), (3, 2)))
-            flip_mm(1, ((2, 3), (3, 3)))
+            flip_back(6, 0, 1)
+            flip_back(4, 1, 1)
+            adj_turn(5, 15)
+            flip_mm(7, ((2, 2), (3, 2)))
+            flip_mm(3, ((2, 3), (3, 3)))
+            out_mm(2, 3, 0)
+            store(0, 0)
+            store(1, 0)
             adj_weave((12,))
-            flip_out(0, 1)
             flip_out(1, 1)
+            flip_out(0, 1)
             flip_relu(((2, 2), (3, 2)))
             adj_planes(15)
             flip_relu(((2, 3), (3, 3)))
-            out_mm(4, 3, 0)
-            flip_mm(2, ((2, 0), (2, 1)))
-            adj_turn(5, 17)
-            flip_back(3, 3, 1)
-            vector_bias(3, 0)
+            flip_back(6, 2, 0)
+            adj_turn(4, 17)
+            flip_back(0, 2, 1)
+            flip_back(7, 3, 1)
             adj_quant(12)
+            vector_bias(3, 0)
             adj_mult(17)
-            store(0, 1)
             store(1, 1)
-            store(0, 0)
-            store(1, 0)
+            store(0, 1)
             adj_weave((15,))
-            flip_relu(((2, 0), (2, 1)))
-            scalar_relu(3, 0)
+            flip_out(2, 0)
             flip_out(3, 1)
-            flip_back(6, 2, 2)
-            flip_back(7, 2, 3)
-            out_mm(0, 4, 2)
-            out_mm(1, 4, 3)
-            out_mm(4, 5, 4, passes=(1,), closes=False)
-            out_mm(2, 5, 5, passes=(1,), closes=False)
-            out_mm(3, 5, 6, passes=(1,), closes=False)
-            out_mm(5, 5, 7, passes=(1,), closes=False)
+            flip_out(2, 1)
+            scalar_relu(3, 0)
+            out_mm(1, 4, 2)
+            out_mm(3, 4, 3)
+            out_mm(5, 5, 4, passes=(1,), closes=False)
+            out_mm(6, 5, 5, passes=(1,), closes=False)
+            out_mm(2, 5, 6, passes=(1,), closes=False)
+            out_mm(0, 5, 7, passes=(1,), closes=False)
             vector_bias(4, 2)
             adj_quant(15)
             vector_bias(4, 3)
-            store(3, 0)
+            store(2, 0)
             store(3, 1)
-            flip_out(2, 2)
-            flip_out(2, 3)
+            store(2, 1)
+            store(3, 0)
             scalar_relu(4, 2)
             scalar_relu(4, 3, 0, 1)
             scalar_relu(4, 3, 1, 2)
-            out_mm(4, 5, 4, passes=(0, 2), opens=False)
-            out_mm(2, 5, 5, passes=(0, 2), opens=False)
-            out_mm(3, 5, 6, passes=(0, 2), opens=False)
-            out_mm(5, 5, 7, passes=(0, 2), opens=False)
+            out_mm(5, 5, 4, passes=(0, 2), opens=False)
+            out_mm(6, 5, 5, passes=(0, 2), opens=False)
+            out_mm(2, 5, 6, passes=(0, 2), opens=False)
+            out_mm(0, 5, 7, passes=(0, 2), opens=False)
             vector_bias(5, 4)
             vector_bias(5, 5)
             vector_bias(5, 6)
             vector_bias(5, 7)
             vector_relu(5, 7)
-            store(2, 2)
-            store(2, 3)
             store(4, 2)
             store(4, 3, 0, 1)
             store(4, 3, 1, 2)

@@ -26,7 +26,7 @@ CHUNKS = HID // P
 HALF = HID // 2
 QUANT_CALLS = ((0, 1, 2, 3), (18, 19), (4, 5, 6, 7), (20, 21), (22, 23), (8,), (9, 10), (11,), (13, 14), (12, 16), (15, 17))
 STRIP = 8192
-STRIP_STARTS = {22: 0, 9: 1024, 13: 4096, 15: 5120}
+STRIP_STARTS = {22: 0, 9: 1024, 12: 2048, 13: 4096, 15: 5120}
 
 F32_MAX = 3.4028234663852886e38
 
@@ -150,26 +150,38 @@ def tile_gcn_pa_w4_kernel(tc, x_init, adj_bytes, adj_scale, w_words, w_scales, b
                 op=ALU.mult,
             )
 
-        def adj_out(slab):
-            staged = keep.tile([P, 4 * PAIR_ROWS], BF16, name="a_staged%d" % slab)
+        def adj_out(slab, rows=PAIR_ROWS):
+            staged = keep.tile([P, 4 * rows], BF16, name="a_staged%d" % slab)
             a_staged[slab] = staged
             nc.scalar.copy(
                 out=staged[:].bitcast(F32).rearrange("p (r u) -> p r u", u=2),
-                in_=a_bank[slab, 0][:].rearrange("p u r -> p r u"),
+                in_=a_bank[slab, 0][:, :, 0:rows].rearrange("p u r -> p r u"),
             )
 
-        def repeat_scale(g):
+        def adj_mult_rest(slab, rows):
+            part = grouped_part(slab, (0, 1))[:, 4 * rows :]
+            values = a_bank[slab, 0][:].rearrange("p u r -> p (u r)").bitcast(BF16).rearrange("p (u r e) -> p r u e", u=2, e=2)
+            factor = scale_cols[:, slab % PASSES, :].rearrange("p (o u e) -> p o u e", o=1, u=2)
+            nc.vector.tensor_tensor(
+                out=part.rearrange("p (r u e) -> p r u e", u=2, e=2),
+                in0=values[:, rows:, :, :],
+                in1=factor.to_broadcast([P, PAIR_ROWS - rows, 2, 2]),
+                op=ALU.mult,
+            )
+
+        def repeat_scale(g, copy=nc.scalar.copy):
             scale_tile[g] = keep.tile([P, K_PASS], F32, name="scale_tile%d" % g)
             factor = scale_cols[:, g, :].rearrange("p (o t) -> p o t", o=1)
-            nc.scalar.copy(out=scale_tile[g][:].rearrange("p (r t) -> p r t", t=4), in_=factor.to_broadcast([P, P, 4]))
+            copy(out=scale_tile[g][:].rearrange("p (r t) -> p r t", t=4), in_=factor.to_broadcast([P, P, 4]))
 
-        def pool_mult(slab, host):
-            part = grouped_part(slab, (0, 1), host)
-            factor = scale_tile[slab % PASSES][:].rearrange("p (o c) -> p o c", o=1)
+        def pool_mult(slab, host, rows=PAIR_ROWS):
+            part = grouped_part(slab, (0, 1), host)[:, 0 : 4 * rows]
+            width = K_PASS if rows == PAIR_ROWS else 2 * rows
+            factor = scale_tile[slab % PASSES][:, 0:width].rearrange("p (o c) -> p o c", o=1)
             nc.gpsimd.tensor_tensor(
-                out=part.rearrange("p (j c) -> p j c", j=2),
-                in0=a_staged[slab][:].rearrange("p (j c) -> p j c", j=2),
-                in1=factor.to_broadcast([P, 2, K_PASS]),
+                out=part.rearrange("p (j c) -> p j c", c=width),
+                in0=a_staged[slab][:].rearrange("p (j c) -> p j c", c=width),
+                in1=factor.to_broadcast([P, 2, width]),
                 op=ALU.mult,
             )
 
@@ -500,10 +512,10 @@ def tile_gcn_pa_w4_kernel(tc, x_init, adj_bytes, adj_scale, w_words, w_scales, b
             out_mm(5, 1, 0)
             adj_quant(22)
             adj_quant(8)
-            vector_bias(0, 0, slot=0)
+            vector_bias(0, 0)
             adj_mult(10)
             adj_mult(11)
-            vector_bias(1, 0, slot=1)
+            vector_bias(1, 0)
             pool_mult(9, None)
             flip_mm(6, ((0, 2), (1, 2)))
             flip_mm(4, ((0, 3), (1, 3)))
@@ -518,11 +530,12 @@ def tile_gcn_pa_w4_kernel(tc, x_init, adj_bytes, adj_scale, w_words, w_scales, b
             adj_mult(14)
             adj_mult(16)
             adj_quant(13)
-            pool_relu_both(((0, 0), (1, 0)), strip[:, 1024:])
-            flip_relu(((0, 3), (1, 3)))
+            adj_out(12)
             flip_relu(((0, 2), (1, 2)))
+            flip_relu(((0, 3), (1, 3)))
+            scalar_relu(0, 0)
             flip_relu(((2, 0), (2, 1)))
-            adj_planes(12)
+            scalar_relu(1, 0)
             flip_back(6, 0, 1)
             flip_back(4, 1, 1)
             adj_turn(5, 15)
@@ -531,29 +544,30 @@ def tile_gcn_pa_w4_kernel(tc, x_init, adj_bytes, adj_scale, w_words, w_scales, b
             out_mm(2, 3, 0)
             store(0, 0)
             store(1, 0)
-            adj_weave((12,))
-            flip_out(1, 1)
+            pool_mult(12, None)
             flip_out(0, 1)
+            flip_out(1, 1)
             flip_relu(((2, 2), (3, 2)))
-            adj_planes(15)
+            adj_out(15, 192)
             flip_relu(((2, 3), (3, 3)))
             flip_back(6, 2, 0)
             adj_turn(4, 17)
             flip_back(0, 2, 1)
             flip_back(7, 3, 1)
             adj_quant(12)
+            adj_mult_rest(15, 192)
             vector_bias(3, 0)
             adj_mult(17)
-            store(1, 1)
             store(0, 1)
-            adj_weave((15,))
+            store(1, 1)
+            pool_mult(15, None, 192)
             flip_out(2, 0)
-            flip_out(3, 1)
             flip_out(2, 1)
+            flip_out(3, 1)
             scalar_relu(3, 0)
             out_mm(1, 4, 2)
             out_mm(3, 4, 3)
-            out_mm(5, 5, 4, passes=(1,), closes=False)
+            out_mm(4, 5, 4, passes=(1,), closes=False)
             out_mm(6, 5, 5, passes=(1,), closes=False)
             out_mm(2, 5, 6, passes=(1,), closes=False)
             out_mm(0, 5, 7, passes=(1,), closes=False)
@@ -561,13 +575,13 @@ def tile_gcn_pa_w4_kernel(tc, x_init, adj_bytes, adj_scale, w_words, w_scales, b
             adj_quant(15)
             vector_bias(4, 3)
             store(2, 0)
-            store(3, 1)
             store(2, 1)
+            store(3, 1)
             store(3, 0)
             scalar_relu(4, 2)
             scalar_relu(4, 3, 0, 1)
             scalar_relu(4, 3, 1, 2)
-            out_mm(5, 5, 4, passes=(0, 2), opens=False)
+            out_mm(4, 5, 4, passes=(0, 2), opens=False)
             out_mm(6, 5, 5, passes=(0, 2), opens=False)
             out_mm(2, 5, 6, passes=(0, 2), opens=False)
             out_mm(0, 5, 7, passes=(0, 2), opens=False)

@@ -542,8 +542,6 @@ def tile_gcn_pa_w4_kernel(tc, x_init, adj_bytes, adj_scale, w_words, w_scales, b
             flip_mm(7, ((2, 2), (3, 2)))
             flip_mm(3, ((2, 3), (3, 3)))
             out_mm(2, 3, 0)
-            store(0, 0)
-            store(1, 0)
             pool_mult(12, None)
             flip_out(0, 1)
             flip_out(1, 1)
@@ -558,8 +556,8 @@ def tile_gcn_pa_w4_kernel(tc, x_init, adj_bytes, adj_scale, w_words, w_scales, b
             adj_mult_rest(15, 192)
             vector_bias(3, 0)
             adj_mult(17)
-            store(0, 1)
-            store(1, 1)
+            store(0)
+            store(1)
             pool_mult(15, None, 192)
             flip_out(2, 0)
             flip_out(2, 1)
@@ -574,13 +572,10 @@ def tile_gcn_pa_w4_kernel(tc, x_init, adj_bytes, adj_scale, w_words, w_scales, b
             vector_bias(4, 2)
             adj_quant(15)
             vector_bias(4, 3)
-            store(2, 0)
-            store(2, 1)
-            store(3, 1)
-            store(3, 0)
+            store(2)
+            store(3)
             scalar_relu(4, 2)
-            scalar_relu(4, 3, 0, 1)
-            scalar_relu(4, 3, 1, 2)
+            scalar_relu(4, 3)
             out_mm(4, 5, 4, passes=(0, 2), opens=False)
             out_mm(6, 5, 5, passes=(0, 2), opens=False)
             out_mm(2, 5, 6, passes=(0, 2), opens=False)
@@ -591,12 +586,9 @@ def tile_gcn_pa_w4_kernel(tc, x_init, adj_bytes, adj_scale, w_words, w_scales, b
             vector_bias(5, 7)
             vector_relu(5, 7)
             store(4, 2)
-            store(4, 3, 0, 1)
-            store(4, 3, 1, 2)
+            store(4, 3)
             scalar_relu(5, 4)
             scalar_relu(5, 5)
             scalar_relu(5, 6)
-            store(5, 4)
-            store(5, 5)
-            store(5, 6)
-            store(5, 7)
+            store(5, 2)
+            store(5, 3)

@@ -424,7 +424,6 @@ def tile_gcn_pa_w4_kernel(tc, x_init, adj_bytes, adj_scale, w_words, w_scales, b
             load_adj(4)
             load_adj(5)
             widen(on_pool, [(1, 1, 1), (1, 1, 2)])
-            cast_bias(on_pool)
             repeat_scale(0)
             widen(on_scalar, [(0, 0, 1)])
             widen(on_scalar, [(0, 1, 1)])
@@ -445,6 +444,7 @@ def tile_gcn_pa_w4_kernel(tc, x_init, adj_bytes, adj_scale, w_words, w_scales, b
             adj_mult(2)
             x_out(0, 0)
             x_out(0, 1)
+            cast_bias()
             adj_turn(0, 3)
             x_turn(6, 1, 0)
             x_turn(7, 1, 1)
@@ -591,4 +591,5 @@ def tile_gcn_pa_w4_kernel(tc, x_init, adj_bytes, adj_scale, w_words, w_scales, b
             scalar_relu(5, 5)
             scalar_relu(5, 6)
             store(5, 2)
-            store(5, 3)
+            store(5, 6)
+            store(5, 7)

@@ -536,22 +536,23 @@ def tile_gcn_pa_w4_kernel(tc, x_init, adj_bytes, adj_scale, w_words, w_scales, b
             scalar_relu(0, 0)
             flip_relu(((2, 0), (2, 1)))
             scalar_relu(1, 0)
-            flip_back(6, 0, 1)
-            flip_back(4, 1, 1)
-            adj_turn(5, 15)
             flip_mm(7, ((2, 2), (3, 2)))
+            flip_back(5, 0, 1)
+            flip_back(6, 1, 1)
+            flip_back(4, 2, 0)
+            adj_turn(2, 15)
             flip_mm(3, ((2, 3), (3, 3)))
-            out_mm(2, 3, 0)
+            out_mm(0, 3, 0)
+            adj_turn(1, 17)
             pool_mult(12, None)
             flip_out(0, 1)
             flip_out(1, 1)
             flip_relu(((2, 2), (3, 2)))
             adj_out(15, 192)
             flip_relu(((2, 3), (3, 3)))
-            flip_back(6, 2, 0)
-            adj_turn(4, 17)
-            flip_back(0, 2, 1)
-            flip_back(7, 3, 1)
+            flip_out(2, 0)
+            flip_back(5, 2, 1)
+            flip_back(6, 3, 1)
             adj_quant(12)
             adj_mult_rest(15, 192)
             vector_bias(3, 0)
@@ -559,16 +560,15 @@ def tile_gcn_pa_w4_kernel(tc, x_init, adj_bytes, adj_scale, w_words, w_scales, b
             store(0)
             store(1)
             pool_mult(15, None, 192)
-            flip_out(2, 0)
             flip_out(2, 1)
             flip_out(3, 1)
             scalar_relu(3, 0)
-            out_mm(1, 4, 2)
+            out_mm(7, 4, 2)
             out_mm(3, 4, 3)
             out_mm(4, 5, 4, passes=(1,), closes=False)
-            out_mm(6, 5, 5, passes=(1,), closes=False)
+            out_mm(0, 5, 5, passes=(1,), closes=False)
             out_mm(2, 5, 6, passes=(1,), closes=False)
-            out_mm(0, 5, 7, passes=(1,), closes=False)
+            out_mm(1, 5, 7, passes=(1,), closes=False)
             vector_bias(4, 2)
             adj_quant(15)
             vector_bias(4, 3)
@@ -577,9 +577,9 @@ def tile_gcn_pa_w4_kernel(tc, x_init, adj_bytes, adj_scale, w_words, w_scales, b
             scalar_relu(4, 2)
             scalar_relu(4, 3)
             out_mm(4, 5, 4, passes=(0, 2), opens=False)
-            out_mm(6, 5, 5, passes=(0, 2), opens=False)
+            out_mm(0, 5, 5, passes=(0, 2), opens=False)
             out_mm(2, 5, 6, passes=(0, 2), opens=False)
-            out_mm(0, 5, 7, passes=(0, 2), opens=False)
+            out_mm(1, 5, 7, passes=(0, 2), opens=False)
             vector_bias(5, 4)
             vector_bias(5, 5)
             vector_bias(5, 6)

from contextlib import ExitStack

import concourse.mybir as mybir
from concourse.masks import make_identity

NODES, FEAT, HID = 1536, 512, 512

F32 = mybir.dt.float32
BF16 = mybir.dt.bfloat16
I32 = mybir.dt.int32
U32 = mybir.dt.uint32
U8 = mybir.dt.uint8
E4M3 = mybir.dt.float8_e4m3fn
E4M3X4 = mybir.dt.float8_e4m3fn_x4
E2M1X4 = mybir.dt.float4_e2m1fn_x4
ALU = mybir.AluOpType
ACT = mybir.ActivationFunctionType

P = 128
K_PASS = 4 * P
PASSES = NODES // K_PASS
PAIR_ROWS = 2 * P
PAIRS = NODES // PAIR_ROWS
SEGMENTS = 2 * PASSES
CHUNKS = HID // P
HALF = HID // 2
QUANT_CALLS = ((0, 1, 2, 3), (18, 19), (4, 5, 6, 7), (20, 21), (22, 23), (8,), (9, 10), (11,), (13, 14), (12, 16), (15, 17))
STRIP = 8192
STRIP_STARTS = {22: 0, 9: 1024, 12: 2048, 13: 4096, 15: 5120}

F32_MAX = 3.4028234663852886e38

FLOPS = 2 * NODES * FEAT * HID + 2 * NODES * NODES * HID


def tile_gcn_pa_w4_kernel(tc, x_init, adj_bytes, adj_scale, w_words, w_scales, b1, out):
    nc = tc.nc
    with ExitStack() as ctx:
        keep = ctx.enter_context(tc.tile_pool(name="keep", bufs=1))
        psum = ctx.enter_context(tc.psum_pool(name="psum", bufs=1))

        ident = keep.tile([P, P], F32, name="ident")
        scale_cols = keep.tile([P, PASSES, 4], F32, name="scale_cols")
        scale_tile = {}
        bias = keep.tile([P, HID], BF16, name="bias")
        w_codes = keep.tile([P, 2 * HID], U8, name="w_codes", align_bytes=64)
        w_plane = keep.tile([P, HID], U8, name="w_plane", align_bytes=64)
        x_codes = keep.tile([P, PASSES * K_PASS], U32, name="x_codes", align_bytes=64)
        x_plane = keep.tile([P, PASSES * K_PASS], U8, name="x_plane", align_bytes=64)
        a_codes = keep.tile([P, 24 * PAIR_ROWS], U32, name="a_codes", align_bytes=64)
        a_plane = keep.tile([P, 24 * PAIR_ROWS], U8, name="a_plane", align_bytes=64)
        x_grouped = keep.tile([P, 6144], BF16, name="x_grouped", align_bytes=64)
        strip = keep.tile([P, STRIP], BF16, name="strip", align_bytes=64)
        bias_rows = keep.tile([P, P], BF16, name="bias_rows")
        bias_rows_f32 = keep.tile([P, P], F32, name="bias_rows_f32")
        pool_in = keep.tile([P, 2, 2, HALF], F32, name="pool_in")
        bias_col = keep.tile([P, CHUNKS], F32, name="bias_col")
        a_raw, a_wide, a_bank, a_grouped, a_staged, a_planes = {}, {}, {}, {}, {}, {}
        x_raw, x_bank, s_bank = {}, {}, {}
        total, moved, res, pool_sum = {}, {}, {}, {}
        flip_total, flip_flat, back_bank, bias_bank = {}, {}, {}, {}

        def take(bank, shape):
            return psum.tile(shape, F32, name="bank%d" % bank)

        def load_scale():
            nc.sync.dma_start(out=scale_cols[:], in_=adj_scale.rearrange("o (g p t) -> p (o g) t", p=P, t=4))

        def load_adj(q, first=0, last=PASSES, tiles=(0, 1)):
            raw = keep.tile([P, len(tiles), K_PASS * (last - first)], U8, name="a_raw%d_%d_%d" % (q, first, tiles[0]))
            flat = raw[:].rearrange("p j k -> p (j k)")
            for i, j in enumerate(tiles):
                for g in range(first, last):
                    a_raw[q, j, g] = (flat, (last - first) * i + g - first)
            block = adj_bytes[PAIR_ROWS * q : PAIR_ROWS * (q + 1), K_PASS * first : K_PASS * last]
            by_tile = block.rearrange("(m j) k -> m j k", j=2)
            nc.sync.dma_start(out=raw[:], in_=by_tile[:, tiles[0] : tiles[-1] + 1, :])

        def load_x(g, halves):
            raw = keep.tile([P, 2 * len(halves), FEAT], BF16, name="x_raw%d_%d" % (g, halves[0]))
            for i, b in enumerate(halves):
                x_raw[g, b] = raw[:, 2 * i : 2 * i + 2, :]
            by_t = x_init[K_PASS * g : K_PASS * (g + 1), :].rearrange("(m t) f -> m t f", t=4)
            nc.sync.dma_start(out=raw[:], in_=by_t[:, 2 * halves[0] : 2 * halves[-1] + 2, :])

        def load_w_codes():
            nc.sync.dma_start(out=w_codes[:].bitcast(I32), in_=w_words[0].bitcast(I32))

        def load_w_scales(queue=nc.sync):
            for quad in range(4):
                queue.dma_start(
                    out=w_plane[32 * quad : 32 * quad + 4, :].bitcast(I32),
                    in_=w_scales[0, 4 * quad : 4 * quad + 4, :].bitcast(I32),
                )

        def load_bias():
            nc.sync.dma_start(out=bias[:], in_=b1.partition_broadcast(P))

        def x_part(g):
            return x_grouped[:, 4 * K_PASS * g : 4 * K_PASS * (g + 1)]

        def widen(copy, segs, host=None):
            flat, lo = a_raw[segs[0]]
            n = len(segs)
            if host is None:
                host = keep.tile([P, K_PASS * n], BF16, name="a_wide%d_%d_%d" % segs[0])
            wide = host[:, 0 : K_PASS * n]
            copy(out=wide, in_=flat[:, K_PASS * lo : K_PASS * (lo + n)].bitcast(E4M3))
            for i, seg in enumerate(segs):
                a_wide[seg] = wide[:, K_PASS * i : K_PASS * (i + 1)]

        def widen_half(copy, seg, half):
            flat, lo = a_raw[seg]
            if seg not in a_wide:
                a_wide[seg] = keep.tile([P, K_PASS], BF16, name="a_wide%d_%d_%d" % seg)[:]
            cols = slice(HALF * half, HALF * (half + 1))
            copy(out=a_wide[seg][:, cols], in_=flat[:, K_PASS * lo : K_PASS * (lo + 1)][:, cols].bitcast(E4M3))

        def adj_turn(bank_no, slab, tiles=(0, 1)):
            q, g = divmod(slab, PASSES)
            bank = take(bank_no, [P, 2, P * len(tiles)])
            a_bank[slab, tiles[0]] = bank
            for i, j in enumerate(tiles):
                words = a_wide[q, j, g].bitcast(F32)
                for u in range(2):
                    nc.tensor.transpose(bank[:, u, P * i : P * (i + 1)], words[:, u : 2 * P : 2], ident[:])

        def grouped_part(slab, tiles, host=None):
            call = [c for c in QUANT_CALLS if slab in c][0]
            if call[0] not in a_grouped:
                if call[0] in STRIP_STARTS:
                    host = strip[:, STRIP_STARTS[call[0]] :]
                if host is None:
                    host = keep.tile([P, 4 * PAIR_ROWS * len(call)], BF16, name="a_grouped%d" % call[0], align_bytes=64)
                a_grouped[call[0]] = host[:, 0 : 4 * PAIR_ROWS * len(call)]
            start = 4 * (PAIR_ROWS * call.index(slab) + P * tiles[0])
            return a_grouped[call[0]][:, start : start + 4 * P * len(tiles)]

        def code_start(slab):
            return PAIR_ROWS * [s for c in QUANT_CALLS for s in c].index(slab)

        def adj_mult(slab, tiles=(0, 1), host=None):
            part = grouped_part(slab, tiles, host)
            values = a_bank[slab, tiles[0]][:].rearrange("p u r -> p (u r)").bitcast(BF16)
            factor = scale_cols[:, slab % PASSES, :].rearrange("p (o u e) -> p o u e", o=1, u=2)
            nc.vector.tensor_tensor(
                out=part.rearrange("p (r u e) -> p r u e", u=2, e=2),
                in0=values.rearrange("p (u r e) -> p r u e", u=2, e=2),
                in1=factor.to_broadcast([P, P * len(tiles), 2, 2]),
                op=ALU.mult,
            )

        def adj_out(slab, rows=PAIR_ROWS):
            staged = keep.tile([P, 4 * rows], BF16, name="a_staged%d" % slab)
            a_staged[slab] = staged
            nc.scalar.copy(
                out=staged[:].bitcast(F32).rearrange("p (r u) -> p r u", u=2),
                in_=a_bank[slab, 0][:, :, 0:rows].rearrange("p u r -> p r u"),
            )

        def adj_mult_rest(slab, rows):
            part = grouped_part(slab, (0, 1))[:, 4 * rows :]
            values = a_bank[slab, 0][:].rearrange("p u r -> p (u r)").bitcast(BF16).rearrange("p (u r e) -> p r u e", u=2, e=2)
            factor = scale_cols[:, slab % PASSES, :].rearrange("p (o u e) -> p o u e", o=1, u=2)
            nc.vector.tensor_tensor(
                out=part.rearrange("p (r u e) -> p r u e", u=2, e=2),
                in0=values[:, rows:, :, :],
                in1=factor.to_broadcast([P, PAIR_ROWS - rows, 2, 2]),
                op=ALU.mult,
            )

        def repeat_scale(g, copy=nc.scalar.copy):
            scale_tile[g] = keep.tile([P, K_PASS], F32, name="scale_tile%d" % g)
            factor = scale_cols[:, g, :].rearrange("p (o t) -> p o t", o=1)
            copy(out=scale_tile[g][:].rearrange("p (r t) -> p r t", t=4), in_=factor.to_broadcast([P, P, 4]))

        def pool_mult(slab, host, rows=PAIR_ROWS):
            part = grouped_part(slab, (0, 1), host)[:, 0 : 4 * rows]
            width = K_PASS if rows == PAIR_ROWS else 2 * rows
            factor = scale_tile[slab % PASSES][:, 0:width].rearrange("p (o c) -> p o c", o=1)
            nc.gpsimd.tensor_tensor(
                out=part.rearrange("p (j c) -> p j c", c=width),
                in0=a_staged[slab][:].rearrange("p (j c) -> p j c", c=width),
                in1=factor.to_broadcast([P, 2, width]),
                op=ALU.mult,
            )

        def adj_planes(slab, into=None):
            first = slab if into is None else into
            if first not in a_planes:
                a_planes[first] = keep.tile([P, 2, 4, PAIR_ROWS], BF16, name="a_planes%d" % first)
            values = a_bank[slab, 0][:].rearrange("p u r -> p (u r)").bitcast(BF16).rearrange("p (u r e) -> p u e r", u=2, e=2)
            for t in range(4):
                nc.scalar.activation(
                    out=a_planes[first][:, 0 if into is None else 1, t, :],
                    in_=values[:, t // 2, t % 2, :],
                    func=ACT.Copy,
                    scale=scale_cols[:, slab % PASSES, t : t + 1],
                )

        def adj_weave(slabs):
            parts = [grouped_part(s, (0, 1)) for s in slabs]
            call = [c for c in QUANT_CALLS if slabs[0] in c][0]
            start = 4 * PAIR_ROWS * call.index(slabs[0])
            whole = a_grouped[call[0]][:, start : start + 4 * PAIR_ROWS * len(parts)]
            nc.gpsimd.tensor_scalar(
                out=whole.rearrange("p (n r t) -> p n r t", n=len(parts), t=4),
                in0=a_planes[slabs[0]][:, 0 : len(parts), :, :].rearrange("p n t r -> p n r t"),
                scalar1=1.0,
                scalar2=0.0,
                op0=ALU.mult,
                op1=ALU.add,
            )

        def adj_quant(lo):
            call = [c for c in QUANT_CALLS if c[0] == lo][0]
            cols = slice(code_start(lo), code_start(lo) + PAIR_ROWS * len(call))
            nc.vector.quantize_mx(out=a_codes[:, cols].bitcast(E4M3X4), scales=a_plane[:, cols], in_=a_grouped[lo])

        def x_turn(bank_no, g, b):
            bank = take(bank_no, [P, 4, P])
            x_bank[g, b] = bank
            for a in range(2):
                words = x_raw[g, b][:, a, :].bitcast(F32)
                for u in range(2):
                    nc.tensor.transpose(bank[:, 2 * a + u, :], words[:, u : 2 * P : 2], ident[:])

        def x_out(g, b, copy=nc.scalar.copy):
            part = x_part(g)[:, 8 * P * b : 8 * P * (b + 1)]
            copy(
                out=part.bitcast(F32).rearrange("p (a m u) -> p a m u", a=2, u=2),
                in_=x_bank[g, b][:].rearrange("p (a u) m -> p a m u", a=2),
            )

        def x_quant(first, last):
            cols = slice(K_PASS * first, K_PASS * last)
            nc.vector.quantize_mx(
                out=x_codes[:, cols].bitcast(E4M3X4),
                scales=x_plane[:, cols],
                in_=x_grouped[:, 4 * K_PASS * first : 4 * K_PASS * last],
            )

        def support_mm(bank_no, g, c):
            bank = take(bank_no, [P, 4, P])
            s_bank[g, c] = bank
            for t in range(4):
                cols = slice(K_PASS * g + P * t, K_PASS * g + P * (t + 1))
                nc.tensor.matmul_mx(
                    out=bank[:, t, :],
                    lhsT=x_codes[:, cols].bitcast(E4M3X4),
                    lhsT_scale=x_plane[:, cols],
                    rhs=w_codes[:, 2 * P * c : 2 * P * (c + 1)].bitcast(E2M1X4),
                    rhs_scale=w_plane[:, P * c : P * (c + 1)],
                    start=True,
                    stop=True,
                )

        def support_out(g, c, copy=nc.scalar.copy):
            h, i = divmod(c, 2)
            part = grouped_part(18 + PASSES * h + g, (0, 1))
            copy(
                out=part[:, 4 * P * i : 4 * P * (i + 1)].rearrange("p (n t) -> p n t", t=4),
                in_=s_bank[g, c][:].rearrange("p t n -> p n t"),
            )

        def pieces(u):
            if u >= 4:
                return [divmod(u - 4, 2)]
            return [(0, u), (1, u)] if u < 2 else [(u - 2, 0), (u - 2, 1)]

        def unit_view(whole, u):
            by_piece = whole.rearrange("p j (h c) -> p j h c", c=HALF)
            if u >= 4:
                j, h = divmod(u - 4, 2)
                return by_piece[:, j, h : h + 1, :]
            return by_piece[:, :, u, :] if u < 2 else by_piece[:, u - 2, :, :]

        def unit_bias(u):
            by_half = bias[:].rearrange("p (h c) -> p h c", c=HALF)
            if u >= 4:
                return by_half[:, u % 2 : u % 2 + 1, :]
            return by_half[:, u : u + 1, :].to_broadcast([P, 2, HALF]) if u < 2 else by_half

        def result(q):
            if q not in res:
                res[q] = keep.tile([P, 2, HID], F32, name="res%d" % q)[:]
            return res[q]

        def store(q, u=None, lo=0, hi=None):
            rows = out[PAIR_ROWS * q : PAIR_ROWS * (q + 1), :].rearrange("(m j) h -> m j h", j=2)
            if u is None:
                nc.sync.dma_start(out=rows, in_=res[q])
            else:
                nc.sync.dma_start(out=unit_view(rows, u)[:, lo:hi, :], in_=(moved[q, u] if (q, u) in moved else unit_view(res[q], u))[:, lo:hi, :])

        def out_mm(bank_no, q, u, passes=(0, 1, 2), opens=True, closes=True):
            if opens:
                total[q, u] = take(bank_no, [P, len(pieces(u)), HALF])
            for g in passes:
                for i, (j, h) in enumerate(pieces(u)):
                    cols = slice(code_start(18 + PASSES * h + g), code_start(18 + PASSES * h + g) + HALF)
                    start = code_start(PASSES * q + g) + P * j
                    rows = slice(start, start + P)
                    nc.tensor.matmul_mx(
                        out=total[q, u][:, i, :],
                        lhsT=a_codes[:, rows].bitcast(E4M3X4),
                        lhsT_scale=a_plane[:, rows],
                        rhs=a_codes[:, cols].bitcast(E4M3X4),
                        rhs_scale=a_plane[:, cols],
                        start=(opens and g == passes[0] and i == 0),
                        stop=(closes and g == passes[-1] and i == len(pieces(u)) - 1),
                    )

        def vector_bias(q, u, lo=0, hi=None, slot=None):
            dst = unit_view(result(q), u) if slot is None else pool_in[:, slot, :, :]
            if slot is not None:
                moved[q, u] = dst
            nc.vector.tensor_tensor(
                out=dst[:, lo:hi, :], in0=total[q, u][:, lo:hi, :], in1=unit_bias(u)[:, lo:hi, :], op=ALU.add
            )

        def relu_operands(q, u, lo, hi):
            if u is None:
                dst = result(q).rearrange("p j h -> p (j h)")
                return dst, pool_sum.get((q, u), dst)
            dst = moved[q, u] if (q, u) in moved else unit_view(result(q), u)
            return dst[:, lo:hi, :], pool_sum.get((q, u), dst)[:, lo:hi, :]

        def scalar_relu(q, u=None, lo=0, hi=None):
            dst, src = relu_operands(q, u, lo, hi)
            nc.scalar.activation(out=dst, in_=src, func=ACT.Relu)

        def vector_relu(q, u=None, lo=0, hi=None):
            dst, src = relu_operands(q, u, lo, hi)
            nc.vector.tensor_scalar(out=dst, in0=src, scalar1=0.0, scalar2=None, op0=ALU.max)

        def pool_relu(q, u=None, lo=0, hi=None, host=None):
            dst, src = relu_operands(q, u, lo, hi)
            if host is not None:
                dst = host[:, 0 : 2 * HID].bitcast(F32).rearrange("p (i c) -> p i c", c=HALF)
                moved[q, u] = dst
            nc.gpsimd.tensor_scalar(out=dst, in0=src, scalar1=F32_MAX, scalar2=0.0, op0=ALU.min, op1=ALU.max)

        def pool_relu_both(units, host):
            dst = host[:, 0 : 4 * HID].bitcast(F32)
            for i, unit in enumerate(units):
                moved[unit] = dst[:, HID * i : HID * (i + 1)].rearrange("p (i c) -> p i c", c=HALF)
            src = pool_in[:].rearrange("p n i c -> p (n i c)")
            nc.gpsimd.tensor_scalar(out=dst, in0=src, scalar1=F32_MAX, scalar2=0.0, op0=ALU.min, op1=ALU.max)

        def flip_mm(bank_no, parts):
            bank = take(bank_no, [P, 2, PAIR_ROWS])
            flip_total[parts] = bank
            for i, (q, c) in enumerate(parts):
                for g in range(PASSES):
                    start = code_start(18 + PASSES * (c // 2) + g) + P * (c % 2)
                    cols = slice(start, start + P)
                    rows = slice(code_start(PASSES * q + g), code_start(PASSES * q + g) + PAIR_ROWS)
                    nc.tensor.matmul_mx(
                        out=bank[:, i, :],
                        lhsT=a_codes[:, cols].bitcast(E4M3X4),
                        lhsT_scale=a_plane[:, cols],
                        rhs=a_codes[:, rows].bitcast(E4M3X4),
                        rhs_scale=a_plane[:, rows],
                        start=(g == 0),
                        stop=(g == PASSES - 1),
                    )

        def flip_relu(parts):
            flat = keep.tile([P, 2, PAIR_ROWS], F32, name="flip_flat%d_%d" % parts[0])
            step = 2 if parts[0][1] == parts[1][1] else 1
            for i in range(0, 2, step):
                c = parts[i][1]
                nc.scalar.activation(
                    out=flat[:, i : i + step, :], in_=flip_total[parts][:, i : i + step, :], func=ACT.Relu, bias=bias_col[:, c : c + 1]
                )
            for i, part in enumerate(parts):
                flip_flat[part] = flat[:, i, :]

        def flip_back(bank_no, q, u):
            bank = take(bank_no, [P, 2, HALF])
            back_bank[q, u] = bank
            for n, (j, h) in enumerate(pieces(u)):
                for i in range(2):
                    nc.tensor.transpose(bank[:, n, P * i : P * (i + 1)], flip_flat[q, 2 * h + i][:, P * j : P * (j + 1)], ident[:])

        def flip_out(q, u):
            nc.scalar.copy(out=unit_view(result(q), u), in_=back_bank[q, u][:])

        def load_bias_rows():
            nc.sync.dma_start(out=bias_rows[0:CHUNKS, :], in_=b1.rearrange("(c m) -> c m", m=P))

        def cast_bias(copy=nc.scalar.copy):
            copy(out=bias_rows_f32[:], in_=bias_rows[:])

        def turn_bias(bank_no):
            bias_bank[0] = take(bank_no, [P, 4, P])
            nc.tensor.transpose(bias_bank[0][:, 0, :], bias_rows_f32[:], ident[:])

        def bias_out():
            nc.scalar.copy(out=bias_col[:], in_=bias_bank[0][:, 0, 0:CHUNKS])

        on_vector, on_scalar, on_pool = nc.vector.tensor_copy, nc.scalar.copy, nc.gpsimd.tensor_copy

        with tc.manual_schedule():
            make_identity(nc, ident[:])
            nc.gpsimd.memset(w_plane[:].bitcast(I32), 0)
            nc.gpsimd.memset(bias_rows[:], 0.0)
            load_adj(0, 0, 1, (0,))
            load_scale()
            load_adj(0, 0, 1, (1,))
            load_adj(0, 1, PASSES)
            load_x(0, (0,))
            load_adj(1)
            load_x(0, (1,))
            load_bias_rows()
            load_x(1, (0, 1))
            load_x(2, (0, 1))
            load_w_codes()
            load_w_scales()
            load_adj(2)
            load_adj(3)
            load_bias()
            load_adj(4)
            load_adj(5)
            widen(on_pool, [(1, 1, 1), (1, 1, 2)])
            repeat_scale(0)
            widen(on_scalar, [(0, 0, 1)])
            widen(on_scalar, [(0, 1, 1)])
            widen(on_scalar, [(0, 0, 2)])
            widen(on_scalar, [(0, 1, 2)])
            widen(on_scalar, [(1, 0, 0), (1, 0, 1), (1, 0, 2), (1, 1, 0)])
            widen(on_vector, [(0, 0, 0)])
            widen(on_vector, [(0, 1, 0)])
            adj_turn(0, 0, (0,))
            adj_turn(1, 0, (1,))
            adj_turn(2, 1)
            adj_turn(3, 2)
            x_turn(4, 0, 0)
            x_turn(5, 0, 1)
            adj_mult(0, (0,))
            adj_mult(0, (1,))
            adj_mult(1)
            adj_mult(2)
            x_out(0, 0)
            x_out(0, 1)
            cast_bias()
            adj_turn(0, 3)
            x_turn(6, 1, 0)
            x_turn(7, 1, 1)
            x_turn(4, 2, 0)
            x_turn(5, 2, 1)
            adj_turn(1, 4)
            adj_turn(2, 5)
            adj_mult(3)
            x_quant(0, 1)
            adj_quant(0)
            x_out(1, 0)
            x_out(1, 1)
            x_out(2, 0)
            x_out(2, 1)
            widen(on_scalar, [(2, 0, 0), (2, 0, 1), (2, 0, 2), (2, 1, 0)])
            turn_bias(6)
            support_mm(7, 0, 0)
            support_mm(4, 0, 1)
            adj_turn(3, 6)
            x_quant(1, 3)
            adj_mult(5)
            adj_mult(4)
            adj_mult(6)
            widen(on_pool, [(3, 0, 0), (3, 0, 1), (3, 0, 2), (3, 1, 0), (3, 1, 1)], x_grouped[:, 4 * K_PASS :])
            bias_out()
            widen(on_scalar, [(2, 1, 1), (2, 1, 2)])
            support_out(0, 1)
            support_out(0, 0)
            support_mm(5, 1, 0)
            support_mm(6, 1, 1)
            support_mm(0, 2, 0)
            support_mm(2, 2, 1)
            adj_turn(4, 7)
            adj_turn(7, 8)
            support_mm(1, 0, 2)
            adj_mult(7)
            support_out(1, 1)
            support_out(1, 0)
            support_out(2, 1)
            support_out(2, 0)
            widen(on_scalar, [(3, 1, 2)])
            support_mm(6, 0, 3)
            support_mm(5, 1, 2)
            support_mm(3, 1, 3)
            adj_turn(2, 9)
            adj_turn(0, 10)
            support_mm(4, 2, 2)
            adj_quant(18)
            adj_quant(4)
            support_out(0, 3)
            support_out(0, 2)
            support_out(1, 3)
            support_out(1, 2)
            support_mm(6, 2, 3)
            adj_turn(1, 11)
            adj_quant(20)
            adj_mult(8)
            support_out(2, 3)
            support_out(2, 2)
            adj_out(9)
            widen(on_scalar, [(4, 0, 0), (4, 0, 1), (4, 0, 2), (4, 1, 0)])
            widen(on_scalar, [(4, 1, 1), (4, 1, 2)])
            widen(on_scalar, [(5, 0, 0), (5, 0, 1), (5, 0, 2), (5, 1, 0), (5, 1, 1), (5, 1, 2)])
            out_mm(3, 0, 0)
            out_mm(5, 1, 0)
            adj_quant(22)
            adj_quant(8)
            vector_bias(0, 0)
            adj_mult(10)
            adj_mult(11)
            vector_bias(1, 0)
            pool_mult(9, None)
            flip_mm(6, ((0, 2), (1, 2)))
            flip_mm(4, ((0, 3), (1, 3)))
            adj_turn(7, 12)
            adj_turn(2, 13)
            flip_mm(3, ((2, 0), (2, 1)))
            adj_turn(0, 14)
            adj_turn(1, 16)
            adj_quant(9)
            adj_quant(11)
            adj_mult(13)
            adj_mult(14)
            adj_mult(16)
            adj_quant(13)
            adj_out(12)
            flip_relu(((0, 2), (1, 2)))
            flip_relu(((0, 3), (1, 3)))
            scalar_relu(0, 0)
            flip_relu(((2, 0), (2, 1)))
            scalar_relu(1, 0)
            flip_mm(7, ((2, 2), (3, 2)))
            flip_back(5, 0, 1)
            flip_back(6, 1, 1)
            flip_back(4, 2, 0)
            adj_turn(2, 15)
            flip_mm(3, ((2, 3), (3, 3)))
            out_mm(0, 3, 0)
            adj_turn(1, 17)
            pool_mult(12, None)
            flip_out(0, 1)
            flip_out(1, 1)
            flip_relu(((2, 2), (3, 2)))
            adj_out(15, 192)
            flip_relu(((2, 3), (3, 3)))
            flip_out(2, 0)
            flip_back(5, 2, 1)
            flip_back(6, 3, 1)
            adj_quant(12)
            adj_mult_rest(15, 192)
            vector_bias(3, 0)
            adj_mult(17)
            store(0)
            store(1)
            pool_mult(15, None, 192)
            flip_out(2, 1)
            flip_out(3, 1)
            scalar_relu(3, 0)
            out_mm(7, 4, 2)
            out_mm(3, 4, 3)
            out_mm(4, 5, 4, passes=(1,), closes=False)
            out_mm(0, 5, 5, passes=(1,), closes=False)
            out_mm(2, 5, 6, passes=(1,), closes=False)
            out_mm(1, 5, 7, passes=(1,), closes=False)
            vector_bias(4, 2)
            adj_quant(15)
            vector_bias(4, 3)
            store(2)
            store(3)
            scalar_relu(4, 2)
            scalar_relu(4, 3)
            out_mm(4, 5, 4, passes=(0, 2), opens=False)
            out_mm(0, 5, 5, passes=(0, 2), opens=False)
            out_mm(2, 5, 6, passes=(0, 2), opens=False)
            out_mm(1, 5, 7, passes=(0, 2), opens=False)
            vector_bias(5, 4)
            vector_bias(5, 5)
            vector_bias(5, 6)
            vector_bias(5, 7)
            vector_relu(5, 7)
            store(4, 2)
            store(4, 3)
            scalar_relu(5, 4)
            scalar_relu(5, 5)
            scalar_relu(5, 6)
            store(5, 2)
            store(5, 6)
            store(5, 7)
